import numpy as np
import ml_dtypes


def mxq(x, axis, fmt="e4m3"):
    dtype, down = {"e4m3": (ml_dtypes.float8_e4m3fn, 7), "e5m2": (ml_dtypes.float8_e5m2, 14)}[fmt]
    v = np.moveaxis(np.asarray(x, np.float32).astype(ml_dtypes.bfloat16).astype(np.float64), axis, -1)
    blocks = v.reshape(v.shape[:-1] + (-1, 32))
    amax = np.abs(blocks).max(-1, keepdims=True)
    byte = np.maximum(np.where(amax > 0, np.frexp(amax)[1] - 1 + 127, 0) - down, 1)
    scale = np.exp2(byte - 127.0)
    codes = (blocks / scale).astype(np.float32).astype(dtype).astype(np.float64)
    return np.moveaxis((codes * scale).reshape(v.shape), -1, axis)


WIDE = False


def mx_kscale(k):
    if not WIDE:
        return np.ones(k)
    levels = np.array([10, -10, 5, -5, 0])
    if k % 512:
        return np.exp2(np.random.permutation(np.resize(levels, k // 32))).repeat(32)
    a = np.empty((k // 512, 16))
    for p in range(k // 512):
        a[p, :8] = np.random.permutation(np.resize(levels, 8))
        for g in range(8):
            far = levels[np.abs(levels - a[p, g]) >= 10]
            a[p, g + 8] = far[np.random.randint(len(far))]
    return np.exp2(a.ravel()).repeat(32)


BF16 = ml_dtypes.bfloat16


def bf(x):
    return np.asarray(x, np.float32).astype(BF16)


def f64(x):
    return np.asarray(x).astype(np.float64)


B, S, D, H, DK, F = 2, 2048, 512, 4, 128, 256
HD = H * DK
EPS = 1e-6


def rmsnorm(v, g):
    return v / np.sqrt(np.mean(v * v, axis=-1, keepdims=True) + EPS) * g


def silu(v):
    return v / (1.0 + np.exp(-v))


def draw0():
    s, t = mx_kscale(HD), mx_kscale(D)
    return {"x": bf(np.random.standard_normal((B, S, D))),
            "ao": bf(np.random.standard_normal((B, H, S, DK)) * 0.3 * s.reshape(H, 1, DK)),
            "wo": bf(np.random.standard_normal((HD, D)) * 1.5 / np.sqrt(HD) / s[:, None]),
            "bo": bf(np.random.standard_normal(D) * 0.1),
            "g2": bf((1.0 + 0.1 * np.random.standard_normal(D)) * t),
            "w1": bf(np.random.standard_normal((D, F)) / np.sqrt(D) / t[:, None]),
            "w3": bf(np.random.standard_normal((D, F)) / np.sqrt(D) / t[:, None])}


def core(x, ao, wo, bo, g2, w1, w3):
    a = f64(ao).transpose(0, 2, 1, 3).reshape(B, S, HD)
    x1 = f64(x) + ((mxq(a, 2, "e4m3") @ mxq(f64(wo), 0, "e4m3")) + f64(bo))
    n = mxq(rmsnorm(x1, f64(g2)), 2, "e4m3")
    h = silu(n @ mxq(f64(w1), 0, "e4m3")) * (n @ mxq(f64(w3), 0, "e4m3"))
    return x1, h


def e4m3fn_bytes(y):
    return np.clip(np.asarray(y, np.float64), -448.0, 448.0).astype(np.float32).astype(ml_dtypes.float8_e4m3fn).view(np.uint8)


def e4m3fn_values(b):
    return np.asarray(b, np.uint8).view(ml_dtypes.float8_e4m3fn).astype(np.float64)


def setup_inputs():
    d = draw0()
    x0 = np.asarray(d['wo']).astype(np.float64)
    s = (np.max(np.abs(x0), axis=(1,), keepdims=True) / 448.0).astype(np.float32)
    out = {}
    for k, v in d.items():
        if k == 'wo':
            out['wo_bytes'] = e4m3fn_bytes(x0 / s.astype(np.float64))
            out['wo_scale'] = s
        else:
            out[k] = v
    return out


def reference(x, ao, wo_bytes, wo_scale, bo, g2, w1, w3):
    return core(x, ao, e4m3fn_values(wo_bytes) * wo_scale.astype(np.float64), bo, g2, w1, w3)

@@ -1,0 +1,321 @@
+from contextlib import ExitStack
+
+import concourse.mybir as mybir
+from concourse.masks import make_identity
+
+F32 = mybir.dt.float32
+BF16 = mybir.dt.bfloat16
+U32 = mybir.dt.uint32
+U8 = mybir.dt.uint8
+FP8 = mybir.dt.float8_e4m3fn
+FP8X4 = mybir.dt.float8_e4m3fn_x4
+ACT = mybir.ActivationFunctionType
+ALU = mybir.AluOpType
+
+B, S, D, H, DK, F = 2, 2048, 512, 4, 128, 256
+EPS = 1e-6
+FLOPS = 2 * B * S * (H * DK * D + D * 2 * F)
+
+P = 128
+J = 4
+I = S // P
+TILES = B * I
+WIDTHS = (1, 1) + (2,) * 14 + (1, 1)
+NU = len(WIDTHS)
+FIRST = tuple(sum(WIDTHS[:u]) for u in range(NU))
+CUT = 320
+C = D // P
+
+
+def tile_transformerblock_pb_t_kernel(tc, x, ao, wo_bytes, wo_scale, bo, g2, w1, w3, out_0, out_1):
+    nc = tc.nc
+    with ExitStack() as ctx:
+        const = ctx.enter_context(tc.tile_pool(name="const", bufs=1))
+        loads = ctx.enter_context(tc.tile_pool(name="loads", bufs=1))
+        res = ctx.enter_context(tc.tile_pool(name="res", bufs=NU))
+        hres = ctx.enter_context(tc.tile_pool(name="hres", bufs=10))
+        work = ctx.enter_context(tc.tile_pool(name="work", bufs=3))
+        psum = ctx.enter_context(tc.psum_pool(name="psum", bufs=2))
+        psum1 = ctx.enter_context(tc.psum_pool(name="psum1", bufs=1))
+        ctx.enter_context(tc.manual_schedule())
+
+        bo_rows = const.tile([P, P], BF16)
+        nc.vector.memset(bo_rows[:], 0.0)
+        g2_row = const.tile([P, D], BF16)
+        nc.vector.memset(g2_row[:], 0.0)
+        ones = const.tile([P, P], BF16)
+        nc.vector.memset(ones[:], 1.0)
+        zeros = const.tile([P, D], BF16)
+        nc.vector.memset(zeros[:], 0.0)
+        warm = const.tile([P, 1], F32)
+        nc.vector.memset(warm[:], 0.0)
+        neg_half = const.tile([P, 2], F32)
+        nc.gpsimd.memset(neg_half[:], -0.5)
+        ident = const.tile([P, P], F32)
+        make_identity(nc, ident[:])
+        ident_bf = const.tile([P, P], BF16)
+        nc.vector.tensor_copy(out=ident_bf[:], in_=ident[:])
+
+        wsc = const.tile([P, J], F32)
+        nc.scalar.dma_start(out=wsc[:], in_=wo_scale.rearrange("(p t) o -> p (t o)", t=J))
+        nc.scalar.dma_start(out=bo_rows[0:C, :], in_=bo.rearrange("(c p) -> c p", c=C))
+        nc.scalar.dma_start(out=g2_row[0:1, :], in_=g2.rearrange("(o n) -> o n", o=1))
+        warm2 = const.tile([P, 1], F32)
+        nc.scalar.activation(out=warm2[:], in_=warm[:], func=ACT.Silu)
+
+        wob = const.tile([P, J, D], U8, align_bytes=64)
+        nc.sync.dma_start(out=wob[:], in_=wo_bytes.rearrange("(p t) n -> p t n", t=J))
+        ao_t = {}
+        x_t = {}
+
+        def load(k0, n):
+            b, i0 = k0 // I, k0 % I
+            src = ao[b].rearrange("h (p i) d -> p i h d", i=I)
+            for i in range(n):
+                at = loads.tile([P, H, DK], BF16, name="ao%d" % (k0 + i), align_bytes=64)
+                nc.sync.dma_start(out=at[:], in_=src[:, i0 + i, :, :])
+                ao_t[k0 + i] = at
+            xt = loads.tile([P, n, D], BF16, name="x%d" % k0, align_bytes=64)
+            nc.sync.dma_start(out=xt[:], in_=x[b].rearrange("(p i) d -> p i d", i=I)[:, i0 : i0 + n, :])
+            for i in range(n):
+                x_t[k0 + i] = xt[:, i, :]
+
+        w_raw1 = const.tile([P, J, F], BF16, align_bytes=64)
+        w_raw3 = const.tile([P, J, F], BF16, align_bytes=64)
+        load(0, 1)
+        load(1, 1)
+        load(2, 2)
+        nc.sync.dma_start(out=w_raw1[:], in_=w1.rearrange("(p j) f -> p j f", j=J))
+        nc.sync.dma_start(out=w_raw3[:], in_=w3.rearrange("(p j) f -> p j f", j=J))
+        for k0 in range(4, TILES, 4):
+            load(k0, 4)
+
+        st = {}
+
+        def span(u):
+            return range(WIDTHS[u])
+
+        def hbm_rows(t, u, width):
+            b, i0 = FIRST[u] // I, FIRST[u] % I
+            return t[b].rearrange("(p i) d -> p i d", i=I)[:, i0 : i0 + WIDTHS[u], :]
+
+        def t_stage(u, dummies=0):
+            bank = psum1.tile([P, 2, 2, P], F32, name="aT_ps")
+            for i in range(dummies):
+                nc.tensor.matmul(bank[:].rearrange("p a u r -> p (a u r)"), lhsT=ones[:], rhs=zeros[:], start=True, stop=True)
+            for a in span(u):
+                words = ao_t[FIRST[u] + a][:].rearrange("p h d -> p (h d)").bitcast(F32)
+                for e in range(2):
+                    nc.tensor.transpose(bank[:, a, e, :], words[:, e : 2 * P : 2], ident[:])
+            st["aT", u] = bank
+
+        def copy_words(copy, bank, u, name):
+            n = WIDTHS[u]
+            g = work.tile([P, 2, P, J], BF16, name=name, align_bytes=64)
+            copy(
+                out=g[:, 0:n].rearrange("p a r j -> p (a r j)").bitcast(F32).rearrange("p (a r e) -> p a r e", a=n, e=2),
+                in_=bank[:, 0:n].rearrange("p a e r -> p a r e"),
+            )
+            return g
+
+        def c_stage(u):
+            st["ag", u] = copy_words(nc.scalar.copy, st["aT", u], u, "ag")
+
+        def quant(u, src, name):
+            n = WIDTHS[u]
+            codes = work.tile([P, 2 * P], U32, name=name + "c", align_bytes=64)
+            scales = work.tile([P, 2 * P], U8, name=name + "s", align_bytes=64)
+            nc.vector.quantize_mx(
+                out=codes[:, 0 : n * P].bitcast(FP8X4), scales=scales[:, 0 : n * P], in_=src[:, 0:n].rearrange("p a r j -> p (a r j)")
+            )
+            return codes, scales
+
+        def qa_stage(u):
+            st["qa", u] = quant(u, st["ag", u], "qa")
+
+        def yt_stage(u):
+            codes, scales = st["qa", u]
+            cols = slice(0, WIDTHS[u] * P)
+            for c in range(C):
+                if c % 2 == 0:
+                    bank = psum.tile([P, 2, 2 * P], F32, name="yT_ps")
+                    st["yT", u, c // 2] = bank
+                nc.tensor.matmul_mx(
+                    out=bank[:, c % 2, cols],
+                    lhsT=wo_codes[:, c * P : (c + 1) * P].bitcast(FP8X4),
+                    lhsT_scale=wo_scales[:, c * P : (c + 1) * P],
+                    rhs=codes[:, cols].bitcast(FP8X4),
+                    rhs_scale=scales[:, cols],
+                    start=True,
+                    stop=True,
+                )
+
+        def yb_stage(u):
+            cols = slice(0, WIDTHS[u] * P)
+            yb = st["yb", u]
+            for c in range(C - 1):
+                nc.scalar.activation(out=yb[:, c, cols], in_=st["yT", u, c // 2][:, c % 2, cols], func=ACT.Identity, bias=bo_col[:, c : c + 1])
+
+        def ybv_stage(u):
+            cols = slice(0, WIDTHS[u] * P)
+            st["yb", u] = work.tile([P, C, 2 * P], F32, name="yb")
+            nc.vector.tensor_scalar(
+                out=st["yb", u][:, 3, cols], in0=st["yT", u, 1][:, 1, cols], scalar1=bo_col[:, 3:4], scalar2=None, op0=ALU.add
+            )
+
+        def yk_stage(u):
+            for a in span(u):
+                bank = psum.tile([P, C, P], F32, name="y_ps")
+                if a == 0:
+                    nc.tensor.matmul(bank[:].rearrange("p c q -> p (c q)"), lhsT=ones[:], rhs=zeros[:], start=True, stop=True)
+                for c in range(C):
+                    nc.tensor.transpose(bank[:, c, :], st["yb", u][:, c, a * P : (a + 1) * P], ident[:])
+                st["y", u, a] = bank
+
+        def x_stage(u):
+            x1 = res.tile([P, 2, D], F32, name="x1")
+            for a in span(u):
+                nc.vector.tensor_tensor(out=x1[:, a, :], in0=st["y", u, a][:].rearrange("p c q -> p (c q)"), in1=x_t[FIRST[u] + a], op=ALU.add)
+            st["x1", u] = x1
+            nc.sync.dma_start(out=hbm_rows(out_0, u, D), in_=x1[:, 0 : WIDTHS[u], :])
+
+        def sq_stage(u):
+            ssum = work.tile([P, 2], F32, name="ssum")
+            for a in span(u):
+                junk = work.tile([P, D], BF16, name="junk")
+                nc.scalar.activation(out=junk[:], in_=st["x1", u][:, a, :], func=ACT.Square, accum_out=ssum[:, a : a + 1])
+            st["ssum", u] = ssum
+
+        def r_stage(u):
+            n = WIDTHS[u]
+            ms = work.tile([P, 2], F32, name="ms")
+            nc.vector.tensor_scalar(out=ms[:, 0:n], in0=st["ssum", u][:, 0:n], scalar1=1.0 / D, scalar2=EPS, op0=ALU.mult, op1=ALU.add)
+            rstd = work.tile([P, 2], F32, name="rstd")
+            nc.gpsimd.tensor_tensor(out=rstd[:, 0:n], in0=ms[:, 0:n], in1=neg_half[:, 0:n], op=ALU.pow)
+            st["rstd", u] = rstd
+
+        def n_stage(u):
+            for a in span(u):
+                xn = work.tile([P, D], BF16, name="xn%d" % a, align_bytes=64)
+                nc.vector.scalar_tensor_tensor(
+                    out=xn[:], in0=st["x1", u][:, a, :], scalar=st["rstd", u][:, a : a + 1], in1=g2_all[:], op0=ALU.mult, op1=ALU.mult
+                )
+                st["xn", u, a] = xn
+
+        def nt_stage(u):
+            bank = psum1.tile([P, 2, 2, P], F32, name="nT_ps")
+            for a in span(u):
+                words = st["xn", u, a][:].bitcast(F32)
+                for e in range(2):
+                    nc.tensor.transpose(bank[:, a, e, :], words[:, e : 2 * P : 2], ident[:])
+            st["nT", u] = bank
+
+        def nc_stage(u):
+            st["ng", u] = copy_words(nc.scalar.copy, st["nT", u], u, "ng")
+
+        def qn_stage(u):
+            st["qn", u] = quant(u, st["ng", u], "qn")
+
+        def uv_stage(u):
+            codes, scales = st["qn", u]
+            gate = psum1.tile([P, 2, F], F32, name="u_ps")
+            up = psum1.tile([P, 2, F], F32, name="v_ps")
+            for a in span(u):
+                for dst, f0 in ((gate, 0), (up, F)):
+                    nc.tensor.matmul_mx(
+                        out=dst[:, a, :],
+                        lhsT=codes[:, a * P : (a + 1) * P].bitcast(FP8X4),
+                        lhsT_scale=scales[:, a * P : (a + 1) * P],
+                        rhs=w_codes[:, f0 : f0 + F].bitcast(FP8X4),
+                        rhs_scale=w_scales[:, f0 : f0 + F],
+                        start=True,
+                        stop=True,
+                    )
+            st["uv", u] = (gate, up)
+
+        def sl_stage(u):
+            n = WIDTHS[u]
+            sil = work.tile([P, 2, F], F32, name="sil")
+            nc.scalar.activation(out=sil[:, 0:n], in_=st["uv", u][0][:, 0:n], func=ACT.Silu)
+            st["sil", u] = sil
+
+        def ml_stage(u):
+            n = WIDTHS[u]
+            h = hres.tile([P, 2, F], F32, name="h")
+            nc.vector.tensor_tensor(out=h[:, 0:n], in0=st["uv", u][1][:, 0:n], in1=st["sil", u][:, 0:n], op=ALU.mult)
+            nc.sync.dma_start(out=hbm_rows(out_1, u, F), in_=h[:, 0:n, :])
+
+        wide = const.tile([P, J, D], BF16, align_bytes=64)
+        wo_g = const.tile([P, D, J], BF16, align_bytes=64)
+        wo_codes = const.tile([P, D], U32, align_bytes=64)
+        wo_scales = const.tile([P, D], U8, align_bytes=64)
+        w_g = const.tile([P, 2 * F, J], BF16, align_bytes=64)
+        w_codes = const.tile([P, 2 * F], U32, align_bytes=64)
+        w_scales = const.tile([P, 2 * F], U8, align_bytes=64)
+        bo_col = const.tile([P, C], F32)
+        g2_all = const.tile([P, D], BF16)
+
+        def interleave(copy, dst, src):
+            copy(out=dst.rearrange("p (c i) t -> p c t i", i=4), in_=src.rearrange("p t (c i) -> p c t i", i=4))
+
+        warm_ps = psum1.tile([P, D], F32, name="v_ps")
+        for i in range(4):
+            nc.tensor.matmul(warm_ps[:], lhsT=ones[:], rhs=zeros[:], start=True, stop=True)
+        for t in range(J):
+            if t < 3:
+                nc.vector.tensor_scalar(out=wide[:, t, :], in0=wob[:, t, :].bitcast(FP8), scalar1=wsc[:, t : t + 1], scalar2=None, op0=ALU.mult)
+            else:
+                nc.scalar.activation(out=wide[:, t, :], in_=wob[:, t, :].bitcast(FP8), func=ACT.Copy, scale=wsc[:, t : t + 1])
+
+        def ok(u):
+            return 0 <= u < NU
+
+        for s in range(-3, NU + 4):
+            if ok(s - 2):
+                nt_stage(s - 2)
+            if ok(s + 3):
+                t_stage(s + 3)
+            if ok(s - 3):
+                sl_stage(s - 3)
+            if ok(s - 2):
+                nc_stage(s - 2)
+            if ok(s + 2):
+                qa_stage(s + 2)
+            if ok(s - 1):
+                r_stage(s - 1)
+            if ok(s):
+                x_stage(s)
+                sq_stage(s)
+            if s == -3:
+                interleave(nc.vector.tensor_copy, wo_g[:, 0:CUT, :], wide[:, :, 0:CUT])
+                interleave(nc.scalar.copy, wo_g[:, CUT:D, :], wide[:, :, CUT:D])
+                nc.vector.quantize_mx(out=wo_codes[:].bitcast(FP8X4), scales=wo_scales[:], in_=wo_g[:].rearrange("p n j -> p (n j)"))
+                bo_ps = psum1.tile([P, P], F32, name="nT_ps")
+                nc.tensor.matmul(bo_ps[:], lhsT=bo_rows[:], rhs=ident_bf[:], start=True, stop=True)
+                nc.scalar.copy(out=bo_col[:], in_=bo_ps[:, 0:C])
+            if ok(s + 2):
+                yt_stage(s + 2)
+            if ok(s + 3):
+                c_stage(s + 3)
+            if s == -1:
+                g2_ps = psum1.tile([P, D], F32, name="u_ps")
+                nc.tensor.matmul(g2_ps[:], lhsT=ones[:], rhs=g2_row[:], start=True, stop=True)
+                nc.scalar.copy(out=g2_all[:], in_=g2_ps[:])
+            if ok(s + 1):
+                yk_stage(s + 1)
+            if s == 0:
+                interleave(nc.vector.tensor_copy, w_g[:, 0:F, :], w_raw1[:])
+                interleave(nc.vector.tensor_copy, w_g[:, F : 2 * F, :], w_raw3[:])
+            if ok(s - 3):
+                ml_stage(s - 3)
+            if ok(s + 2):
+                ybv_stage(s + 2)
+                yb_stage(s + 2)
+            if ok(s - 2):
+                qn_stage(s - 2)
+            if s == 1:
+                nc.vector.quantize_mx(out=w_codes[:].bitcast(FP8X4), scales=w_scales[:], in_=w_g[:].rearrange("p n j -> p (n j)"))
+            if ok(s - 1):
+                n_stage(s - 1)
+            if ok(s - 2):
+                uv_stage(s - 2)

@@ -23,8 +23,9 @@ TILES = B * I
 WIDTHS = (1, 1) + (2,) * 14 + (1, 1)
 NU = len(WIDTHS)
 FIRST = tuple(sum(WIDTHS[:u]) for u in range(NU))
+LAG = 4
 CUT = 320
-C = D // P
+WORDS = D // 2
 
 
 def tile_transformerblock_pb_t_kernel(tc, x, ao, wo_bytes, wo_scale, bo, g2, w1, w3, out_0, out_1):
@@ -32,200 +33,165 @@ def tile_transformerblock_pb_t_kernel(tc, x, ao, wo_bytes, wo_scale, bo, g2, w1,
     with ExitStack() as ctx:
         const = ctx.enter_context(tc.tile_pool(name="const", bufs=1))
         loads = ctx.enter_context(tc.tile_pool(name="loads", bufs=1))
-        res = ctx.enter_context(tc.tile_pool(name="res", bufs=NU))
         hres = ctx.enter_context(tc.tile_pool(name="hres", bufs=10))
         work = ctx.enter_context(tc.tile_pool(name="work", bufs=3))
-        psum = ctx.enter_context(tc.psum_pool(name="psum", bufs=2))
+        psum2 = ctx.enter_context(tc.psum_pool(name="psum2", bufs=2))
         psum1 = ctx.enter_context(tc.psum_pool(name="psum1", bufs=1))
         ctx.enter_context(tc.manual_schedule())
 
-        bo_rows = const.tile([P, P], BF16)
-        nc.vector.memset(bo_rows[:], 0.0)
-        g2_row = const.tile([P, D], BF16)
-        nc.vector.memset(g2_row[:], 0.0)
+        rows = const.tile([P, 2, D], BF16)
+        nc.vector.memset(rows[:], 0.0)
         ones = const.tile([P, P], BF16)
         nc.vector.memset(ones[:], 1.0)
-        zeros = const.tile([P, D], BF16)
-        nc.vector.memset(zeros[:], 0.0)
-        warm = const.tile([P, 1], F32)
-        nc.vector.memset(warm[:], 0.0)
-        neg_half = const.tile([P, 2], F32)
-        nc.gpsimd.memset(neg_half[:], -0.5)
         ident = const.tile([P, P], F32)
         make_identity(nc, ident[:])
-        ident_bf = const.tile([P, P], BF16)
-        nc.vector.tensor_copy(out=ident_bf[:], in_=ident[:])
+        neg_half = const.tile([P, 2], F32)
+        nc.gpsimd.memset(neg_half[:], -0.5)
 
         wsc = const.tile([P, J], F32)
         nc.scalar.dma_start(out=wsc[:], in_=wo_scale.rearrange("(p t) o -> p (t o)", t=J))
-        nc.scalar.dma_start(out=bo_rows[0:C, :], in_=bo.rearrange("(c p) -> c p", c=C))
-        nc.scalar.dma_start(out=g2_row[0:1, :], in_=g2.rearrange("(o n) -> o n", o=1))
-        warm2 = const.tile([P, 1], F32)
-        nc.scalar.activation(out=warm2[:], in_=warm[:], func=ACT.Silu)
+        nc.scalar.dma_start(out=rows[0:1, 0, :], in_=bo.rearrange("(o n) -> o n", o=1))
+        nc.scalar.dma_start(out=rows[0:1, 1, :], in_=g2.rearrange("(o n) -> o n", o=1))
 
         wob = const.tile([P, J, D], U8, align_bytes=64)
-        nc.sync.dma_start(out=wob[:], in_=wo_bytes.rearrange("(p t) n -> p t n", t=J))
         ao_t = {}
         x_t = {}
 
-        def load(k0, n):
-            b, i0 = k0 // I, k0 % I
-            src = ao[b].rearrange("h (p i) d -> p i h d", i=I)
-            for i in range(n):
-                at = loads.tile([P, H, DK], BF16, name="ao%d" % (k0 + i), align_bytes=64)
-                nc.sync.dma_start(out=at[:], in_=src[:, i0 + i, :, :])
-                ao_t[k0 + i] = at
-            xt = loads.tile([P, n, D], BF16, name="x%d" % k0, align_bytes=64)
-            nc.sync.dma_start(out=xt[:], in_=x[b].rearrange("(p i) d -> p i d", i=I)[:, i0 : i0 + n, :])
-            for i in range(n):
-                x_t[k0 + i] = xt[:, i, :]
+        def load_ao(k):
+            at = loads.tile([P, H, DK], BF16, name="ao%d" % k, align_bytes=64)
+            nc.sync.dma_start(out=at[:], in_=ao[k // I].rearrange("h (p i) d -> p i h d", i=I)[:, k % I, :, :])
+            ao_t[k] = at
 
-        w_raw1 = const.tile([P, J, F], BF16, align_bytes=64)
-        w_raw3 = const.tile([P, J, F], BF16, align_bytes=64)
-        load(0, 1)
-        load(1, 1)
-        load(2, 2)
-        nc.sync.dma_start(out=w_raw1[:], in_=w1.rearrange("(p j) f -> p j f", j=J))
-        nc.sync.dma_start(out=w_raw3[:], in_=w3.rearrange("(p j) f -> p j f", j=J))
+        def load_x(k0, n):
+            xt = loads.tile([P, n, D], BF16, name="x%d" % k0, align_bytes=64)
+            nc.sync.dma_start(out=xt[:], in_=x[k0 // I].rearrange("(p i) d -> p i d", i=I)[:, k0 % I : k0 % I + n, :])
+            for i in range(n):
+                x_t[k0 + i] = (xt, i)
+
+        w_raw = const.tile([P, 2, J, F], BF16, align_bytes=64)
+        nc.sync.dma_start(out=wob[:], in_=wo_bytes.rearrange("(p t) n -> p t n", t=J))
+        load_ao(0)
+        load_x(0, 2)
+        for k in range(1, 4):
+            load_ao(k)
+        load_x(2, 2)
+        nc.sync.dma_start(out=w_raw[:, 0], in_=w1.rearrange("(p j) f -> p j f", j=J))
+        nc.sync.dma_start(out=w_raw[:, 1], in_=w3.rearrange("(p j) f -> p j f", j=J))
         for k0 in range(4, TILES, 4):
-            load(k0, 4)
+            for k in range(k0, k0 + 4):
+                load_ao(k)
+            load_x(k0, 4)
 
         st = {}
 
-        def span(u):
-            return range(WIDTHS[u])
+        def width(u):
+            return WIDTHS[u] if 0 <= u < NU else 0
 
-        def hbm_rows(t, u, width):
+        def slot(u):
+            if ("slot", u) not in st:
+                st["slot", u] = loads.tile([P, 2 * D], F32, name="slot%d" % u, align_bytes=64)
+            return st["slot", u]
+
+        def hbm_rows(t, u):
             b, i0 = FIRST[u] // I, FIRST[u] % I
             return t[b].rearrange("(p i) d -> p i d", i=I)[:, i0 : i0 + WIDTHS[u], :]
 
-        def t_stage(u, dummies=0):
-            bank = psum1.tile([P, 2, 2, P], F32, name="aT_ps")
-            for i in range(dummies):
-                nc.tensor.matmul(bank[:].rearrange("p a u r -> p (a u r)"), lhsT=ones[:], rhs=zeros[:], start=True, stop=True)
-            for a in span(u):
-                words = ao_t[FIRST[u] + a][:].rearrange("p h d -> p (h d)").bitcast(F32)
+        def turn(rows_bf16, name):
+            bank = psum1.tile([P, 2, 2, P], F32, name=name)
+            for a, row in enumerate(rows_bf16):
+                words = row.bitcast(F32)
                 for e in range(2):
                     nc.tensor.transpose(bank[:, a, e, :], words[:, e : 2 * P : 2], ident[:])
-            st["aT", u] = bank
+            return bank
 
-        def copy_words(copy, bank, u, name):
-            n = WIDTHS[u]
-            g = work.tile([P, 2, P, J], BF16, name=name, align_bytes=64)
-            copy(
-                out=g[:, 0:n].rearrange("p a r j -> p (a r j)").bitcast(F32).rearrange("p (a r e) -> p a r e", a=n, e=2),
-                in_=bank[:, 0:n].rearrange("p a e r -> p a r e"),
+        def stage(bank, n, dst):
+            nc.scalar.copy(out=dst.rearrange("p (a r e) -> p a r e", a=n, e=2), in_=bank[:, 0:n].rearrange("p a e r -> p a r e"))
+
+        def turn_a(u):
+            st["aT", u] = turn([ao_t[FIRST[u] + a][:].rearrange("p h d -> p (h d)") for a in range(width(u))], "aT_ps")
+
+        def stage_a(u):
+            stage(st["aT", u], width(u), slot(u)[:, 0 : width(u) * WORDS])
+
+        def turn_n(u):
+            st["nT", u] = turn([st["xn", u, a][:] for a in range(width(u))], "nT_ps")
+
+        def stage_n(u):
+            w0 = width(u + LAG) * WORDS
+            stage(st["nT", u], width(u), slot(u + LAG)[:, w0 : w0 + width(u) * WORDS])
+
+        def quantise(u):
+            n = width(u) + width(u - LAG)
+            codes = work.tile([P, 4 * P], U32, name="codes", align_bytes=64)
+            scales = work.tile([P, 4 * P], U8, name="scales", align_bytes=64)
+            nc.vector.quantize_mx(out=codes[:, 0 : n * P].bitcast(FP8X4), scales=scales[:, 0 : n * P], in_=slot(u)[:, 0 : n * WORDS].bitcast(BF16))
+            st["q", u] = (codes, scales)
+
+        def x_rows(u):
+            xt, i = x_t[FIRST[u]]
+            return xt[:, i : i + width(u), :]
+
+        def bias_gpsimd(u):
+            n = width(u)
+            nc.gpsimd.tensor_tensor(
+                out=slot(u)[:, 0 : n * D].rearrange("p (a d) -> p a d", a=n), in0=x_rows(u), in1=bo_all[:].unsqueeze(1).to_broadcast([P, n, D]), op=ALU.add
             )
-            return g
 
-        def c_stage(u):
-            st["ag", u] = copy_words(nc.scalar.copy, st["aT", u], u, "ag")
+        def bias_vector(u):
+            nc.vector.tensor_tensor(out=slot(u)[:, 0:D], in0=bo_ps[:], in1=x_rows(u)[:, 0, :], op=ALU.add)
 
-        def quant(u, src, name):
-            n = WIDTHS[u]
-            codes = work.tile([P, 2 * P], U32, name=name + "c", align_bytes=64)
-            scales = work.tile([P, 2 * P], U8, name=name + "s", align_bytes=64)
-            nc.vector.quantize_mx(
-                out=codes[:, 0 : n * P].bitcast(FP8X4), scales=scales[:, 0 : n * P], in_=src[:, 0:n].rearrange("p a r j -> p (a r j)")
-            )
-            return codes, scales
-
-        def qa_stage(u):
-            st["qa", u] = quant(u, st["ag", u], "qa")
-
-        def yt_stage(u):
-            codes, scales = st["qa", u]
-            cols = slice(0, WIDTHS[u] * P)
-            for c in range(C):
-                if c % 2 == 0:
-                    bank = psum.tile([P, 2, 2 * P], F32, name="yT_ps")
-                    st["yT", u, c // 2] = bank
+        def project(u):
+            codes, scales = st["q", u]
+            for a in range(width(u)):
+                bank = psum2.tile([P, D], F32, name="y_ps")
                 nc.tensor.matmul_mx(
-                    out=bank[:, c % 2, cols],
-                    lhsT=wo_codes[:, c * P : (c + 1) * P].bitcast(FP8X4),
-                    lhsT_scale=wo_scales[:, c * P : (c + 1) * P],
-                    rhs=codes[:, cols].bitcast(FP8X4),
-                    rhs_scale=scales[:, cols],
+                    out=bank[:],
+                    lhsT=codes[:, a * P : (a + 1) * P].bitcast(FP8X4),
+                    lhsT_scale=scales[:, a * P : (a + 1) * P],
+                    rhs=wo_codes[:].bitcast(FP8X4),
+                    rhs_scale=wo_scales[:],
                     start=True,
                     stop=True,
                 )
-
-        def yb_stage(u):
-            cols = slice(0, WIDTHS[u] * P)
-            yb = st["yb", u]
-            for c in range(C - 1):
-                nc.scalar.activation(out=yb[:, c, cols], in_=st["yT", u, c // 2][:, c % 2, cols], func=ACT.Identity, bias=bo_col[:, c : c + 1])
-
-        def ybv_stage(u):
-            cols = slice(0, WIDTHS[u] * P)
-            st["yb", u] = work.tile([P, C, 2 * P], F32, name="yb")
-            nc.vector.tensor_scalar(
-                out=st["yb", u][:, 3, cols], in0=st["yT", u, 1][:, 1, cols], scalar1=bo_col[:, 3:4], scalar2=None, op0=ALU.add
-            )
-
-        def yk_stage(u):
-            for a in span(u):
-                bank = psum.tile([P, C, P], F32, name="y_ps")
-                if a == 0:
-                    nc.tensor.matmul(bank[:].rearrange("p c q -> p (c q)"), lhsT=ones[:], rhs=zeros[:], start=True, stop=True)
-                for c in range(C):
-                    nc.tensor.transpose(bank[:, c, :], st["yb", u][:, c, a * P : (a + 1) * P], ident[:])
                 st["y", u, a] = bank
 
-        def x_stage(u):
-            x1 = res.tile([P, 2, D], F32, name="x1")
-            for a in span(u):
-                nc.vector.tensor_tensor(out=x1[:, a, :], in0=st["y", u, a][:].rearrange("p c q -> p (c q)"), in1=x_t[FIRST[u] + a], op=ALU.add)
-            st["x1", u] = x1
-            nc.sync.dma_start(out=hbm_rows(out_0, u, D), in_=x1[:, 0 : WIDTHS[u], :])
+        def residual(u):
+            for a in range(width(u)):
+                x1 = slot(u)[:, a * D : (a + 1) * D]
+                nc.vector.tensor_tensor(out=x1, in0=st["y", u, a][:], in1=x1, op=ALU.add)
+            nc.sync.dma_start(out=hbm_rows(out_0, u), in_=slot(u)[:, 0 : width(u) * D].rearrange("p (a d) -> p a d", d=D))
 
-        def sq_stage(u):
+        def squares(u):
+            n = width(u)
             ssum = work.tile([P, 2], F32, name="ssum")
-            for a in span(u):
-                junk = work.tile([P, D], BF16, name="junk")
-                nc.scalar.activation(out=junk[:], in_=st["x1", u][:, a, :], func=ACT.Square, accum_out=ssum[:, a : a + 1])
-            st["ssum", u] = ssum
-
-        def r_stage(u):
-            n = WIDTHS[u]
+            for a in range(n):
+                sq = work.tile([P, D], BF16, name="sq")
+                nc.scalar.activation(out=sq[:], in_=slot(u)[:, a * D : (a + 1) * D], func=ACT.Square, accum_out=ssum[:, a : a + 1])
             ms = work.tile([P, 2], F32, name="ms")
-            nc.vector.tensor_scalar(out=ms[:, 0:n], in0=st["ssum", u][:, 0:n], scalar1=1.0 / D, scalar2=EPS, op0=ALU.mult, op1=ALU.add)
+            nc.scalar.activation(out=ms[:, 0:n], in_=ssum[:, 0:n], func=ACT.Copy, scale=1.0 / D, bias=EPS)
             rstd = work.tile([P, 2], F32, name="rstd")
             nc.gpsimd.tensor_tensor(out=rstd[:, 0:n], in0=ms[:, 0:n], in1=neg_half[:, 0:n], op=ALU.pow)
             st["rstd", u] = rstd
 
-        def n_stage(u):
-            for a in span(u):
+        def norm(u):
+            for a in range(width(u)):
                 xn = work.tile([P, D], BF16, name="xn%d" % a, align_bytes=64)
                 nc.vector.scalar_tensor_tensor(
-                    out=xn[:], in0=st["x1", u][:, a, :], scalar=st["rstd", u][:, a : a + 1], in1=g2_all[:], op0=ALU.mult, op1=ALU.mult
+                    out=xn[:], in0=slot(u)[:, a * D : (a + 1) * D], scalar=st["rstd", u][:, a : a + 1], in1=g2_ps[:], op0=ALU.mult, op1=ALU.mult
                 )
                 st["xn", u, a] = xn
 
-        def nt_stage(u):
-            bank = psum1.tile([P, 2, 2, P], F32, name="nT_ps")
-            for a in span(u):
-                words = st["xn", u, a][:].bitcast(F32)
-                for e in range(2):
-                    nc.tensor.transpose(bank[:, a, e, :], words[:, e : 2 * P : 2], ident[:])
-            st["nT", u] = bank
-
-        def nc_stage(u):
-            st["ng", u] = copy_words(nc.scalar.copy, st["nT", u], u, "ng")
-
-        def qn_stage(u):
-            st["qn", u] = quant(u, st["ng", u], "qn")
-
-        def uv_stage(u):
-            codes, scales = st["qn", u]
+        def gate_up(u):
+            codes, scales = st["q", u + LAG]
             gate = psum1.tile([P, 2, F], F32, name="u_ps")
             up = psum1.tile([P, 2, F], F32, name="v_ps")
-            for a in span(u):
-                for dst, f0 in ((gate, 0), (up, F)):
+            for dst, f0 in ((gate, 0), (up, F)):
+                for a in range(width(u)):
+                    c0 = (width(u + LAG) + a) * P
                     nc.tensor.matmul_mx(
                         out=dst[:, a, :],
-                        lhsT=codes[:, a * P : (a + 1) * P].bitcast(FP8X4),
-                        lhsT_scale=scales[:, a * P : (a + 1) * P],
+                        lhsT=codes[:, c0 : c0 + P].bitcast(FP8X4),
+                        lhsT_scale=scales[:, c0 : c0 + P],
                         rhs=w_codes[:, f0 : f0 + F].bitcast(FP8X4),
                         rhs_scale=w_scales[:, f0 : f0 + F],
                         start=True,
@@ -233,17 +199,17 @@ def tile_transformerblock_pb_t_kernel(tc, x, ao, wo_bytes, wo_scale, bo, g2, w1,
                     )
             st["uv", u] = (gate, up)
 
-        def sl_stage(u):
-            n = WIDTHS[u]
+        def silu(u):
+            n = width(u)
             sil = work.tile([P, 2, F], F32, name="sil")
             nc.scalar.activation(out=sil[:, 0:n], in_=st["uv", u][0][:, 0:n], func=ACT.Silu)
             st["sil", u] = sil
 
-        def ml_stage(u):
-            n = WIDTHS[u]
+        def product(u):
+            n = width(u)
             h = hres.tile([P, 2, F], F32, name="h")
             nc.vector.tensor_tensor(out=h[:, 0:n], in0=st["uv", u][1][:, 0:n], in1=st["sil", u][:, 0:n], op=ALU.mult)
-            nc.sync.dma_start(out=hbm_rows(out_1, u, F), in_=h[:, 0:n, :])
+            nc.sync.dma_start(out=hbm_rows(out_1, u), in_=h[:, 0:n, :])
 
         wide = const.tile([P, J, D], BF16, align_bytes=64)
         wo_g = const.tile([P, D, J], BF16, align_bytes=64)
@@ -252,70 +218,57 @@ def tile_transformerblock_pb_t_kernel(tc, x, ao, wo_bytes, wo_scale, bo, g2, w1,
         w_g = const.tile([P, 2 * F, J], BF16, align_bytes=64)
         w_codes = const.tile([P, 2 * F], U32, align_bytes=64)
         w_scales = const.tile([P, 2 * F], U8, align_bytes=64)
-        bo_col = const.tile([P, C], F32)
-        g2_all = const.tile([P, D], BF16)
+        bo_all = const.tile([P, D], BF16)
+        bo_ps = psum1.tile([P, D], F32, name="bo_ps")
+        g2_ps = psum1.tile([P, D], F32, name="g2_ps")
 
         def interleave(copy, dst, src):
             copy(out=dst.rearrange("p (c i) t -> p c t i", i=4), in_=src.rearrange("p t (c i) -> p c t i", i=4))
 
-        warm_ps = psum1.tile([P, D], F32, name="v_ps")
-        for i in range(4):
-            nc.tensor.matmul(warm_ps[:], lhsT=ones[:], rhs=zeros[:], start=True, stop=True)
-        for t in range(J):
-            if t < 3:
-                nc.vector.tensor_scalar(out=wide[:, t, :], in0=wob[:, t, :].bitcast(FP8), scalar1=wsc[:, t : t + 1], scalar2=None, op0=ALU.mult)
-            else:
-                nc.scalar.activation(out=wide[:, t, :], in_=wob[:, t, :].bitcast(FP8), func=ACT.Copy, scale=wsc[:, t : t + 1])
+        for t in range(J - 1):
+            nc.vector.tensor_scalar(out=wide[:, t, :], in0=wob[:, t, :].bitcast(FP8), scalar1=wsc[:, t : t + 1], scalar2=None, op0=ALU.mult)
+        nc.scalar.activation(out=wide[:, J - 1, :], in_=wob[:, J - 1, :].bitcast(FP8), func=ACT.Copy, scale=wsc[:, J - 1 : J])
+        turn_a(0)
+        stage_a(0)
+        nc.tensor.matmul(bo_ps[:], lhsT=ones[:], rhs=rows[:, 0, :], start=True, stop=True)
+        nc.tensor.matmul(g2_ps[:], lhsT=ones[:], rhs=rows[:, 1, :], start=True, stop=True)
+        interleave(nc.vector.tensor_copy, wo_g[:, 0:CUT, :], wide[:, :, 0:CUT])
+        interleave(nc.scalar.copy, wo_g[:, CUT:D, :], wide[:, :, CUT:D])
+        nc.scalar.copy(out=bo_all[:], in_=bo_ps[:])
 
-        def ok(u):
-            return 0 <= u < NU
+        def live(u):
+            return width(u) > 0
 
-        for s in range(-3, NU + 4):
-            if ok(s - 2):
-                nt_stage(s - 2)
-            if ok(s + 3):
-                t_stage(s + 3)
-            if ok(s - 3):
-                sl_stage(s - 3)
-            if ok(s - 2):
-                nc_stage(s - 2)
-            if ok(s + 2):
-                qa_stage(s + 2)
-            if ok(s - 1):
-                r_stage(s - 1)
-            if ok(s):
-                x_stage(s)
-                sq_stage(s)
-            if s == -3:
-                interleave(nc.vector.tensor_copy, wo_g[:, 0:CUT, :], wide[:, :, 0:CUT])
-                interleave(nc.scalar.copy, wo_g[:, CUT:D, :], wide[:, :, CUT:D])
-                nc.vector.quantize_mx(out=wo_codes[:].bitcast(FP8X4), scales=wo_scales[:], in_=wo_g[:].rearrange("p n j -> p (n j)"))
-                bo_ps = psum1.tile([P, P], F32, name="nT_ps")
-                nc.tensor.matmul(bo_ps[:], lhsT=bo_rows[:], rhs=ident_bf[:], start=True, stop=True)
-                nc.scalar.copy(out=bo_col[:], in_=bo_ps[:, 0:C])
-            if ok(s + 2):
-                yt_stage(s + 2)
-            if ok(s + 3):
-                c_stage(s + 3)
-            if s == -1:
-                g2_ps = psum1.tile([P, D], F32, name="u_ps")
-                nc.tensor.matmul(g2_ps[:], lhsT=ones[:], rhs=g2_row[:], start=True, stop=True)
-                nc.scalar.copy(out=g2_all[:], in_=g2_ps[:])
-            if ok(s + 1):
-                yk_stage(s + 1)
-            if s == 0:
-                interleave(nc.vector.tensor_copy, w_g[:, 0:F, :], w_raw1[:])
-                interleave(nc.vector.tensor_copy, w_g[:, F : 2 * F, :], w_raw3[:])
-            if ok(s - 3):
-                ml_stage(s - 3)
-            if ok(s + 2):
-                ybv_stage(s + 2)
-                yb_stage(s + 2)
-            if ok(s - 2):
-                qn_stage(s - 2)
-            if s == 1:
+        turn_a(1)
+        for p in range(-1, NU + LAG - 1):
+            if p == 2:
                 nc.vector.quantize_mx(out=w_codes[:].bitcast(FP8X4), scales=w_scales[:], in_=w_g[:].rearrange("p n j -> p (n j)"))
-            if ok(s - 1):
-                n_stage(s - 1)
-            if ok(s - 2):
-                uv_stage(s - 2)
+            quantise(p + 1)
+            if p == -1:
+                nc.vector.quantize_mx(out=wo_codes[:].bitcast(FP8X4), scales=wo_scales[:], in_=wo_g[:].rearrange("p n j -> p (n j)"))
+                bias_vector(0)
+            elif live(p + 1):
+                bias_gpsimd(p + 1)
+            if live(p + 2):
+                stage_a(p + 2)
+            if live(p - 1):
+                squares(p - 1)
+            if p in (0, 1):
+                interleave(nc.scalar.copy, w_g[:, p * F : (p + 1) * F, :], w_raw[:, p])
+            if live(p - 3):
+                gate_up(p - 3)
+            if live(p - 2):
+                norm(p - 2)
+                turn_n(p - 2)
+            if live(p - 3):
+                silu(p - 3)
+            if live(p - 2):
+                stage_n(p - 2)
+            if live(p + 3):
+                turn_a(p + 3)
+            if live(p):
+                residual(p)
+            if live(p + 1):
+                project(p + 1)
+            if live(p - 3):
+                product(p - 3)

@@ -24,7 +24,10 @@ WIDTHS = (1, 1) + (2,) * 14 + (1, 1)
 NU = len(WIDTHS)
 FIRST = tuple(sum(WIDTHS[:u]) for u in range(NU))
 LAG = 4
+EARLY = 2
+W_STEP = 3
 CUT = 320
+GPSIMD_COLS = 384
 WORDS = D // 2
 
 
@@ -45,13 +48,12 @@ def tile_transformerblock_pb_t_kernel(tc, x, ao, wo_bytes, wo_scale, bo, g2, w1,
         nc.vector.memset(ones[:], 1.0)
         ident = const.tile([P, P], F32)
         make_identity(nc, ident[:])
+        ident_bf = const.tile([P, P], BF16)
+        nc.vector.tensor_copy(out=ident_bf[:], in_=ident[:])
         neg_half = const.tile([P, 2], F32)
         nc.gpsimd.memset(neg_half[:], -0.5)
 
         wsc = const.tile([P, J], F32)
-        nc.scalar.dma_start(out=wsc[:], in_=wo_scale.rearrange("(p t) o -> p (t o)", t=J))
-        nc.scalar.dma_start(out=rows[0:1, 0, :], in_=bo.rearrange("(o n) -> o n", o=1))
-        nc.scalar.dma_start(out=rows[0:1, 1, :], in_=g2.rearrange("(o n) -> o n", o=1))
 
         wob = const.tile([P, J, D], U8, align_bytes=64)
         ao_t = {}
@@ -69,15 +71,21 @@ def tile_transformerblock_pb_t_kernel(tc, x, ao, wo_bytes, wo_scale, bo, g2, w1,
                 x_t[k0 + i] = (xt, i)
 
         w_raw = const.tile([P, 2, J, F], BF16, align_bytes=64)
+        nc.sync.dma_start(out=wsc[:], in_=wo_scale.rearrange("(p t) o -> p (t o)", t=J))
         nc.sync.dma_start(out=wob[:], in_=wo_bytes.rearrange("(p t) n -> p t n", t=J))
         load_ao(0)
+        nc.sync.dma_start(out=rows[0:1, 0, :], in_=bo.rearrange("(o n) -> o n", o=1))
         load_x(0, 2)
         for k in range(1, 4):
             load_ao(k)
         load_x(2, 2)
-        nc.sync.dma_start(out=w_raw[:, 0], in_=w1.rearrange("(p j) f -> p j f", j=J))
-        nc.sync.dma_start(out=w_raw[:, 1], in_=w3.rearrange("(p j) f -> p j f", j=J))
-        for k0 in range(4, TILES, 4):
+        nc.sync.dma_start(out=rows[0:1, 1, :], in_=g2.rearrange("(o n) -> o n", o=1))
+        for i, w in enumerate((w1, w3)):
+            nc.sync.dma_start(out=w_raw[:, i], in_=w.rearrange("(p j) f -> p j f", j=J))
+            load_ao(4 + 2 * i)
+            load_ao(5 + 2 * i)
+            load_x(4 + 2 * i, 2)
+        for k0 in range(8, TILES, 4):
             for k in range(k0, k0 + 4):
                 load_ao(k)
             load_x(k0, 4)
@@ -91,6 +99,9 @@ def tile_transformerblock_pb_t_kernel(tc, x, ao, wo_bytes, wo_scale, bo, g2, w1,
             if ("slot", u) not in st:
                 st["slot", u] = loads.tile([P, 2 * D], F32, name="slot%d" % u, align_bytes=64)
             return st["slot", u]
+
+        def staging(u):
+            return slot(u + 1 if u else 0)
 
         def hbm_rows(t, u):
             b, i0 = FIRST[u] // I, FIRST[u] % I
@@ -111,34 +122,47 @@ def tile_transformerblock_pb_t_kernel(tc, x, ao, wo_bytes, wo_scale, bo, g2, w1,
             st["aT", u] = turn([ao_t[FIRST[u] + a][:].rearrange("p h d -> p (h d)") for a in range(width(u))], "aT_ps")
 
         def stage_a(u):
-            stage(st["aT", u], width(u), slot(u)[:, 0 : width(u) * WORDS])
+            stage(st["aT", u], width(u), staging(u)[:, 0 : width(u) * WORDS])
 
         def turn_n(u):
             st["nT", u] = turn([st["xn", u, a][:] for a in range(width(u))], "nT_ps")
 
         def stage_n(u):
             w0 = width(u + LAG) * WORDS
-            stage(st["nT", u], width(u), slot(u + LAG)[:, w0 : w0 + width(u) * WORDS])
+            stage(st["nT", u], width(u), staging(u + LAG)[:, w0 : w0 + width(u) * WORDS])
 
         def quantise(u):
             n = width(u) + width(u - LAG)
+            if n == 0:
+                return
             codes = work.tile([P, 4 * P], U32, name="codes", align_bytes=64)
             scales = work.tile([P, 4 * P], U8, name="scales", align_bytes=64)
-            nc.vector.quantize_mx(out=codes[:, 0 : n * P].bitcast(FP8X4), scales=scales[:, 0 : n * P], in_=slot(u)[:, 0 : n * WORDS].bitcast(BF16))
+            nc.vector.quantize_mx(out=codes[:, 0 : n * P].bitcast(FP8X4), scales=scales[:, 0 : n * P], in_=staging(u)[:, 0 : n * WORDS].bitcast(BF16))
             st["q", u] = (codes, scales)
 
         def x_rows(u):
             xt, i = x_t[FIRST[u]]
-            return xt[:, i : i + width(u), :]
+            return xt[:, i : i + width(u), :].rearrange("p a d -> p (a d)")
+
+        def cut(u):
+            return 0 if u == 0 else width(u) * (D // 2 if u < EARLY else GPSIMD_COLS)
 
         def bias_gpsimd(u):
-            n = width(u)
-            nc.gpsimd.tensor_tensor(
-                out=slot(u)[:, 0 : n * D].rearrange("p (a d) -> p a d", a=n), in0=x_rows(u), in1=bo_all[:].unsqueeze(1).to_broadcast([P, n, D]), op=ALU.add
-            )
+            nc.gpsimd.tensor_tensor(out=slot(u)[:, 0 : cut(u)], in0=x_rows(u)[:, 0 : cut(u)], in1=bo_all[:, 0 : cut(u)], op=ALU.add)
 
         def bias_vector(u):
-            nc.vector.tensor_tensor(out=slot(u)[:, 0:D], in0=bo_ps[:], in1=x_rows(u)[:, 0, :], op=ALU.add)
+            n = width(u) * D - cut(u)
+            nc.vector.tensor_tensor(out=slot(u)[:, cut(u) : width(u) * D], in0=bo_ps[:, D - n : D], in1=x_rows(u)[:, cut(u) :], op=ALU.add)
+
+        def bias_tensor(u):
+            n = width(u) * D - cut(u)
+            bank = psum1.tile([P, D], F32, name="xb_ps")
+            nc.tensor.matmul(bank[:, 0:n], lhsT=ident_bf[:], rhs=x_rows(u)[:, cut(u) :], start=True, stop=False)
+            nc.tensor.matmul(bank[:, 0:n], lhsT=ones[:], rhs=rows[:, 0, D - n : D], start=False, stop=True)
+            st["xb", u] = bank
+
+        def bias_scalar(u):
+            nc.scalar.copy(out=slot(u)[:, cut(u) : width(u) * D], in_=st["xb", u][:, 0 : width(u) * D - cut(u)])
 
         def project(u):
             codes, scales = st["q", u]
@@ -167,6 +191,11 @@ def tile_transformerblock_pb_t_kernel(tc, x, ao, wo_bytes, wo_scale, bo, g2, w1,
             for a in range(n):
                 sq = work.tile([P, D], BF16, name="sq")
                 nc.scalar.activation(out=sq[:], in_=slot(u)[:, a * D : (a + 1) * D], func=ACT.Square, accum_out=ssum[:, a : a + 1])
+            st["ssum", u] = ssum
+
+        def inverse_root(u):
+            n = width(u)
+            ssum = st["ssum", u]
             ms = work.tile([P, 2], F32, name="ms")
             nc.scalar.activation(out=ms[:, 0:n], in_=ssum[:, 0:n], func=ACT.Copy, scale=1.0 / D, bias=EPS)
             rstd = work.tile([P, 2], F32, name="rstd")
@@ -212,14 +241,14 @@ def tile_transformerblock_pb_t_kernel(tc, x, ao, wo_bytes, wo_scale, bo, g2, w1,
             nc.sync.dma_start(out=hbm_rows(out_1, u), in_=h[:, 0:n, :])
 
         wide = const.tile([P, J, D], BF16, align_bytes=64)
-        wo_g = const.tile([P, D, J], BF16, align_bytes=64)
+        wo_g = slot(1)[:].bitcast(BF16).rearrange("p (n j) -> p n j", j=J)
         wo_codes = const.tile([P, D], U32, align_bytes=64)
         wo_scales = const.tile([P, D], U8, align_bytes=64)
         w_g = const.tile([P, 2 * F, J], BF16, align_bytes=64)
         w_codes = const.tile([P, 2 * F], U32, align_bytes=64)
         w_scales = const.tile([P, 2 * F], U8, align_bytes=64)
-        bo_all = const.tile([P, D], BF16)
-        bo_ps = psum1.tile([P, D], F32, name="bo_ps")
+        bo_all = const.tile([P, 2 * GPSIMD_COLS], BF16)
+        bo_ps = psum1.tile([P, D], F32, name="u_ps")
         g2_ps = psum1.tile([P, D], F32, name="g2_ps")
 
         def interleave(copy, dst, src):
@@ -231,44 +260,46 @@ def tile_transformerblock_pb_t_kernel(tc, x, ao, wo_bytes, wo_scale, bo, g2, w1,
         turn_a(0)
         stage_a(0)
         nc.tensor.matmul(bo_ps[:], lhsT=ones[:], rhs=rows[:, 0, :], start=True, stop=True)
-        nc.tensor.matmul(g2_ps[:], lhsT=ones[:], rhs=rows[:, 1, :], start=True, stop=True)
+        turn_a(1)
         interleave(nc.vector.tensor_copy, wo_g[:, 0:CUT, :], wide[:, :, 0:CUT])
         interleave(nc.scalar.copy, wo_g[:, CUT:D, :], wide[:, :, CUT:D])
-        nc.scalar.copy(out=bo_all[:], in_=bo_ps[:])
 
-        def live(u):
-            return width(u) > 0
+        quantise(0)
+        bias_vector(0)
+        nc.scalar.copy(out=bo_all[:, 0:D], in_=bo_ps[:])
+        stage_a(1)
+        nc.vector.quantize_mx(out=wo_codes[:].bitcast(FP8X4), scales=wo_scales[:], in_=slot(1)[:].bitcast(BF16))
+        project(0)
+        nc.vector.tensor_copy(out=bo_all[:, D:], in_=bo_all[:, 0 : 2 * GPSIMD_COLS - D])
 
-        turn_a(1)
-        for p in range(-1, NU + LAG - 1):
-            if p == 2:
+        def each(stage_fn, u, first=0):
+            if u >= first and width(u) > 0:
+                stage_fn(u)
+
+        for p in range(NU + LAG + 1):
+            if p == W_STEP:
                 nc.vector.quantize_mx(out=w_codes[:].bitcast(FP8X4), scales=w_scales[:], in_=w_g[:].rearrange("p n j -> p (n j)"))
-            quantise(p + 1)
-            if p == -1:
-                nc.vector.quantize_mx(out=wo_codes[:].bitcast(FP8X4), scales=wo_scales[:], in_=wo_g[:].rearrange("p n j -> p (n j)"))
-                bias_vector(0)
-            elif live(p + 1):
-                bias_gpsimd(p + 1)
-            if live(p + 2):
-                stage_a(p + 2)
-            if live(p - 1):
-                squares(p - 1)
-            if p in (0, 1):
-                interleave(nc.scalar.copy, w_g[:, p * F : (p + 1) * F, :], w_raw[:, p])
-            if live(p - 3):
-                gate_up(p - 3)
-            if live(p - 2):
-                norm(p - 2)
-                turn_n(p - 2)
-            if live(p - 3):
-                silu(p - 3)
-            if live(p - 2):
-                stage_n(p - 2)
-            if live(p + 3):
-                turn_a(p + 3)
-            if live(p):
-                residual(p)
-            if live(p + 1):
-                project(p + 1)
-            if live(p - 3):
-                product(p - 3)
+            if p >= 1:
+                quantise(p)
+            each(bias_gpsimd, p + 1)
+            if p + 1 < EARLY:
+                bias_vector(p + 1)
+            each(project, p, first=1)
+            if p == 1:
+                nc.tensor.matmul(g2_ps[:], lhsT=ones[:], rhs=rows[:, 1, :], start=True, stop=True)
+            each(product, p - LAG - 1)
+            each(squares, p - 1)
+            each(stage_n, p - LAG + 1)
+            each(bias_scalar, p + 1, first=EARLY)
+            each(inverse_root, p - 1)
+            each(turn_a, p + 2)
+            each(stage_a, p + 2)
+            if W_STEP - 2 <= p + 1 < W_STEP:
+                i = p + 3 - W_STEP
+                interleave(nc.scalar.copy, w_g[:, i * F : (i + 1) * F, :], w_raw[:, i])
+            each(gate_up, p - LAG)
+            each(bias_tensor, p + 2, first=EARLY)
+            each(norm, p - 2)
+            each(turn_n, p - 2)
+            each(silu, p - LAG)
+            each(residual, p)

@@ -54,6 +54,8 @@ def tile_transformerblock_pb_t_kernel(tc, x, ao, wo_bytes, wo_scale, bo, g2, w1,
         nc.gpsimd.memset(neg_half[:], -0.5)
 
         wsc = const.tile([P, J], F32)
+        warm = const.tile([P, 2], F32)
+        nc.scalar.activation(out=warm[:], in_=neg_half[:], func=ACT.Silu)
 
         wob = const.tile([P, J, D], U8, align_bytes=64)
         ao_t = {}

@@ -20,10 +20,10 @@ P = 128
 J = 4
 I = S // P
 TILES = B * I
-WIDTHS = (1, 1) + (2,) * 14 + (1, 1)
+WIDTHS = (2,) * 16
 NU = len(WIDTHS)
 FIRST = tuple(sum(WIDTHS[:u]) for u in range(NU))
-LAG = 4
+LAG = 5
 EARLY = 2
 W_STEP = 3
 CUT = 320
@@ -76,21 +76,22 @@ def tile_transformerblock_pb_t_kernel(tc, x, ao, wo_bytes, wo_scale, bo, g2, w1,
         nc.sync.dma_start(out=wsc[:], in_=wo_scale.rearrange("(p t) o -> p (t o)", t=J))
         nc.sync.dma_start(out=wob[:], in_=wo_bytes.rearrange("(p t) n -> p t n", t=J))
         load_ao(0)
+        load_ao(1)
         nc.sync.dma_start(out=rows[0:1, 0, :], in_=bo.rearrange("(o n) -> o n", o=1))
+        load_ao(2)
         load_x(0, 2)
-        for k in range(1, 4):
-            load_ao(k)
+        load_ao(3)
         load_x(2, 2)
         nc.sync.dma_start(out=rows[0:1, 1, :], in_=g2.rearrange("(o n) -> o n", o=1))
         for i, w in enumerate((w1, w3)):
-            nc.sync.dma_start(out=w_raw[:, i], in_=w.rearrange("(p j) f -> p j f", j=J))
             load_ao(4 + 2 * i)
             load_ao(5 + 2 * i)
+            nc.sync.dma_start(out=w_raw[:, i], in_=w.rearrange("(p j) f -> p j f", j=J))
             load_x(4 + 2 * i, 2)
-        for k0 in range(8, TILES, 4):
-            for k in range(k0, k0 + 4):
-                load_ao(k)
-            load_x(k0, 4)
+        for k0 in range(8, TILES, 2):
+            load_ao(k0)
+            load_ao(k0 + 1)
+            load_x(k0, 2)
 
         st = {}
 
@@ -103,7 +104,7 @@ def tile_transformerblock_pb_t_kernel(tc, x, ao, wo_bytes, wo_scale, bo, g2, w1,
             return st["slot", u]
 
         def staging(u):
-            return slot(u + 1 if u else 0)
+            return slot(u)
 
         def hbm_rows(t, u):
             b, i0 = FIRST[u] // I, FIRST[u] % I
@@ -120,14 +121,14 @@ def tile_transformerblock_pb_t_kernel(tc, x, ao, wo_bytes, wo_scale, bo, g2, w1,
         def stage(bank, n, dst):
             nc.scalar.copy(out=dst.rearrange("p (a r e) -> p a r e", a=n, e=2), in_=bank[:, 0:n].rearrange("p a e r -> p a r e"))
 
-        def turn_a(u):
-            st["aT", u] = turn([ao_t[FIRST[u] + a][:].rearrange("p h d -> p (h d)") for a in range(width(u))], "aT_ps")
+        def turn_a(u, bank="aT_ps"):
+            st["aT", u] = turn([ao_t[FIRST[u] + a][:].rearrange("p h d -> p (h d)") for a in range(width(u))], bank)
 
         def stage_a(u):
             stage(st["aT", u], width(u), staging(u)[:, 0 : width(u) * WORDS])
 
         def turn_n(u):
-            st["nT", u] = turn([st["xn", u, a][:] for a in range(width(u))], "nT_ps")
+            st["nT", u] = turn([st["xn", u, a][:] for a in range(width(u))], "aT_ps" if u == NU - 2 else "nT_ps")
 
         def stage_n(u):
             w0 = width(u + LAG) * WORDS
@@ -153,8 +154,10 @@ def tile_transformerblock_pb_t_kernel(tc, x, ao, wo_bytes, wo_scale, bo, g2, w1,
             nc.gpsimd.tensor_tensor(out=slot(u)[:, 0 : cut(u)], in0=x_rows(u)[:, 0 : cut(u)], in1=bo_all[:, 0 : cut(u)], op=ALU.add)
 
         def bias_vector(u):
-            n = width(u) * D - cut(u)
-            nc.vector.tensor_tensor(out=slot(u)[:, cut(u) : width(u) * D], in0=bo_ps[:, D - n : D], in1=x_rows(u)[:, cut(u) :], op=ALU.add)
+            for a in range(width(u)):
+                c0 = max(cut(u), a * D)
+                if c0 < (a + 1) * D:
+                    nc.vector.tensor_tensor(out=slot(u)[:, c0 : (a + 1) * D], in0=bo_ps[:, c0 - a * D : D], in1=x_rows(u)[:, c0 : (a + 1) * D], op=ALU.add)
 
         def bias_tensor(u):
             n = width(u) * D - cut(u)
@@ -214,8 +217,12 @@ def tile_transformerblock_pb_t_kernel(tc, x, ao, wo_bytes, wo_scale, bo, g2, w1,
 
         def gate_up(u):
             codes, scales = st["q", u + LAG]
-            gate = psum1.tile([P, 2, F], F32, name="u_ps")
-            up = psum1.tile([P, 2, F], F32, name="v_ps")
+            if u in (NU - 2, NU - 4):
+                gate = psum2.tile([P, 2, F], F32, name="y_ps")
+                up = psum2.tile([P, 2, F], F32, name="y_ps")
+            else:
+                gate = psum1.tile([P, 2, F], F32, name="u_ps")
+                up = psum1.tile([P, 2, F], F32, name="v_ps")
             for dst, f0 in ((gate, 0), (up, F)):
                 for a in range(width(u)):
                     c0 = (width(u + LAG) + a) * P
@@ -243,7 +250,7 @@ def tile_transformerblock_pb_t_kernel(tc, x, ao, wo_bytes, wo_scale, bo, g2, w1,
             nc.sync.dma_start(out=hbm_rows(out_1, u), in_=h[:, 0:n, :])
 
         wide = const.tile([P, J, D], BF16, align_bytes=64)
-        wo_g = slot(1)[:].bitcast(BF16).rearrange("p (n j) -> p n j", j=J)
+        wo_g = const.tile([P, D, J], BF16, align_bytes=64)
         wo_codes = const.tile([P, D], U32, align_bytes=64)
         wo_scales = const.tile([P, D], U8, align_bytes=64)
         w_g = const.tile([P, 2 * F, J], BF16, align_bytes=64)
@@ -260,48 +267,83 @@ def tile_transformerblock_pb_t_kernel(tc, x, ao, wo_bytes, wo_scale, bo, g2, w1,
             nc.vector.tensor_scalar(out=wide[:, t, :], in0=wob[:, t, :].bitcast(FP8), scalar1=wsc[:, t : t + 1], scalar2=None, op0=ALU.mult)
         nc.scalar.activation(out=wide[:, J - 1, :], in_=wob[:, J - 1, :].bitcast(FP8), func=ACT.Copy, scale=wsc[:, J - 1 : J])
         turn_a(0)
-        stage_a(0)
         nc.tensor.matmul(bo_ps[:], lhsT=ones[:], rhs=rows[:, 0, :], start=True, stop=True)
-        turn_a(1)
+        turn_a(1, "nT_ps")
         interleave(nc.vector.tensor_copy, wo_g[:, 0:CUT, :], wide[:, :, 0:CUT])
         interleave(nc.scalar.copy, wo_g[:, CUT:D, :], wide[:, :, CUT:D])
-
+        stage_a(0)
+        stage_a(1)
+        nc.vector.quantize_mx(out=wo_codes[:].bitcast(FP8X4), scales=wo_scales[:], in_=wo_g[:].rearrange("p n j -> p (n j)"))
         quantise(0)
         bias_vector(0)
         nc.scalar.copy(out=bo_all[:, 0:D], in_=bo_ps[:])
-        stage_a(1)
-        nc.vector.quantize_mx(out=wo_codes[:].bitcast(FP8X4), scales=wo_scales[:], in_=slot(1)[:].bitcast(BF16))
-        project(0)
-        nc.vector.tensor_copy(out=bo_all[:, D:], in_=bo_all[:, 0 : 2 * GPSIMD_COLS - D])
+        nc.scalar.copy(out=bo_all[:, D:], in_=bo_all[:, 0 : 2 * GPSIMD_COLS - D])
 
         def each(stage_fn, u, first=0):
             if u >= first and width(u) > 0:
                 stage_fn(u)
 
-        for p in range(NU + LAG + 1):
+        for p in range(NU - 1):
+            each(project, p)
+            each(bias_tensor, p + 1, first=EARLY)
             if p == W_STEP:
                 nc.vector.quantize_mx(out=w_codes[:].bitcast(FP8X4), scales=w_scales[:], in_=w_g[:].rearrange("p n j -> p (n j)"))
-            if p >= 1:
-                quantise(p)
+            quantise(p + 1)
             each(bias_gpsimd, p + 1)
-            if p + 1 < EARLY:
-                bias_vector(p + 1)
-            each(project, p, first=1)
-            if p == 1:
+            if p == 0:
                 nc.tensor.matmul(g2_ps[:], lhsT=ones[:], rhs=rows[:, 1, :], start=True, stop=True)
-            each(product, p - LAG - 1)
+            each(product, p - LAG)
             each(squares, p - 1)
-            each(stage_n, p - LAG + 1)
             each(bias_scalar, p + 1, first=EARLY)
             each(inverse_root, p - 1)
+            each(stage_n, p - LAG + 2)
             each(turn_a, p + 2)
             each(stage_a, p + 2)
-            if W_STEP - 2 <= p + 1 < W_STEP:
-                i = p + 3 - W_STEP
+            if W_STEP - 2 <= p < W_STEP:
+                i = p + 2 - W_STEP
                 interleave(nc.scalar.copy, w_g[:, i * F : (i + 1) * F, :], w_raw[:, i])
-            each(gate_up, p - LAG)
-            each(bias_tensor, p + 2, first=EARLY)
+            each(gate_up, p + 1 - LAG)
             each(norm, p - 2)
             each(turn_n, p - 2)
-            each(silu, p - LAG)
+            each(silu, p + 1 - LAG)
             each(residual, p)
+            if p + 1 < EARLY:
+                bias_vector(p + 1)
+        last = NU - 1
+        project(last)
+        quantise(last + LAG - 4)
+        product(last - 5)
+        squares(last - 1)
+        residual(last)
+        inverse_root(last - 1)
+        stage_n(last - 3)
+        squares(last)
+        gate_up(last - 4)
+        inverse_root(last)
+        norm(last - 2)
+        turn_n(last - 2)
+        quantise(last + LAG - 3)
+        gate_up(last - 3)
+        silu(last - 4)
+        norm(last - 1)
+        turn_n(last - 1)
+        stage_n(last - 2)
+        norm(last)
+        turn_n(last)
+        product(last - 4)
+        silu(last - 3)
+        stage_n(last - 1)
+        quantise(last + LAG - 2)
+        gate_up(last - 2)
+        product(last - 3)
+        stage_n(last)
+        quantise(last + LAG - 1)
+        gate_up(last - 1)
+        silu(last - 2)
+        quantise(last + LAG)
+        product(last - 2)
+        gate_up(last)
+        silu(last - 1)
+        silu(last)
+        product(last - 1)
+        product(last)

@@ -24,10 +24,10 @@ WIDTHS = (2,) * 16
 NU = len(WIDTHS)
 FIRST = tuple(sum(WIDTHS[:u]) for u in range(NU))
 LAG = 5
-EARLY = 2
+EARLY = 4
 W_STEP = 3
 CUT = 320
-GPSIMD_COLS = 384
+GPSIMD_COLS = 320
 WORDS = D // 2
 
 
@@ -42,10 +42,10 @@ def tile_transformerblock_pb_t_kernel(tc, x, ao, wo_bytes, wo_scale, bo, g2, w1,
         psum1 = ctx.enter_context(tc.psum_pool(name="psum1", bufs=1))
         ctx.enter_context(tc.manual_schedule())
 
-        rows = const.tile([P, 2, D], BF16)
-        nc.vector.memset(rows[:], 0.0)
         ones = const.tile([P, P], BF16)
         nc.vector.memset(ones[:], 1.0)
+        rows = const.tile([P, 2, D], BF16)
+        nc.vector.memset(rows[:], 0.0)
         ident = const.tile([P, P], F32)
         make_identity(nc, ident[:])
         ident_bf = const.tile([P, P], BF16)
@@ -55,7 +55,7 @@ def tile_transformerblock_pb_t_kernel(tc, x, ao, wo_bytes, wo_scale, bo, g2, w1,
 
         wsc = const.tile([P, J], F32)
         warm = const.tile([P, 2], F32)
-        nc.scalar.activation(out=warm[:], in_=neg_half[:], func=ACT.Silu)
+        nc.scalar.activation(out=warm[:], in_=ones[:, 0:2], func=ACT.Silu)
 
         wob = const.tile([P, J, D], U8, align_bytes=64)
         ao_t = {}
@@ -79,15 +79,18 @@ def tile_transformerblock_pb_t_kernel(tc, x, ao, wo_bytes, wo_scale, bo, g2, w1,
         load_ao(1)
         nc.sync.dma_start(out=rows[0:1, 0, :], in_=bo.rearrange("(o n) -> o n", o=1))
         load_ao(2)
-        load_x(0, 2)
         load_ao(3)
+        load_x(0, 2)
         load_x(2, 2)
+        nc.sync.dma_start(out=w_raw[:, 0], in_=w1.rearrange("(p j) f -> p j f", j=J))
         nc.sync.dma_start(out=rows[0:1, 1, :], in_=g2.rearrange("(o n) -> o n", o=1))
-        for i, w in enumerate((w1, w3)):
-            load_ao(4 + 2 * i)
-            load_ao(5 + 2 * i)
-            nc.sync.dma_start(out=w_raw[:, i], in_=w.rearrange("(p j) f -> p j f", j=J))
-            load_x(4 + 2 * i, 2)
+        load_ao(4)
+        load_ao(5)
+        nc.sync.dma_start(out=w_raw[:, 1], in_=w3.rearrange("(p j) f -> p j f", j=J))
+        load_x(4, 2)
+        load_ao(6)
+        load_ao(7)
+        load_x(6, 2)
         for k0 in range(8, TILES, 2):
             load_ao(k0)
             load_ao(k0 + 1)
@@ -272,12 +275,13 @@ def tile_transformerblock_pb_t_kernel(tc, x, ao, wo_bytes, wo_scale, bo, g2, w1,
         interleave(nc.vector.tensor_copy, wo_g[:, 0:CUT, :], wide[:, :, 0:CUT])
         interleave(nc.scalar.copy, wo_g[:, CUT:D, :], wide[:, :, CUT:D])
         stage_a(0)
+        nc.scalar.copy(out=bo_all[:, 0:D], in_=bo_ps[:])
+        nc.scalar.copy(out=bo_all[:, D:], in_=bo_all[:, 0 : 2 * GPSIMD_COLS - D])
         stage_a(1)
         nc.vector.quantize_mx(out=wo_codes[:].bitcast(FP8X4), scales=wo_scales[:], in_=wo_g[:].rearrange("p n j -> p (n j)"))
         quantise(0)
         bias_vector(0)
-        nc.scalar.copy(out=bo_all[:, 0:D], in_=bo_ps[:])
-        nc.scalar.copy(out=bo_all[:, D:], in_=bo_all[:, 0 : 2 * GPSIMD_COLS - D])
+        interleave(nc.scalar.copy, w_g[:, 0:F, :], w_raw[:, 0])
 
         def each(stage_fn, u, first=0):
             if u >= first and width(u) > 0:
@@ -299,9 +303,8 @@ def tile_transformerblock_pb_t_kernel(tc, x, ao, wo_bytes, wo_scale, bo, g2, w1,
             each(stage_n, p - LAG + 2)
             each(turn_a, p + 2)
             each(stage_a, p + 2)
-            if W_STEP - 2 <= p < W_STEP:
-                i = p + 2 - W_STEP
-                interleave(nc.scalar.copy, w_g[:, i * F : (i + 1) * F, :], w_raw[:, i])
+            if p == 1:
+                interleave(nc.scalar.copy, w_g[:, 1 * F : 2 * F, :], w_raw[:, 1])
             each(gate_up, p + 1 - LAG)
             each(norm, p - 2)
             each(turn_n, p - 2)

@@ -24,10 +24,10 @@ WIDTHS = (2,) * 16
 NU = len(WIDTHS)
 FIRST = tuple(sum(WIDTHS[:u]) for u in range(NU))
 LAG = 5
-EARLY = 4
+EARLY = 5
 W_STEP = 3
 CUT = 320
-GPSIMD_COLS = 320
+GPSIMD_COLS = 352
 WORDS = D // 2
 
 
@@ -57,7 +57,7 @@ def tile_transformerblock_pb_t_kernel(tc, x, ao, wo_bytes, wo_scale, bo, g2, w1,
         warm = const.tile([P, 2], F32)
         nc.scalar.activation(out=warm[:], in_=ones[:, 0:2], func=ACT.Silu)
 
-        wob = const.tile([P, J, D], U8, align_bytes=64)
+        wob = [const.tile([P, 2, D], U8, name="wob%d" % half, align_bytes=64) for half in range(2)]
         ao_t = {}
         x_t = {}
 
@@ -74,22 +74,23 @@ def tile_transformerblock_pb_t_kernel(tc, x, ao, wo_bytes, wo_scale, bo, g2, w1,
 
         w_raw = const.tile([P, 2, J, F], BF16, align_bytes=64)
         nc.sync.dma_start(out=wsc[:], in_=wo_scale.rearrange("(p t) o -> p (t o)", t=J))
-        nc.sync.dma_start(out=wob[:], in_=wo_bytes.rearrange("(p t) n -> p t n", t=J))
+        for half in range(2):
+            nc.sync.dma_start(out=wob[half][:], in_=wo_bytes.rearrange("(p t) n -> p t n", t=J)[:, 2 * half : 2 * half + 2, :])
         load_ao(0)
         load_ao(1)
         nc.sync.dma_start(out=rows[0:1, 0, :], in_=bo.rearrange("(o n) -> o n", o=1))
+        nc.sync.dma_start(out=rows[0:1, 1, :], in_=g2.rearrange("(o n) -> o n", o=1))
         load_ao(2)
         load_ao(3)
         load_x(0, 2)
         load_x(2, 2)
-        nc.sync.dma_start(out=w_raw[:, 0], in_=w1.rearrange("(p j) f -> p j f", j=J))
-        nc.sync.dma_start(out=rows[0:1, 1, :], in_=g2.rearrange("(o n) -> o n", o=1))
         load_ao(4)
         load_ao(5)
-        nc.sync.dma_start(out=w_raw[:, 1], in_=w3.rearrange("(p j) f -> p j f", j=J))
+        nc.sync.dma_start(out=w_raw[:, 0], in_=w1.rearrange("(p j) f -> p j f", j=J))
         load_x(4, 2)
         load_ao(6)
         load_ao(7)
+        nc.sync.dma_start(out=w_raw[:, 1], in_=w3.rearrange("(p j) f -> p j f", j=J))
         load_x(6, 2)
         for k0 in range(8, TILES, 2):
             load_ao(k0)
@@ -240,17 +241,19 @@ def tile_transformerblock_pb_t_kernel(tc, x, ao, wo_bytes, wo_scale, bo, g2, w1,
                     )
             st["uv", u] = (gate, up)
 
-        def silu(u):
-            n = width(u)
+        def silu(u, pieces=1):
             sil = work.tile([P, 2, F], F32, name="sil")
-            nc.scalar.activation(out=sil[:, 0:n], in_=st["uv", u][0][:, 0:n], func=ACT.Silu)
+            n = width(u) // pieces
+            for a in range(0, width(u), n):
+                nc.scalar.activation(out=sil[:, a : a + n], in_=st["uv", u][0][:, a : a + n], func=ACT.Silu)
             st["sil", u] = sil
 
-        def product(u):
-            n = width(u)
+        def product(u, pieces=1):
             h = hres.tile([P, 2, F], F32, name="h")
-            nc.vector.tensor_tensor(out=h[:, 0:n], in0=st["uv", u][1][:, 0:n], in1=st["sil", u][:, 0:n], op=ALU.mult)
-            nc.sync.dma_start(out=hbm_rows(out_1, u), in_=h[:, 0:n, :])
+            n = width(u) // pieces
+            for a in range(0, width(u), n):
+                nc.vector.tensor_tensor(out=h[:, a : a + n], in0=st["uv", u][1][:, a : a + n], in1=st["sil", u][:, a : a + n], op=ALU.mult)
+                nc.sync.dma_start(out=hbm_rows(out_1, u)[:, a : a + n, :], in_=h[:, a : a + n, :])
 
         wide = const.tile([P, J, D], BF16, align_bytes=64)
         wo_g = const.tile([P, D, J], BF16, align_bytes=64)
@@ -267,10 +270,11 @@ def tile_transformerblock_pb_t_kernel(tc, x, ao, wo_bytes, wo_scale, bo, g2, w1,
             copy(out=dst.rearrange("p (c i) t -> p c t i", i=4), in_=src.rearrange("p t (c i) -> p c t i", i=4))
 
         for t in range(J - 1):
-            nc.vector.tensor_scalar(out=wide[:, t, :], in0=wob[:, t, :].bitcast(FP8), scalar1=wsc[:, t : t + 1], scalar2=None, op0=ALU.mult)
-        nc.scalar.activation(out=wide[:, J - 1, :], in_=wob[:, J - 1, :].bitcast(FP8), func=ACT.Copy, scale=wsc[:, J - 1 : J])
+            nc.vector.tensor_scalar(out=wide[:, t, :], in0=wob[t // 2][:, t % 2, :].bitcast(FP8), scalar1=wsc[:, t : t + 1], scalar2=None, op0=ALU.mult)
+        nc.scalar.activation(out=wide[:, J - 1, :], in_=wob[1][:, 1, :].bitcast(FP8), func=ACT.Copy, scale=wsc[:, J - 1 : J])
         turn_a(0)
         nc.tensor.matmul(bo_ps[:], lhsT=ones[:], rhs=rows[:, 0, :], start=True, stop=True)
+        nc.tensor.matmul(g2_ps[:], lhsT=ones[:], rhs=rows[:, 1, :], start=True, stop=True)
         turn_a(1, "nT_ps")
         interleave(nc.vector.tensor_copy, wo_g[:, 0:CUT, :], wide[:, :, 0:CUT])
         interleave(nc.scalar.copy, wo_g[:, CUT:D, :], wide[:, :, CUT:D])
@@ -280,8 +284,8 @@ def tile_transformerblock_pb_t_kernel(tc, x, ao, wo_bytes, wo_scale, bo, g2, w1,
         stage_a(1)
         nc.vector.quantize_mx(out=wo_codes[:].bitcast(FP8X4), scales=wo_scales[:], in_=wo_g[:].rearrange("p n j -> p (n j)"))
         quantise(0)
-        bias_vector(0)
-        interleave(nc.scalar.copy, w_g[:, 0:F, :], w_raw[:, 0])
+        nc.vector.tensor_tensor(out=slot(0)[:, 0:D], in0=bo_ps[:], in1=x_rows(0)[:, 0:D], op=ALU.add)
+        nc.gpsimd.tensor_tensor(out=slot(0)[:, D:], in0=x_rows(0)[:, D:], in1=bo_all[:, 0:D], op=ALU.add)
 
         def each(stage_fn, u, first=0):
             if u >= first and width(u) > 0:
@@ -294,8 +298,6 @@ def tile_transformerblock_pb_t_kernel(tc, x, ao, wo_bytes, wo_scale, bo, g2, w1,
                 nc.vector.quantize_mx(out=w_codes[:].bitcast(FP8X4), scales=w_scales[:], in_=w_g[:].rearrange("p n j -> p (n j)"))
             quantise(p + 1)
             each(bias_gpsimd, p + 1)
-            if p == 0:
-                nc.tensor.matmul(g2_ps[:], lhsT=ones[:], rhs=rows[:, 1, :], start=True, stop=True)
             each(product, p - LAG)
             each(squares, p - 1)
             each(bias_scalar, p + 1, first=EARLY)
@@ -303,6 +305,8 @@ def tile_transformerblock_pb_t_kernel(tc, x, ao, wo_bytes, wo_scale, bo, g2, w1,
             each(stage_n, p - LAG + 2)
             each(turn_a, p + 2)
             each(stage_a, p + 2)
+            if p == 0:
+                interleave(nc.scalar.copy, w_g[:, 0 * F : 1 * F, :], w_raw[:, 0])
             if p == 1:
                 interleave(nc.scalar.copy, w_g[:, 1 * F : 2 * F, :], w_raw[:, 1])
             each(gate_up, p + 1 - LAG)
@@ -347,6 +351,6 @@ def tile_transformerblock_pb_t_kernel(tc, x, ao, wo_bytes, wo_scale, bo, g2, w1,
         product(last - 2)
         gate_up(last)
         silu(last - 1)
-        silu(last)
+        silu(last, 2)
         product(last - 1)
-        product(last)
+        product(last, 2)

@@ -24,8 +24,7 @@ WIDTHS = (2,) * 16
 NU = len(WIDTHS)
 FIRST = tuple(sum(WIDTHS[:u]) for u in range(NU))
 LAG = 5
-EARLY = 5
-W_STEP = 3
+EARLY = 3
 CUT = 320
 GPSIMD_COLS = 352
 WORDS = D // 2
@@ -76,21 +75,21 @@ def tile_transformerblock_pb_t_kernel(tc, x, ao, wo_bytes, wo_scale, bo, g2, w1,
         nc.sync.dma_start(out=wsc[:], in_=wo_scale.rearrange("(p t) o -> p (t o)", t=J))
         for half in range(2):
             nc.sync.dma_start(out=wob[half][:], in_=wo_bytes.rearrange("(p t) n -> p t n", t=J)[:, 2 * half : 2 * half + 2, :])
+        nc.sync.dma_start(out=w_raw[:, 0], in_=w1.rearrange("(p j) f -> p j f", j=J))
         load_ao(0)
-        load_ao(1)
         nc.sync.dma_start(out=rows[0:1, 0, :], in_=bo.rearrange("(o n) -> o n", o=1))
+        load_ao(1)
         nc.sync.dma_start(out=rows[0:1, 1, :], in_=g2.rearrange("(o n) -> o n", o=1))
+        nc.sync.dma_start(out=w_raw[:, 1], in_=w3.rearrange("(p j) f -> p j f", j=J))
         load_ao(2)
         load_ao(3)
         load_x(0, 2)
         load_x(2, 2)
         load_ao(4)
         load_ao(5)
-        nc.sync.dma_start(out=w_raw[:, 0], in_=w1.rearrange("(p j) f -> p j f", j=J))
         load_x(4, 2)
         load_ao(6)
         load_ao(7)
-        nc.sync.dma_start(out=w_raw[:, 1], in_=w3.rearrange("(p j) f -> p j f", j=J))
         load_x(6, 2)
         for k0 in range(8, TILES, 2):
             load_ao(k0)
@@ -152,7 +151,7 @@ def tile_transformerblock_pb_t_kernel(tc, x, ao, wo_bytes, wo_scale, bo, g2, w1,
             return xt[:, i : i + width(u), :].rearrange("p a d -> p (a d)")
 
         def cut(u):
-            return 0 if u == 0 else width(u) * (D // 2 if u < EARLY else GPSIMD_COLS)
+            return 0 if u == 0 else width(u) * (128 if u < EARLY else 256 if u < 6 else GPSIMD_COLS)
 
         def bias_gpsimd(u):
             nc.gpsimd.tensor_tensor(out=slot(u)[:, 0 : cut(u)], in0=x_rows(u)[:, 0 : cut(u)], in1=bo_all[:, 0 : cut(u)], op=ALU.add)
@@ -278,12 +277,15 @@ def tile_transformerblock_pb_t_kernel(tc, x, ao, wo_bytes, wo_scale, bo, g2, w1,
         turn_a(1, "nT_ps")
         interleave(nc.vector.tensor_copy, wo_g[:, 0:CUT, :], wide[:, :, 0:CUT])
         interleave(nc.scalar.copy, wo_g[:, CUT:D, :], wide[:, :, CUT:D])
+        interleave(nc.vector.tensor_copy, w_g[:, 0:F, :], w_raw[:, 0])
+        nc.vector.quantize_mx(out=wo_codes[:].bitcast(FP8X4), scales=wo_scales[:], in_=wo_g[:].rearrange("p n j -> p (n j)"))
+        interleave(nc.vector.tensor_copy, w_g[:, F : 2 * F, :], w_raw[:, 1])
         stage_a(0)
         nc.scalar.copy(out=bo_all[:, 0:D], in_=bo_ps[:])
         nc.scalar.copy(out=bo_all[:, D:], in_=bo_all[:, 0 : 2 * GPSIMD_COLS - D])
         stage_a(1)
-        nc.vector.quantize_mx(out=wo_codes[:].bitcast(FP8X4), scales=wo_scales[:], in_=wo_g[:].rearrange("p n j -> p (n j)"))
         quantise(0)
+        nc.vector.quantize_mx(out=w_codes[:].bitcast(FP8X4), scales=w_scales[:], in_=w_g[:].rearrange("p n j -> p (n j)"))
         nc.vector.tensor_tensor(out=slot(0)[:, 0:D], in0=bo_ps[:], in1=x_rows(0)[:, 0:D], op=ALU.add)
         nc.gpsimd.tensor_tensor(out=slot(0)[:, D:], in0=x_rows(0)[:, D:], in1=bo_all[:, 0:D], op=ALU.add)
 
@@ -293,9 +295,8 @@ def tile_transformerblock_pb_t_kernel(tc, x, ao, wo_bytes, wo_scale, bo, g2, w1,
 
         for p in range(NU - 1):
             each(project, p)
-            each(bias_tensor, p + 1, first=EARLY)
-            if p == W_STEP:
-                nc.vector.quantize_mx(out=w_codes[:].bitcast(FP8X4), scales=w_scales[:], in_=w_g[:].rearrange("p n j -> p (n j)"))
+            if p == 0:
+                residual(0)
             quantise(p + 1)
             each(bias_gpsimd, p + 1)
             each(product, p - LAG)
@@ -305,15 +306,12 @@ def tile_transformerblock_pb_t_kernel(tc, x, ao, wo_bytes, wo_scale, bo, g2, w1,
             each(stage_n, p - LAG + 2)
             each(turn_a, p + 2)
             each(stage_a, p + 2)
-            if p == 0:
-                interleave(nc.scalar.copy, w_g[:, 0 * F : 1 * F, :], w_raw[:, 0])
-            if p == 1:
-                interleave(nc.scalar.copy, w_g[:, 1 * F : 2 * F, :], w_raw[:, 1])
             each(gate_up, p + 1 - LAG)
+            each(bias_tensor, p + 2, first=EARLY)
             each(norm, p - 2)
             each(turn_n, p - 2)
             each(silu, p + 1 - LAG)
-            each(residual, p)
+            each(residual, p, first=1)
             if p + 1 < EARLY:
                 bias_vector(p + 1)
         last = NU - 1

@@ -17,25 +17,27 @@ EPS = 1e-6
 FLOPS = 2 * B * S * (H * DK * D + D * 2 * F)
 
 P = 128
-J = 4
-I = S // P
-TILES = B * I
-WIDTHS = (2,) * 16
-NU = len(WIDTHS)
-FIRST = tuple(sum(WIDTHS[:u]) for u in range(NU))
-LAG = 5
-EARLY = 3
-CUT = 320
-GPSIMD_COLS = 352
+PACK = 4
+ROWS = S // P
+PAIR = 2
+UNITS = B * ROWS // PAIR
+LAST = UNITS - 1
 WORDS = D // 2
+PAD = 16
+LAG = 5
+
+VECTOR_HELPS = 3
+SCALAR_HALF = 6
+GPSIMD_FIRST, GPSIMD_NEXT, GPSIMD_STEADY = 256, 512, 704
+WO_VECTOR = 320
 
 
 def tile_transformerblock_pb_t_kernel(tc, x, ao, wo_bytes, wo_scale, bo, g2, w1, w3, out_0, out_1):
     nc = tc.nc
     with ExitStack() as ctx:
         const = ctx.enter_context(tc.tile_pool(name="const", bufs=1))
-        loads = ctx.enter_context(tc.tile_pool(name="loads", bufs=1))
-        hres = ctx.enter_context(tc.tile_pool(name="hres", bufs=10))
+        keep = ctx.enter_context(tc.tile_pool(name="keep", bufs=1))
+        results = ctx.enter_context(tc.tile_pool(name="results", bufs=10))
         work = ctx.enter_context(tc.tile_pool(name="work", bufs=3))
         psum2 = ctx.enter_context(tc.psum_pool(name="psum2", bufs=2))
         psum1 = ctx.enter_context(tc.psum_pool(name="psum1", bufs=1))
@@ -49,306 +51,277 @@ def tile_transformerblock_pb_t_kernel(tc, x, ao, wo_bytes, wo_scale, bo, g2, w1,
         make_identity(nc, ident[:])
         ident_bf = const.tile([P, P], BF16)
         nc.vector.tensor_copy(out=ident_bf[:], in_=ident[:])
-        neg_half = const.tile([P, 2], F32)
+        neg_half = const.tile([P, PAIR], F32)
         nc.gpsimd.memset(neg_half[:], -0.5)
-
-        wsc = const.tile([P, J], F32)
         warm = const.tile([P, 2], F32)
         nc.scalar.activation(out=warm[:], in_=ones[:, 0:2], func=ACT.Silu)
 
-        wob = [const.tile([P, 2, D], U8, name="wob%d" % half, align_bytes=64) for half in range(2)]
-        ao_t = {}
-        x_t = {}
+        wo_sc = const.tile([P, PACK], F32)
+        wo_raw = [const.tile([P, 2, D], U8, name="wo_raw%d" % half, align_bytes=64) for half in range(2)]
+        w_raw = const.tile([P, 2, PACK, F], BF16, align_bytes=64)
+        a_tiles = {}
+        x_units = {}
 
-        def load_ao(k):
-            at = loads.tile([P, H, DK], BF16, name="ao%d" % k, align_bytes=64)
-            nc.sync.dma_start(out=at[:], in_=ao[k // I].rearrange("h (p i) d -> p i h d", i=I)[:, k % I, :, :])
-            ao_t[k] = at
+        def unit_rows(t, u):
+            b, i = divmod(PAIR * u, ROWS)
+            return t[b].rearrange("(p i) d -> p i d", i=ROWS)[:, i : i + PAIR, :]
 
-        def load_x(k0, n):
-            xt = loads.tile([P, n, D], BF16, name="x%d" % k0, align_bytes=64)
-            nc.sync.dma_start(out=xt[:], in_=x[k0 // I].rearrange("(p i) d -> p i d", i=I)[:, k0 % I : k0 % I + n, :])
-            for i in range(n):
-                x_t[k0 + i] = (xt, i)
+        def load_a(tile):
+            a_tiles[tile] = keep.tile([P, H, DK], BF16, name="a%d" % tile, align_bytes=64)
+            src = ao[tile // ROWS].rearrange("h (p i) d -> p i h d", i=ROWS)[:, tile % ROWS, :, :]
+            nc.sync.dma_start(out=a_tiles[tile][:], in_=src)
 
-        w_raw = const.tile([P, 2, J, F], BF16, align_bytes=64)
-        nc.sync.dma_start(out=wsc[:], in_=wo_scale.rearrange("(p t) o -> p (t o)", t=J))
+        def load_x(u):
+            xt = keep.tile([P, PAIR, D], BF16, name="x%d" % u, align_bytes=64)
+            nc.sync.dma_start(out=xt[:], in_=unit_rows(x, u))
+            x_units[u] = xt[:].rearrange("p a d -> p (a d)")
+
+        def load_w(i, w):
+            nc.sync.dma_start(out=w_raw[:, i], in_=w.rearrange("(p t) f -> p t f", t=PACK))
+
+        def load_row(i, v):
+            nc.sync.dma_start(out=rows[0:1, i, :], in_=v.rearrange("(o n) -> o n", o=1))
+
+        nc.sync.dma_start(out=wo_sc[:], in_=wo_scale.rearrange("(p t) o -> p (t o)", t=PACK))
         for half in range(2):
-            nc.sync.dma_start(out=wob[half][:], in_=wo_bytes.rearrange("(p t) n -> p t n", t=J)[:, 2 * half : 2 * half + 2, :])
-        nc.sync.dma_start(out=w_raw[:, 0], in_=w1.rearrange("(p j) f -> p j f", j=J))
-        load_ao(0)
-        nc.sync.dma_start(out=rows[0:1, 0, :], in_=bo.rearrange("(o n) -> o n", o=1))
-        load_ao(1)
-        nc.sync.dma_start(out=rows[0:1, 1, :], in_=g2.rearrange("(o n) -> o n", o=1))
-        nc.sync.dma_start(out=w_raw[:, 1], in_=w3.rearrange("(p j) f -> p j f", j=J))
-        load_ao(2)
-        load_ao(3)
-        load_x(0, 2)
-        load_x(2, 2)
-        load_ao(4)
-        load_ao(5)
-        load_x(4, 2)
-        load_ao(6)
-        load_ao(7)
-        load_x(6, 2)
-        for k0 in range(8, TILES, 2):
-            load_ao(k0)
-            load_ao(k0 + 1)
-            load_x(k0, 2)
+            nc.sync.dma_start(out=wo_raw[half][:], in_=wo_bytes.rearrange("(p t) n -> p t n", t=PACK)[:, 2 * half : 2 * half + 2, :])
+        load_w(0, w1)
+        load_a(0)
+        load_row(0, bo)
+        load_a(1)
+        load_row(1, g2)
+        load_w(1, w3)
+        load_a(2)
+        load_a(3)
+        load_x(0)
+        load_x(1)
+        for u in range(2, UNITS):
+            load_a(PAIR * u)
+            load_a(PAIR * u + 1)
+            load_x(u)
 
-        st = {}
+        homes = [keep.tile([P, PAD + PAIR * D + PAD], F32, name="home%d" % u, align_bytes=64) for u in range(UNITS + LAG)]
+        for u in range(UNITS):
+            nc.vector.memset(homes[u][:, PAD - 1 : PAD + PAIR * D + 1 : PAIR * D + 1], (D * EPS) ** 0.5)
 
-        def width(u):
-            return WIDTHS[u] if 0 <= u < NU else 0
+        def home(u, first, last):
+            return homes[u][:, PAD + first : PAD + last]
 
-        def slot(u):
-            if ("slot", u) not in st:
-                st["slot", u] = loads.tile([P, 2 * D], F32, name="slot%d" % u, align_bytes=64)
-            return st["slot", u]
+        def a_count(u):
+            return PAIR if u < UNITS else 0
 
-        def staging(u):
-            return slot(u)
+        made = {}
 
-        def hbm_rows(t, u):
-            b, i0 = FIRST[u] // I, FIRST[u] % I
-            return t[b].rearrange("(p i) d -> p i d", i=I)[:, i0 : i0 + WIDTHS[u], :]
-
-        def turn(rows_bf16, name):
-            bank = psum1.tile([P, 2, 2, P], F32, name=name)
+        def turn(rows_bf16, bank_name):
+            bank = psum1.tile([P, PAIR, 2, P], F32, name=bank_name)
             for a, row in enumerate(rows_bf16):
                 words = row.bitcast(F32)
                 for e in range(2):
-                    nc.tensor.transpose(bank[:, a, e, :], words[:, e : 2 * P : 2], ident[:])
+                    nc.tensor.transpose(bank[:, a, e, :], words[:, e : WORDS : 2], ident[:])
             return bank
 
-        def stage(bank, n, dst):
-            nc.scalar.copy(out=dst.rearrange("p (a r e) -> p a r e", a=n, e=2), in_=bank[:, 0:n].rearrange("p a e r -> p a r e"))
+        def copy_turned(bank, u, first):
+            dst = home(u, first, first + PAIR * WORDS).rearrange("p (a r e) -> p a r e", a=PAIR, e=2)
+            nc.scalar.copy(out=dst, in_=bank[:].rearrange("p a e r -> p a r e"))
 
-        def turn_a(u, bank="aT_ps"):
-            st["aT", u] = turn([ao_t[FIRST[u] + a][:].rearrange("p h d -> p (h d)") for a in range(width(u))], bank)
+        def turn_a(u, bank_name="aT_ps"):
+            made["aT", u] = turn([a_tiles[PAIR * u + a][:].rearrange("p h d -> p (h d)") for a in range(PAIR)], bank_name)
 
-        def stage_a(u):
-            stage(st["aT", u], width(u), staging(u)[:, 0 : width(u) * WORDS])
+        def copy_a(u):
+            copy_turned(made["aT", u], u, 0)
 
-        def turn_n(u):
-            st["nT", u] = turn([st["xn", u, a][:] for a in range(width(u))], "aT_ps" if u == NU - 2 else "nT_ps")
+        def turn_n(u, bank_name="nT_ps"):
+            made["nT", u] = turn([made["n", u, a][:] for a in range(PAIR)], bank_name)
 
-        def stage_n(u):
-            w0 = width(u + LAG) * WORDS
-            stage(st["nT", u], width(u), staging(u + LAG)[:, w0 : w0 + width(u) * WORDS])
+        def copy_n(u):
+            copy_turned(made["nT", u], u + LAG, a_count(u + LAG) * WORDS)
 
         def quantise(u):
-            n = width(u) + width(u - LAG)
-            if n == 0:
-                return
-            codes = work.tile([P, 4 * P], U32, name="codes", align_bytes=64)
-            scales = work.tile([P, 4 * P], U8, name="scales", align_bytes=64)
-            nc.vector.quantize_mx(out=codes[:, 0 : n * P].bitcast(FP8X4), scales=scales[:, 0 : n * P], in_=staging(u)[:, 0 : n * WORDS].bitcast(BF16))
-            st["q", u] = (codes, scales)
+            tiles = a_count(u) + (PAIR if u >= LAG else 0)
+            codes = work.tile([P, 2 * PAIR * P], U32, name="codes", align_bytes=64)
+            scales = work.tile([P, 2 * PAIR * P], U8, name="scales", align_bytes=64)
+            nc.vector.quantize_mx(
+                out=codes[:, 0 : tiles * P].bitcast(FP8X4), scales=scales[:, 0 : tiles * P], in_=home(u, 0, tiles * WORDS).bitcast(BF16)
+            )
+            made["q", u] = (codes, scales)
 
-        def x_rows(u):
-            xt, i = x_t[FIRST[u]]
-            return xt[:, i : i + width(u), :].rearrange("p a d -> p (a d)")
-
-        def cut(u):
-            return 0 if u == 0 else width(u) * (128 if u < EARLY else 256 if u < 6 else GPSIMD_COLS)
+        def gpsimd_cols(u):
+            return GPSIMD_FIRST if u < VECTOR_HELPS else GPSIMD_NEXT if u < SCALAR_HALF else GPSIMD_STEADY
 
         def bias_gpsimd(u):
-            nc.gpsimd.tensor_tensor(out=slot(u)[:, 0 : cut(u)], in0=x_rows(u)[:, 0 : cut(u)], in1=bo_all[:, 0 : cut(u)], op=ALU.add)
+            n = gpsimd_cols(u)
+            nc.gpsimd.tensor_tensor(out=home(u, 0, n), in0=x_units[u][:, 0:n], in1=bo_all[:, 0:n], op=ALU.add)
 
         def bias_vector(u):
-            for a in range(width(u)):
-                c0 = max(cut(u), a * D)
-                if c0 < (a + 1) * D:
-                    nc.vector.tensor_tensor(out=slot(u)[:, c0 : (a + 1) * D], in0=bo_ps[:, c0 - a * D : D], in1=x_rows(u)[:, c0 : (a + 1) * D], op=ALU.add)
+            for first, last in ((gpsimd_cols(u), D), (D, PAIR * D)):
+                nc.vector.tensor_tensor(out=home(u, first, last), in0=bo_ps[:, first % D : D], in1=x_units[u][:, first:last], op=ALU.add)
 
         def bias_tensor(u):
-            n = width(u) * D - cut(u)
+            n = PAIR * D - gpsimd_cols(u)
             bank = psum1.tile([P, D], F32, name="xb_ps")
-            nc.tensor.matmul(bank[:, 0:n], lhsT=ident_bf[:], rhs=x_rows(u)[:, cut(u) :], start=True, stop=False)
+            nc.tensor.matmul(bank[:, 0:n], lhsT=ident_bf[:], rhs=x_units[u][:, gpsimd_cols(u) :], start=True, stop=False)
             nc.tensor.matmul(bank[:, 0:n], lhsT=ones[:], rhs=rows[:, 0, D - n : D], start=False, stop=True)
-            st["xb", u] = bank
+            made["xb", u] = bank[:, 0:n]
 
         def bias_scalar(u):
-            nc.scalar.copy(out=slot(u)[:, cut(u) : width(u) * D], in_=st["xb", u][:, 0 : width(u) * D - cut(u)])
+            nc.scalar.copy(out=home(u, gpsimd_cols(u), PAIR * D), in_=made["xb", u])
+
+        def mx(out, q, tile, w_codes, w_scales):
+            codes, scales = q
+            cols = slice(tile * P, (tile + 1) * P)
+            nc.tensor.matmul_mx(
+                out=out, lhsT=codes[:, cols].bitcast(FP8X4), lhsT_scale=scales[:, cols], rhs=w_codes.bitcast(FP8X4), rhs_scale=w_scales, start=True, stop=True
+            )
 
         def project(u):
-            codes, scales = st["q", u]
-            for a in range(width(u)):
-                bank = psum2.tile([P, D], F32, name="y_ps")
-                nc.tensor.matmul_mx(
-                    out=bank[:],
-                    lhsT=codes[:, a * P : (a + 1) * P].bitcast(FP8X4),
-                    lhsT_scale=scales[:, a * P : (a + 1) * P],
-                    rhs=wo_codes[:].bitcast(FP8X4),
-                    rhs_scale=wo_scales[:],
-                    start=True,
-                    stop=True,
-                )
-                st["y", u, a] = bank
+            for a in range(PAIR):
+                made["y", u, a] = psum2.tile([P, D], F32, name="y_ps")
+                mx(made["y", u, a][:], made["q", u], a, wo_codes[:], wo_scales[:])
 
         def residual(u):
-            for a in range(width(u)):
-                x1 = slot(u)[:, a * D : (a + 1) * D]
-                nc.vector.tensor_tensor(out=x1, in0=st["y", u, a][:], in1=x1, op=ALU.add)
-            nc.sync.dma_start(out=hbm_rows(out_0, u), in_=slot(u)[:, 0 : width(u) * D].rearrange("p (a d) -> p a d", d=D))
+            for a in range(PAIR):
+                x1 = home(u, a * D, (a + 1) * D)
+                nc.vector.tensor_tensor(out=x1, in0=made["y", u, a][:], in1=x1, op=ALU.add)
+            nc.sync.dma_start(out=unit_rows(out_0, u), in_=home(u, 0, PAIR * D).rearrange("p (a d) -> p a d", d=D))
 
         def squares(u):
-            n = width(u)
-            ssum = work.tile([P, 2], F32, name="ssum")
-            for a in range(n):
-                sq = work.tile([P, D], BF16, name="sq")
-                nc.scalar.activation(out=sq[:], in_=slot(u)[:, a * D : (a + 1) * D], func=ACT.Square, accum_out=ssum[:, a : a + 1])
-            st["ssum", u] = ssum
+            made["ms", u] = work.tile([P, PAIR], F32, name="ms")
+            for a in range(PAIR):
+                sq = work.tile([P, D + 1], BF16, name="sq")
+                row = home(u, a * (D + 1) - 1, a * (D + 1) + D)
+                nc.scalar.activation(out=sq[:], in_=row, func=ACT.Square, scale=D**-0.5, accum_out=made["ms", u][:, a : a + 1])
 
         def inverse_root(u):
-            n = width(u)
-            ssum = st["ssum", u]
-            ms = work.tile([P, 2], F32, name="ms")
-            nc.scalar.activation(out=ms[:, 0:n], in_=ssum[:, 0:n], func=ACT.Copy, scale=1.0 / D, bias=EPS)
-            rstd = work.tile([P, 2], F32, name="rstd")
-            nc.gpsimd.tensor_tensor(out=rstd[:, 0:n], in0=ms[:, 0:n], in1=neg_half[:, 0:n], op=ALU.pow)
-            st["rstd", u] = rstd
+            made["rstd", u] = work.tile([P, PAIR], F32, name="rstd")
+            nc.gpsimd.tensor_tensor(out=made["rstd", u][:], in0=made["ms", u][:], in1=neg_half[:], op=ALU.pow)
 
         def norm(u):
-            for a in range(width(u)):
-                xn = work.tile([P, D], BF16, name="xn%d" % a, align_bytes=64)
+            for a in range(PAIR):
+                made["n", u, a] = work.tile([P, D], BF16, name="n%d" % a, align_bytes=64)
                 nc.vector.scalar_tensor_tensor(
-                    out=xn[:], in0=slot(u)[:, a * D : (a + 1) * D], scalar=st["rstd", u][:, a : a + 1], in1=g2_ps[:], op0=ALU.mult, op1=ALU.mult
+                    out=made["n", u, a][:], in0=home(u, a * D, (a + 1) * D), scalar=made["rstd", u][:, a : a + 1], in1=g2_ps[:], op0=ALU.mult, op1=ALU.mult
                 )
-                st["xn", u, a] = xn
 
-        def gate_up(u):
-            codes, scales = st["q", u + LAG]
-            if u in (NU - 2, NU - 4):
-                gate = psum2.tile([P, 2, F], F32, name="y_ps")
-                up = psum2.tile([P, 2, F], F32, name="y_ps")
-            else:
-                gate = psum1.tile([P, 2, F], F32, name="u_ps")
-                up = psum1.tile([P, 2, F], F32, name="v_ps")
-            for dst, f0 in ((gate, 0), (up, F)):
-                for a in range(width(u)):
-                    c0 = (width(u + LAG) + a) * P
-                    nc.tensor.matmul_mx(
-                        out=dst[:, a, :],
-                        lhsT=codes[:, c0 : c0 + P].bitcast(FP8X4),
-                        lhsT_scale=scales[:, c0 : c0 + P],
-                        rhs=w_codes[:, f0 : f0 + F].bitcast(FP8X4),
-                        rhs_scale=w_scales[:, f0 : f0 + F],
-                        start=True,
-                        stop=True,
-                    )
-            st["uv", u] = (gate, up)
+        def gate_up(u, pool=psum1, names=("gate_ps", "up_ps")):
+            made["uv", u] = [pool.tile([P, PAIR, F], F32, name=name) for name in names]
+            for i, bank in enumerate(made["uv", u]):
+                cols = slice(i * F, (i + 1) * F)
+                for a in range(PAIR):
+                    mx(bank[:, a, :], made["q", u + LAG], a_count(u + LAG) + a, w_codes[:, cols], w_scales[:, cols])
 
-        def silu(u, pieces=1):
-            sil = work.tile([P, 2, F], F32, name="sil")
-            n = width(u) // pieces
-            for a in range(0, width(u), n):
-                nc.scalar.activation(out=sil[:, a : a + n], in_=st["uv", u][0][:, a : a + n], func=ACT.Silu)
-            st["sil", u] = sil
+        def silu(u, step=PAIR):
+            made["silu", u] = work.tile([P, PAIR, F], F32, name="silu")
+            for a in range(0, PAIR, step):
+                nc.scalar.activation(out=made["silu", u][:, a : a + step], in_=made["uv", u][0][:, a : a + step], func=ACT.Silu)
 
-        def product(u, pieces=1):
-            h = hres.tile([P, 2, F], F32, name="h")
-            n = width(u) // pieces
-            for a in range(0, width(u), n):
-                nc.vector.tensor_tensor(out=h[:, a : a + n], in0=st["uv", u][1][:, a : a + n], in1=st["sil", u][:, a : a + n], op=ALU.mult)
-                nc.sync.dma_start(out=hbm_rows(out_1, u)[:, a : a + n, :], in_=h[:, a : a + n, :])
+        def product(u, step=PAIR):
+            h = results.tile([P, PAIR, F], F32, name="h")
+            for a in range(0, PAIR, step):
+                part = slice(a, a + step)
+                nc.vector.tensor_tensor(out=h[:, part], in0=made["uv", u][1][:, part], in1=made["silu", u][:, part], op=ALU.mult)
+                nc.sync.dma_start(out=unit_rows(out_1, u)[:, part, :], in_=h[:, part, :])
 
-        wide = const.tile([P, J, D], BF16, align_bytes=64)
-        wo_g = const.tile([P, D, J], BF16, align_bytes=64)
+        wo_wide = const.tile([P, PACK, D], BF16, align_bytes=64)
+        wo_packed = const.tile([P, D, PACK], BF16, align_bytes=64)
         wo_codes = const.tile([P, D], U32, align_bytes=64)
         wo_scales = const.tile([P, D], U8, align_bytes=64)
-        w_g = const.tile([P, 2 * F, J], BF16, align_bytes=64)
+        w_packed = const.tile([P, 2 * F, PACK], BF16, align_bytes=64)
         w_codes = const.tile([P, 2 * F], U32, align_bytes=64)
         w_scales = const.tile([P, 2 * F], U8, align_bytes=64)
-        bo_all = const.tile([P, 2 * GPSIMD_COLS], BF16)
-        bo_ps = psum1.tile([P, D], F32, name="u_ps")
+        bo_all = const.tile([P, GPSIMD_STEADY], BF16)
+        bo_ps = psum1.tile([P, D], F32, name="gate_ps")
         g2_ps = psum1.tile([P, D], F32, name="g2_ps")
 
         def interleave(copy, dst, src):
             copy(out=dst.rearrange("p (c i) t -> p c t i", i=4), in_=src.rearrange("p t (c i) -> p c t i", i=4))
 
-        for t in range(J - 1):
-            nc.vector.tensor_scalar(out=wide[:, t, :], in0=wob[t // 2][:, t % 2, :].bitcast(FP8), scalar1=wsc[:, t : t + 1], scalar2=None, op0=ALU.mult)
-        nc.scalar.activation(out=wide[:, J - 1, :], in_=wob[1][:, 1, :].bitcast(FP8), func=ACT.Copy, scale=wsc[:, J - 1 : J])
+        def quantise_weight(codes, scales, packed):
+            nc.vector.quantize_mx(out=codes[:].bitcast(FP8X4), scales=scales[:], in_=packed[:].rearrange("p n t -> p (n t)"))
+
+        for t in range(PACK - 1):
+            nc.vector.tensor_scalar(
+                out=wo_wide[:, t, :], in0=wo_raw[t // 2][:, t % 2, :].bitcast(FP8), scalar1=wo_sc[:, t : t + 1], scalar2=None, op0=ALU.mult
+            )
+        nc.scalar.activation(out=wo_wide[:, PACK - 1, :], in_=wo_raw[1][:, 1, :].bitcast(FP8), func=ACT.Copy, scale=wo_sc[:, PACK - 1 : PACK])
         turn_a(0)
         nc.tensor.matmul(bo_ps[:], lhsT=ones[:], rhs=rows[:, 0, :], start=True, stop=True)
         nc.tensor.matmul(g2_ps[:], lhsT=ones[:], rhs=rows[:, 1, :], start=True, stop=True)
         turn_a(1, "nT_ps")
-        interleave(nc.vector.tensor_copy, wo_g[:, 0:CUT, :], wide[:, :, 0:CUT])
-        interleave(nc.scalar.copy, wo_g[:, CUT:D, :], wide[:, :, CUT:D])
-        interleave(nc.vector.tensor_copy, w_g[:, 0:F, :], w_raw[:, 0])
-        nc.vector.quantize_mx(out=wo_codes[:].bitcast(FP8X4), scales=wo_scales[:], in_=wo_g[:].rearrange("p n j -> p (n j)"))
-        interleave(nc.vector.tensor_copy, w_g[:, F : 2 * F, :], w_raw[:, 1])
-        stage_a(0)
+        interleave(nc.vector.tensor_copy, wo_packed[:, 0:WO_VECTOR, :], wo_wide[:, :, 0:WO_VECTOR])
+        interleave(nc.scalar.copy, wo_packed[:, WO_VECTOR:D, :], wo_wide[:, :, WO_VECTOR:D])
+        interleave(nc.vector.tensor_copy, w_packed[:, 0:F, :], w_raw[:, 0])
+        quantise_weight(wo_codes, wo_scales, wo_packed)
+        interleave(nc.vector.tensor_copy, w_packed[:, F : 2 * F, :], w_raw[:, 1])
+        copy_a(0)
         nc.scalar.copy(out=bo_all[:, 0:D], in_=bo_ps[:])
-        nc.scalar.copy(out=bo_all[:, D:], in_=bo_all[:, 0 : 2 * GPSIMD_COLS - D])
-        stage_a(1)
+        nc.scalar.copy(out=bo_all[:, D:], in_=bo_all[:, 0 : GPSIMD_STEADY - D])
+        copy_a(1)
         quantise(0)
-        nc.vector.quantize_mx(out=w_codes[:].bitcast(FP8X4), scales=w_scales[:], in_=w_g[:].rearrange("p n j -> p (n j)"))
-        nc.vector.tensor_tensor(out=slot(0)[:, 0:D], in0=bo_ps[:], in1=x_rows(0)[:, 0:D], op=ALU.add)
-        nc.gpsimd.tensor_tensor(out=slot(0)[:, D:], in0=x_rows(0)[:, D:], in1=bo_all[:, 0:D], op=ALU.add)
+        quantise_weight(w_codes, w_scales, w_packed)
+        nc.vector.tensor_tensor(out=home(0, 0, D), in0=bo_ps[:], in1=x_units[0][:, 0:D], op=ALU.add)
+        nc.gpsimd.tensor_tensor(out=home(0, D, PAIR * D), in0=x_units[0][:, D:], in1=bo_all[:, 0:D], op=ALU.add)
 
-        def each(stage_fn, u, first=0):
-            if u >= first and width(u) > 0:
-                stage_fn(u)
+        def each(stage, u, first=0):
+            if first <= u < UNITS:
+                stage(u)
 
-        for p in range(NU - 1):
-            each(project, p)
+        for p in range(LAST):
+            project(p)
             if p == 0:
                 residual(0)
             quantise(p + 1)
-            each(bias_gpsimd, p + 1)
+            bias_gpsimd(p + 1)
             each(product, p - LAG)
             each(squares, p - 1)
-            each(bias_scalar, p + 1, first=EARLY)
+            each(bias_scalar, p + 1, first=VECTOR_HELPS)
             each(inverse_root, p - 1)
-            each(stage_n, p - LAG + 2)
+            each(copy_n, p - 3)
             each(turn_a, p + 2)
-            each(stage_a, p + 2)
+            each(copy_a, p + 2)
             each(gate_up, p + 1 - LAG)
-            each(bias_tensor, p + 2, first=EARLY)
+            each(bias_tensor, p + 2, first=VECTOR_HELPS)
             each(norm, p - 2)
             each(turn_n, p - 2)
             each(silu, p + 1 - LAG)
             each(residual, p, first=1)
-            if p + 1 < EARLY:
+            if p + 1 < VECTOR_HELPS:
                 bias_vector(p + 1)
-        last = NU - 1
-        project(last)
-        quantise(last + LAG - 4)
-        product(last - 5)
-        squares(last - 1)
-        residual(last)
-        inverse_root(last - 1)
-        stage_n(last - 3)
-        squares(last)
-        gate_up(last - 4)
-        inverse_root(last)
-        norm(last - 2)
-        turn_n(last - 2)
-        quantise(last + LAG - 3)
-        gate_up(last - 3)
-        silu(last - 4)
-        norm(last - 1)
-        turn_n(last - 1)
-        stage_n(last - 2)
-        norm(last)
-        turn_n(last)
-        product(last - 4)
-        silu(last - 3)
-        stage_n(last - 1)
-        quantise(last + LAG - 2)
-        gate_up(last - 2)
-        product(last - 3)
-        stage_n(last)
-        quantise(last + LAG - 1)
-        gate_up(last - 1)
-        silu(last - 2)
-        quantise(last + LAG)
-        product(last - 2)
-        gate_up(last)
-        silu(last - 1)
-        silu(last, 2)
-        product(last - 1)
-        product(last, 2)
+
+        projection_banks = (psum2, ("y_ps", "y_ps"))
+        project(LAST)
+        quantise(LAST - 4 + LAG)
+        product(LAST - 5)
+        squares(LAST - 1)
+        residual(LAST)
+        inverse_root(LAST - 1)
+        copy_n(LAST - 3)
+        squares(LAST)
+        gate_up(LAST - 4)
+        inverse_root(LAST)
+
+        norm(LAST - 2)
+        turn_n(LAST - 2)
+        quantise(LAST - 3 + LAG)
+        gate_up(LAST - 3, *projection_banks)
+        silu(LAST - 4)
+        norm(LAST - 1)
+        turn_n(LAST - 1, "aT_ps")
+        copy_n(LAST - 2)
+        norm(LAST)
+        turn_n(LAST)
+        silu(LAST - 3)
+        copy_n(LAST - 1)
+        copy_n(LAST)
+
+        product(LAST - 4)
+        quantise(LAST - 2 + LAG)
+        gate_up(LAST - 2)
+        product(LAST - 3)
+        quantise(LAST - 1 + LAG)
+        gate_up(LAST - 1, *projection_banks)
+        quantise(LAST + LAG)
+        for u in range(LAST - 2, UNITS):
+            if u == LAST:
+                gate_up(LAST)
+            silu(u, 1)
+            product(u, 1)

@@ -28,7 +28,7 @@ LAG = 5
 
 VECTOR_HELPS = 3
 SCALAR_HALF = 6
-GPSIMD_FIRST, GPSIMD_NEXT, GPSIMD_STEADY = 256, 512, 704
+GPSIMD_FIRST, GPSIMD_NEXT, GPSIMD_STEADY = 256, 512, 768
 WO_VECTOR = 320
 
 
@@ -38,6 +38,7 @@ def tile_transformerblock_pb_t_kernel(tc, x, ao, wo_bytes, wo_scale, bo, g2, w1,
         const = ctx.enter_context(tc.tile_pool(name="const", bufs=1))
         keep = ctx.enter_context(tc.tile_pool(name="keep", bufs=1))
         results = ctx.enter_context(tc.tile_pool(name="results", bufs=10))
+        stages = ctx.enter_context(tc.tile_pool(name="stages", bufs=3))
         work = ctx.enter_context(tc.tile_pool(name="work", bufs=3))
         psum2 = ctx.enter_context(tc.psum_pool(name="psum2", bufs=2))
         psum1 = ctx.enter_context(tc.psum_pool(name="psum1", bufs=1))
@@ -100,12 +101,23 @@ def tile_transformerblock_pb_t_kernel(tc, x, ao, wo_bytes, wo_scale, bo, g2, w1,
             load_a(PAIR * u + 1)
             load_x(u)
 
-        homes = [keep.tile([P, PAD + PAIR * D + PAD], F32, name="home%d" % u, align_bytes=64) for u in range(UNITS + LAG)]
+        homes = [keep.tile([P, PAD + PAIR * D + PAD], F32, name="home%d" % u, align_bytes=64) for u in range(UNITS)]
+        biased = [keep.tile([P, PAIR * D], F32, name="biased%d" % i, align_bytes=64) for i in range(3)]
         for u in range(UNITS):
             nc.vector.memset(homes[u][:, PAD - 1 : PAD + PAIR * D + 1 : PAIR * D + 1], (D * EPS) ** 0.5)
 
         def home(u, first, last):
             return homes[u][:, PAD + first : PAD + last]
+
+        def xb(u, first, last):
+            return biased[u % 3 if u < SCALAR_HALF else 1 + u % 2][:, first:last]
+
+        def stage(call, first, last):
+            if call < SCALAR_HALF:
+                return xb(call, first, last)
+            if ("stage", call) not in made:
+                made["stage", call] = stages.tile([P, PAIR * D], F32, name="stage", align_bytes=64)
+            return made["stage", call][:, first:last]
 
         def a_count(u):
             return PAIR if u < UNITS else 0
@@ -121,7 +133,7 @@ def tile_transformerblock_pb_t_kernel(tc, x, ao, wo_bytes, wo_scale, bo, g2, w1,
             return bank
 
         def copy_turned(bank, u, first):
-            dst = home(u, first, first + PAIR * WORDS).rearrange("p (a r e) -> p a r e", a=PAIR, e=2)
+            dst = stage(u, first, first + PAIR * WORDS).rearrange("p (a r e) -> p a r e", a=PAIR, e=2)
             nc.scalar.copy(out=dst, in_=bank[:].rearrange("p a e r -> p a r e"))
 
         def turn_a(u, bank_name="aT_ps"):
@@ -141,7 +153,7 @@ def tile_transformerblock_pb_t_kernel(tc, x, ao, wo_bytes, wo_scale, bo, g2, w1,
             codes = work.tile([P, 2 * PAIR * P], U32, name="codes", align_bytes=64)
             scales = work.tile([P, 2 * PAIR * P], U8, name="scales", align_bytes=64)
             nc.vector.quantize_mx(
-                out=codes[:, 0 : tiles * P].bitcast(FP8X4), scales=scales[:, 0 : tiles * P], in_=home(u, 0, tiles * WORDS).bitcast(BF16)
+                out=codes[:, 0 : tiles * P].bitcast(FP8X4), scales=scales[:, 0 : tiles * P], in_=stage(u, 0, tiles * WORDS).bitcast(BF16)
             )
             made["q", u] = (codes, scales)
 
@@ -150,11 +162,11 @@ def tile_transformerblock_pb_t_kernel(tc, x, ao, wo_bytes, wo_scale, bo, g2, w1,
 
         def bias_gpsimd(u):
             n = gpsimd_cols(u)
-            nc.gpsimd.tensor_tensor(out=home(u, 0, n), in0=x_units[u][:, 0:n], in1=bo_all[:, 0:n], op=ALU.add)
+            nc.gpsimd.tensor_tensor(out=xb(u, 0, n), in0=x_units[u][:, 0:n], in1=bo_all[:, 0:n], op=ALU.add)
 
         def bias_vector(u):
             for first, last in ((gpsimd_cols(u), D), (D, PAIR * D)):
-                nc.vector.tensor_tensor(out=home(u, first, last), in0=bo_ps[:, first % D : D], in1=x_units[u][:, first:last], op=ALU.add)
+                nc.vector.tensor_tensor(out=xb(u, first, last), in0=bo_ps[:, first % D : D], in1=x_units[u][:, first:last], op=ALU.add)
 
         def bias_tensor(u):
             n = PAIR * D - gpsimd_cols(u)
@@ -164,7 +176,7 @@ def tile_transformerblock_pb_t_kernel(tc, x, ao, wo_bytes, wo_scale, bo, g2, w1,
             made["xb", u] = bank[:, 0:n]
 
         def bias_scalar(u):
-            nc.scalar.copy(out=home(u, gpsimd_cols(u), PAIR * D), in_=made["xb", u])
+            nc.scalar.copy(out=xb(u, gpsimd_cols(u), PAIR * D), in_=made["xb", u])
 
         def mx(out, q, tile, w_codes, w_scales):
             codes, scales = q
@@ -181,7 +193,7 @@ def tile_transformerblock_pb_t_kernel(tc, x, ao, wo_bytes, wo_scale, bo, g2, w1,
         def residual(u):
             for a in range(PAIR):
                 x1 = home(u, a * D, (a + 1) * D)
-                nc.vector.tensor_tensor(out=x1, in0=made["y", u, a][:], in1=x1, op=ALU.add)
+                nc.vector.tensor_tensor(out=x1, in0=made["y", u, a][:], in1=xb(u, a * D, (a + 1) * D), op=ALU.add)
             nc.sync.dma_start(out=unit_rows(out_0, u), in_=home(u, 0, PAIR * D).rearrange("p (a d) -> p a d", d=D))
 
         def squares(u):
@@ -258,8 +270,8 @@ def tile_transformerblock_pb_t_kernel(tc, x, ao, wo_bytes, wo_scale, bo, g2, w1,
         copy_a(1)
         quantise(0)
         quantise_weight(w_codes, w_scales, w_packed)
-        nc.vector.tensor_tensor(out=home(0, 0, D), in0=bo_ps[:], in1=x_units[0][:, 0:D], op=ALU.add)
-        nc.gpsimd.tensor_tensor(out=home(0, D, PAIR * D), in0=x_units[0][:, D:], in1=bo_all[:, 0:D], op=ALU.add)
+        nc.vector.tensor_tensor(out=xb(0, 0, D), in0=bo_ps[:], in1=x_units[0][:, 0:D], op=ALU.add)
+        nc.gpsimd.tensor_tensor(out=xb(0, D, PAIR * D), in0=x_units[0][:, D:], in1=bo_all[:, 0:D], op=ALU.add)
 
         def each(stage, u, first=0):
             if first <= u < UNITS:

@@ -29,6 +29,7 @@ LAG = 5
 VECTOR_HELPS = 3
 SCALAR_HALF = 6
 GPSIMD_FIRST, GPSIMD_NEXT, GPSIMD_STEADY = 256, 512, 768
+REST = GPSIMD_STEADY - D
 WO_VECTOR = 320
 
 
@@ -185,16 +186,52 @@ def tile_transformerblock_pb_t_kernel(tc, x, ao, wo_bytes, wo_scale, bo, g2, w1,
                 out=out, lhsT=codes[:, cols].bitcast(FP8X4), lhsT_scale=scales[:, cols], rhs=w_codes.bitcast(FP8X4), rhs_scale=w_scales, start=True, stop=True
             )
 
+        def turned(u):
+            return u >= SCALAR_HALF and u % 2 == 0
+
         def project(u):
             for a in range(PAIR):
-                made["y", u, a] = psum2.tile([P, D], F32, name="y_ps")
-                mx(made["y", u, a][:], made["q", u], a, wo_codes[:], wo_scales[:])
+                bank = psum2.tile([P, D], F32, name="y_ps")
+                made["y", u, a] = bank
+                if a == 1 and turned(u):
+                    codes, scales = made["q", u]
+                    mx(bank[:, 0:REST], made["q", u], a, wo_codes[:, 0:REST], wo_scales[:, 0:REST])
+                    for c in range(REST // P, D // P):
+                        mx(bank[:, c * P : (c + 1) * P], (wo_codes, wo_scales), c, codes[:, P : 2 * P], scales[:, P : 2 * P])
+                else:
+                    mx(bank[:], made["q", u], a, wo_codes[:], wo_scales[:])
+
+        def copy_y(u):
+            made["yT", u] = work.tile([P, D - REST], F32, name="yT")
+            nc.scalar.copy(out=made["yT", u][:], in_=made["y", u, 1][:, REST:D])
+
+        def sum_tensor(u):
+            if not turned(u):
+                made["sums", u] = psum1.tile([P, 2, D - REST], F32, name="xb_ps")
+            out = made["sums", u + 1][:, 0, :] if turned(u) else made["sums", u][:, 1, :]
+            nc.tensor.matmul(out, lhsT=ident_bf[:], rhs=x_units[u][:, D + REST :], start=True, stop=False)
+            nc.tensor.matmul(out, lhsT=ones[:], rhs=rows[:, 0, REST:D], start=False, stop=not turned(u))
+            if turned(u):
+                chunks = (D - REST) // P
+                for c in range(chunks):
+                    cols = slice(c * P, (c + 1) * P)
+                    nc.tensor.matmul(out[:, cols], lhsT=made["yT", u][:, cols], rhs=ident[:], is_transpose=True, start=False, stop=c == chunks - 1)
+
+        def sum_scalar(u):
+            if turned(u):
+                nc.scalar.copy(out=home(u, D + REST, PAIR * D), in_=made["sums", u + 1][:, 0, :])
+            else:
+                nc.scalar.copy(out=xb(u, D + REST, PAIR * D), in_=made["sums", u][:, 1, :])
+
+        def store_x1(u):
+            nc.sync.dma_start(out=unit_rows(out_0, u), in_=home(u, 0, PAIR * D).rearrange("p (a d) -> p a d", d=D))
 
         def residual(u):
             for a in range(PAIR):
-                x1 = home(u, a * D, (a + 1) * D)
-                nc.vector.tensor_tensor(out=x1, in0=made["y", u, a][:], in1=xb(u, a * D, (a + 1) * D), op=ALU.add)
-            nc.sync.dma_start(out=unit_rows(out_0, u), in_=home(u, 0, PAIR * D).rearrange("p (a d) -> p a d", d=D))
+                n = REST if a == 1 and turned(u) else D
+                nc.vector.tensor_tensor(out=home(u, a * D, a * D + n), in0=made["y", u, a][:, 0:n], in1=xb(u, a * D, a * D + n), op=ALU.add)
+            if not turned(u):
+                store_x1(u)
 
         def squares(u):
             made["ms", u] = work.tile([P, PAIR], F32, name="ms")
@@ -284,14 +321,27 @@ def tile_transformerblock_pb_t_kernel(tc, x, ao, wo_bytes, wo_scale, bo, g2, w1,
             quantise(p + 1)
             bias_gpsimd(p + 1)
             each(product, p - LAG)
+            if turned(p - 1):
+                sum_scalar(p - 1)
+                store_x1(p - 1)
             each(squares, p - 1)
-            each(bias_scalar, p + 1, first=VECTOR_HELPS)
+            if VECTOR_HELPS <= p + 1 < SCALAR_HALF:
+                bias_scalar(p + 1)
+            elif turned(p):
+                copy_y(p)
+            elif p > SCALAR_HALF:
+                sum_scalar(p)
             each(inverse_root, p - 1)
             each(copy_n, p - 3)
             each(turn_a, p + 2)
             each(copy_a, p + 2)
             each(gate_up, p + 1 - LAG)
-            each(bias_tensor, p + 2, first=VECTOR_HELPS)
+            if VECTOR_HELPS <= p + 2 < SCALAR_HALF:
+                bias_tensor(p + 2)
+            elif turned(p):
+                sum_tensor(p)
+            elif turned(p + 1):
+                sum_tensor(p + 2)
             each(norm, p - 2)
             each(turn_n, p - 2)
             each(silu, p + 1 - LAG)
@@ -303,6 +353,9 @@ def tile_transformerblock_pb_t_kernel(tc, x, ao, wo_bytes, wo_scale, bo, g2, w1,
         project(LAST)
         quantise(LAST - 4 + LAG)
         product(LAST - 5)
+        sum_scalar(LAST)
+        sum_scalar(LAST - 1)
+        store_x1(LAST - 1)
         squares(LAST - 1)
         residual(LAST)
         inverse_root(LAST - 1)

@@ -29,6 +29,7 @@ LAG = 5
 VECTOR_HELPS = 3
 SCALAR_HALF = 6
 GPSIMD_FIRST, GPSIMD_NEXT, GPSIMD_STEADY = 256, 512, 768
+EVERY = 4
 REST = GPSIMD_STEADY - D
 WO_VECTOR = 320
 
@@ -187,7 +188,10 @@ def tile_transformerblock_pb_t_kernel(tc, x, ao, wo_bytes, wo_scale, bo, g2, w1,
             )
 
         def turned(u):
-            return u >= SCALAR_HALF and u % 2 == 0
+            return u >= SCALAR_HALF and (LAST - u) % EVERY != 0
+
+        def next_plain(u):
+            return u + (LAST - u) % EVERY
 
         def project(u):
             for a in range(PAIR):
@@ -208,7 +212,7 @@ def tile_transformerblock_pb_t_kernel(tc, x, ao, wo_bytes, wo_scale, bo, g2, w1,
         def sum_tensor(u):
             if not turned(u):
                 made["sums", u] = psum1.tile([P, 2, D - REST], F32, name="xb_ps")
-            out = made["sums", u + 1][:, 0, :] if turned(u) else made["sums", u][:, 1, :]
+            out = made["sums", next_plain(u)][:, 0, :] if turned(u) else made["sums", u][:, 1, :]
             nc.tensor.matmul(out, lhsT=ident_bf[:], rhs=x_units[u][:, D + REST :], start=True, stop=False)
             nc.tensor.matmul(out, lhsT=ones[:], rhs=rows[:, 0, REST:D], start=False, stop=not turned(u))
             if turned(u):
@@ -219,7 +223,7 @@ def tile_transformerblock_pb_t_kernel(tc, x, ao, wo_bytes, wo_scale, bo, g2, w1,
 
         def sum_scalar(u):
             if turned(u):
-                nc.scalar.copy(out=home(u, D + REST, PAIR * D), in_=made["sums", u + 1][:, 0, :])
+                nc.scalar.copy(out=home(u, D + REST, PAIR * D), in_=made["sums", next_plain(u)][:, 0, :])
             else:
                 nc.scalar.copy(out=xb(u, D + REST, PAIR * D), in_=made["sums", u][:, 1, :])
 
@@ -329,7 +333,7 @@ def tile_transformerblock_pb_t_kernel(tc, x, ao, wo_bytes, wo_scale, bo, g2, w1,
                 bias_scalar(p + 1)
             elif turned(p):
                 copy_y(p)
-            elif p > SCALAR_HALF:
+            elif p >= SCALAR_HALF:
                 sum_scalar(p)
             each(inverse_root, p - 1)
             each(copy_n, p - 3)
@@ -340,8 +344,8 @@ def tile_transformerblock_pb_t_kernel(tc, x, ao, wo_bytes, wo_scale, bo, g2, w1,
                 bias_tensor(p + 2)
             elif turned(p):
                 sum_tensor(p)
-            elif turned(p + 1):
-                sum_tensor(p + 2)
+            elif p + 1 >= SCALAR_HALF:
+                sum_tensor(next_plain(p + 1))
             each(norm, p - 2)
             each(turn_n, p - 2)
             each(silu, p + 1 - LAG)

@@ -159,6 +159,10 @@ def tile_transformerblock_pb_t_kernel(tc, x, ao, wo_bytes, wo_scale, bo, g2, w1,
             )
             made["q", u] = (codes, scales)
 
+        def warm_tensor(bank_name, pool=psum1):
+            bank = pool.tile([P, PACK, P], F32, name=bank_name)
+            nc.tensor.matmul(bank[:], lhsT=ident_bf[:], rhs=ident_bf[:].unsqueeze(1).to_broadcast([P, PACK, P]), start=True, stop=True)
+
         def gpsimd_cols(u):
             return GPSIMD_FIRST if u < VECTOR_HELPS else GPSIMD_NEXT if u < SCALAR_HALF else GPSIMD_STEADY
 
@@ -248,30 +252,48 @@ def tile_transformerblock_pb_t_kernel(tc, x, ao, wo_bytes, wo_scale, bo, g2, w1,
             made["rstd", u] = work.tile([P, PAIR], F32, name="rstd")
             nc.gpsimd.tensor_tensor(out=made["rstd", u][:], in0=made["ms", u][:], in1=neg_half[:], op=ALU.pow)
 
-        def norm(u):
-            for a in range(PAIR):
+        def gain_gpsimd(u, a, out):
+            made["gained"] = out
+            nc.gpsimd.tensor_tensor(out=out, in0=home(u, a * D, (a + 1) * D), in1=g2_all[:], op=ALU.mult)
+
+        def norm_scalar(u, a):
+            made["n", u, a] = work.tile([P, D], BF16, name="n%d" % a, align_bytes=64)
+            nc.scalar.activation(out=made["n", u, a][:], in_=made["gained"], func=ACT.Copy, scale=made["rstd", u][:, a : a + 1])
+
+        def norm(u, tiles=range(PAIR)):
+            for a in tiles:
                 made["n", u, a] = work.tile([P, D], BF16, name="n%d" % a, align_bytes=64)
                 nc.vector.scalar_tensor_tensor(
                     out=made["n", u, a][:], in0=home(u, a * D, (a + 1) * D), scalar=made["rstd", u][:, a : a + 1], in1=g2_ps[:], op0=ALU.mult, op1=ALU.mult
                 )
 
-        def gate_up(u, pool=psum1, names=("gate_ps", "up_ps")):
-            made["uv", u] = [pool.tile([P, PAIR, F], F32, name=name) for name in names]
-            for i, bank in enumerate(made["uv", u]):
-                cols = slice(i * F, (i + 1) * F)
-                for a in range(PAIR):
-                    mx(bank[:, a, :], made["q", u + LAG], a_count(u + LAG) + a, w_codes[:, cols], w_scales[:, cols])
+        def half(u, i, pool, name):
+            bank = pool.tile([P, PAIR, F], F32, name=name)
+            made["uv", u, i] = bank
+            cols = slice(i * F, (i + 1) * F)
+            for a in range(PAIR):
+                mx(bank[:, a, :], made["q", u + LAG], a_count(u + LAG) + a, w_codes[:, cols], w_scales[:, cols])
+
+        def gate(u, pool=psum1, name="gate_ps"):
+            half(u, 0, pool, name)
+
+        def up(u, pool=psum1, name="up_ps"):
+            half(u, 1, pool, name)
+
+        def gate_up(u):
+            gate(u)
+            up(u)
 
         def silu(u, step=PAIR):
             made["silu", u] = work.tile([P, PAIR, F], F32, name="silu")
             for a in range(0, PAIR, step):
-                nc.scalar.activation(out=made["silu", u][:, a : a + step], in_=made["uv", u][0][:, a : a + step], func=ACT.Silu)
+                nc.scalar.activation(out=made["silu", u][:, a : a + step], in_=made["uv", u, 0][:, a : a + step], func=ACT.Silu)
 
         def product(u, step=PAIR):
             h = results.tile([P, PAIR, F], F32, name="h")
             for a in range(0, PAIR, step):
                 part = slice(a, a + step)
-                nc.vector.tensor_tensor(out=h[:, part], in0=made["uv", u][1][:, part], in1=made["silu", u][:, part], op=ALU.mult)
+                nc.vector.tensor_tensor(out=h[:, part], in0=made["uv", u, 1][:, part], in1=made["silu", u][:, part], op=ALU.mult)
                 nc.sync.dma_start(out=unit_rows(out_1, u)[:, part, :], in_=h[:, part, :])
 
         wo_wide = const.tile([P, PACK, D], BF16, align_bytes=64)
@@ -284,6 +306,7 @@ def tile_transformerblock_pb_t_kernel(tc, x, ao, wo_bytes, wo_scale, bo, g2, w1,
         bo_all = const.tile([P, GPSIMD_STEADY], BF16)
         bo_ps = psum1.tile([P, D], F32, name="gate_ps")
         g2_ps = psum1.tile([P, D], F32, name="g2_ps")
+        g2_all = const.tile([P, D], BF16)
 
         def interleave(copy, dst, src):
             copy(out=dst.rearrange("p (c i) t -> p c t i", i=4), in_=src.rearrange("p t (c i) -> p c t i", i=4))
@@ -309,6 +332,7 @@ def tile_transformerblock_pb_t_kernel(tc, x, ao, wo_bytes, wo_scale, bo, g2, w1,
         nc.scalar.copy(out=bo_all[:, 0:D], in_=bo_ps[:])
         nc.scalar.copy(out=bo_all[:, D:], in_=bo_all[:, 0 : GPSIMD_STEADY - D])
         copy_a(1)
+        nc.scalar.copy(out=g2_all[:], in_=g2_ps[:])
         quantise(0)
         quantise_weight(w_codes, w_scales, w_packed)
         nc.vector.tensor_tensor(out=xb(0, 0, D), in0=bo_ps[:], in1=x_units[0][:, 0:D], op=ALU.add)
@@ -353,9 +377,9 @@ def tile_transformerblock_pb_t_kernel(tc, x, ao, wo_bytes, wo_scale, bo, g2, w1,
             if p + 1 < VECTOR_HELPS:
                 bias_vector(p + 1)
 
-        projection_banks = (psum2, ("y_ps", "y_ps"))
         project(LAST)
         quantise(LAST - 4 + LAG)
+        gain_gpsimd(LAST - 2, 1, stage(LAST - 4 + LAG, 0, D))
         product(LAST - 5)
         sum_scalar(LAST)
         sum_scalar(LAST - 1)
@@ -366,31 +390,40 @@ def tile_transformerblock_pb_t_kernel(tc, x, ao, wo_bytes, wo_scale, bo, g2, w1,
         copy_n(LAST - 3)
         squares(LAST)
         gate_up(LAST - 4)
-        inverse_root(LAST)
-
-        norm(LAST - 2)
-        turn_n(LAST - 2)
+        norm(LAST - 2, (0,))
+        norm_scalar(LAST - 2, 1)
         quantise(LAST - 3 + LAG)
-        gate_up(LAST - 3, *projection_banks)
+        inverse_root(LAST)
+        warm_tensor("xb_ps")
+        warm_tensor("xb_ps")
+        gate(LAST - 3, psum2, "y_ps")
+        up(LAST - 3, psum2, "y_ps")
+        turn_n(LAST - 2)
         silu(LAST - 4)
+        silu(LAST - 3)
         norm(LAST - 1)
         turn_n(LAST - 1, "aT_ps")
+        warm_tensor("gate_ps")
+        warm_tensor("gate_ps")
         copy_n(LAST - 2)
         norm(LAST)
-        turn_n(LAST)
-        silu(LAST - 3)
-        copy_n(LAST - 1)
-        copy_n(LAST)
-
         product(LAST - 4)
         quantise(LAST - 2 + LAG)
-        gate_up(LAST - 2)
+        copy_n(LAST - 1)
+        turn_n(LAST, "xb_ps")
+        gate(LAST - 2)
+        up(LAST - 2)
+        copy_n(LAST)
+        silu(LAST - 2)
         product(LAST - 3)
         quantise(LAST - 1 + LAG)
-        gate_up(LAST - 1, *projection_banks)
+        gate(LAST - 1, psum1, "nT_ps")
+        up(LAST - 1, psum1, "aT_ps")
         quantise(LAST + LAG)
-        for u in range(LAST - 2, UNITS):
-            if u == LAST:
-                gate_up(LAST)
-            silu(u, 1)
-            product(u, 1)
+        gate(LAST, psum2, "y_ps")
+        up(LAST, psum1, "xb_ps")
+        silu(LAST - 1)
+        silu(LAST, 1)
+        product(LAST - 2)
+        product(LAST - 1)
+        product(LAST, 1)

@@ -28,7 +28,7 @@ LAG = 5
 
 VECTOR_HELPS = 3
 SCALAR_HALF = 6
-GPSIMD_FIRST, GPSIMD_NEXT, GPSIMD_STEADY = 256, 512, 768
+GPSIMD_FIRST, GPSIMD_NEXT, GPSIMD_STEADY = 128, 512, 768
 EVERY = 4
 REST = GPSIMD_STEADY - D
 WO_VECTOR = 320
@@ -147,6 +147,13 @@ def tile_transformerblock_pb_t_kernel(tc, x, ao, wo_bytes, wo_scale, bo, g2, w1,
         def turn_n(u, bank_name="nT_ps"):
             made["nT", u] = turn([made["n", u, a][:] for a in range(PAIR)], bank_name)
 
+        def turn_n_tile(u, a, bank_name):
+            if a == 0:
+                made["nT", u] = psum1.tile([P, PAIR, 2, P], F32, name=bank_name)
+            words = made["n", u, a][:].bitcast(F32)
+            for e in range(2):
+                nc.tensor.transpose(made["nT", u][:, a, e, :], words[:, e:WORDS:2], ident[:])
+
         def copy_n(u):
             copy_turned(made["nT", u], u + LAG, a_count(u + LAG) * WORDS)
 
@@ -171,18 +178,18 @@ def tile_transformerblock_pb_t_kernel(tc, x, ao, wo_bytes, wo_scale, bo, g2, w1,
             nc.gpsimd.tensor_tensor(out=xb(u, 0, n), in0=x_units[u][:, 0:n], in1=bo_all[:, 0:n], op=ALU.add)
 
         def bias_vector(u):
-            for first, last in ((gpsimd_cols(u), D), (D, PAIR * D)):
+            for first, last in ((gpsimd_cols(u), D), (D, PAIR * D))[: VECTOR_HELPS - u]:
                 nc.vector.tensor_tensor(out=xb(u, first, last), in0=bo_ps[:, first % D : D], in1=x_units[u][:, first:last], op=ALU.add)
 
-        def bias_tensor(u):
-            n = PAIR * D - gpsimd_cols(u)
-            bank = psum1.tile([P, D], F32, name="xb_ps")
-            nc.tensor.matmul(bank[:, 0:n], lhsT=ident_bf[:], rhs=x_units[u][:, gpsimd_cols(u) :], start=True, stop=False)
+        def bias_tensor(u, bank_name="xb_ps"):
+            n = D
+            bank = psum1.tile([P, D], F32, name=bank_name)
+            nc.tensor.matmul(bank[:, 0:n], lhsT=ident_bf[:], rhs=x_units[u][:, D:], start=True, stop=False)
             nc.tensor.matmul(bank[:, 0:n], lhsT=ones[:], rhs=rows[:, 0, D - n : D], start=False, stop=True)
             made["xb", u] = bank[:, 0:n]
 
         def bias_scalar(u):
-            nc.scalar.copy(out=xb(u, gpsimd_cols(u), PAIR * D), in_=made["xb", u])
+            nc.scalar.copy(out=xb(u, D, PAIR * D), in_=made["xb", u])
 
         def mx(out, q, tile, w_codes, w_scales):
             codes, scales = q
@@ -312,7 +319,7 @@ def tile_transformerblock_pb_t_kernel(tc, x, ao, wo_bytes, wo_scale, bo, g2, w1,
             copy(out=dst.rearrange("p (c i) t -> p c t i", i=4), in_=src.rearrange("p t (c i) -> p c t i", i=4))
 
         def quantise_weight(codes, scales, packed):
-            nc.vector.quantize_mx(out=codes[:].bitcast(FP8X4), scales=scales[:], in_=packed[:].rearrange("p n t -> p (n t)"))
+            nc.vector.quantize_mx(out=codes.bitcast(FP8X4), scales=scales, in_=packed.rearrange("p n t -> p (n t)"))
 
         for t in range(PACK - 1):
             nc.vector.tensor_scalar(
@@ -323,10 +330,11 @@ def tile_transformerblock_pb_t_kernel(tc, x, ao, wo_bytes, wo_scale, bo, g2, w1,
         nc.tensor.matmul(bo_ps[:], lhsT=ones[:], rhs=rows[:, 0, :], start=True, stop=True)
         nc.tensor.matmul(g2_ps[:], lhsT=ones[:], rhs=rows[:, 1, :], start=True, stop=True)
         turn_a(1, "nT_ps")
+        interleave(nc.vector.tensor_copy, w_packed[:, 0:F, :], w_raw[:, 0])
         interleave(nc.vector.tensor_copy, wo_packed[:, 0:WO_VECTOR, :], wo_wide[:, :, 0:WO_VECTOR])
         interleave(nc.scalar.copy, wo_packed[:, WO_VECTOR:D, :], wo_wide[:, :, WO_VECTOR:D])
-        interleave(nc.vector.tensor_copy, w_packed[:, 0:F, :], w_raw[:, 0])
-        quantise_weight(wo_codes, wo_scales, wo_packed)
+        quantise_weight(w_codes[:, 0:F], w_scales[:, 0:F], w_packed[:, 0:F, :])
+        quantise_weight(wo_codes[:], wo_scales[:], wo_packed[:])
         interleave(nc.vector.tensor_copy, w_packed[:, F : 2 * F, :], w_raw[:, 1])
         copy_a(0)
         nc.scalar.copy(out=bo_all[:, 0:D], in_=bo_ps[:])
@@ -334,7 +342,7 @@ def tile_transformerblock_pb_t_kernel(tc, x, ao, wo_bytes, wo_scale, bo, g2, w1,
         copy_a(1)
         nc.scalar.copy(out=g2_all[:], in_=g2_ps[:])
         quantise(0)
-        quantise_weight(w_codes, w_scales, w_packed)
+        quantise_weight(w_codes[:, F : 2 * F], w_scales[:, F : 2 * F], w_packed[:, F : 2 * F, :])
         nc.vector.tensor_tensor(out=xb(0, 0, D), in0=bo_ps[:], in1=x_units[0][:, 0:D], op=ALU.add)
         nc.gpsimd.tensor_tensor(out=xb(0, D, PAIR * D), in0=x_units[0][:, D:], in1=bo_all[:, 0:D], op=ALU.add)
 
@@ -353,6 +361,8 @@ def tile_transformerblock_pb_t_kernel(tc, x, ao, wo_bytes, wo_scale, bo, g2, w1,
                 sum_scalar(p - 1)
                 store_x1(p - 1)
             each(squares, p - 1)
+            if p == 1:
+                bias_scalar(2)
             if VECTOR_HELPS <= p + 1 < SCALAR_HALF:
                 bias_scalar(p + 1)
             elif turned(p):
@@ -363,6 +373,8 @@ def tile_transformerblock_pb_t_kernel(tc, x, ao, wo_bytes, wo_scale, bo, g2, w1,
             each(copy_n, p - 3)
             each(turn_a, p + 2)
             each(copy_a, p + 2)
+            if p == 0:
+                bias_tensor(2, "up_ps")
             each(gate_up, p + 1 - LAG)
             if VECTOR_HELPS <= p + 2 < SCALAR_HALF:
                 bias_tensor(p + 2)
@@ -395,7 +407,6 @@ def tile_transformerblock_pb_t_kernel(tc, x, ao, wo_bytes, wo_scale, bo, g2, w1,
         quantise(LAST - 3 + LAG)
         inverse_root(LAST)
         warm_tensor("xb_ps")
-        warm_tensor("xb_ps")
         gate(LAST - 3, psum2, "y_ps")
         up(LAST - 3, psum2, "y_ps")
         turn_n(LAST - 2)
@@ -403,22 +414,23 @@ def tile_transformerblock_pb_t_kernel(tc, x, ao, wo_bytes, wo_scale, bo, g2, w1,
         silu(LAST - 3)
         norm(LAST - 1)
         turn_n(LAST - 1, "aT_ps")
-        warm_tensor("gate_ps")
-        warm_tensor("gate_ps")
         copy_n(LAST - 2)
         norm(LAST)
         product(LAST - 4)
         quantise(LAST - 2 + LAG)
         copy_n(LAST - 1)
-        turn_n(LAST, "xb_ps")
+        turn_n_tile(LAST, 0, "xb_ps")
+        warm_tensor("gate_ps")
+        turn_n_tile(LAST, 1, "xb_ps")
+        warm_tensor("gate_ps")
         gate(LAST - 2)
-        up(LAST - 2)
         copy_n(LAST)
         silu(LAST - 2)
-        product(LAST - 3)
         quantise(LAST - 1 + LAG)
         gate(LAST - 1, psum1, "nT_ps")
+        up(LAST - 2)
         up(LAST - 1, psum1, "aT_ps")
+        product(LAST - 3)
         quantise(LAST + LAG)
         gate(LAST, psum2, "y_ps")
         up(LAST, psum1, "xb_ps")

@@ -24,6 +24,7 @@ UNITS = B * ROWS // PAIR
 LAST = UNITS - 1
 WORDS = D // 2
 PAD = 16
+HOME = PAD + PAIR * D + PAD
 LAG = 5
 
 VECTOR_HELPS = 3
@@ -53,11 +54,11 @@ def tile_transformerblock_pb_t_kernel(tc, x, ao, wo_bytes, wo_scale, bo, g2, w1,
         ident = const.tile([P, P], F32)
         make_identity(nc, ident[:])
         ident_bf = const.tile([P, P], BF16)
-        nc.vector.tensor_copy(out=ident_bf[:], in_=ident[:])
         neg_half = const.tile([P, PAIR], F32)
         nc.gpsimd.memset(neg_half[:], -0.5)
         warm = const.tile([P, 2], F32)
         nc.scalar.activation(out=warm[:], in_=ones[:, 0:2], func=ACT.Silu)
+        nc.scalar.copy(out=ident_bf[:], in_=ident[:])
 
         wo_sc = const.tile([P, PACK], F32)
         wo_raw = [const.tile([P, 2, D], U8, name="wo_raw%d" % half, align_bytes=64) for half in range(2)]
@@ -103,13 +104,13 @@ def tile_transformerblock_pb_t_kernel(tc, x, ao, wo_bytes, wo_scale, bo, g2, w1,
             load_a(PAIR * u + 1)
             load_x(u)
 
-        homes = [keep.tile([P, PAD + PAIR * D + PAD], F32, name="home%d" % u, align_bytes=64) for u in range(UNITS)]
+        homes = keep.tile([P, UNITS * HOME], F32, align_bytes=64)
         biased = [keep.tile([P, PAIR * D], F32, name="biased%d" % i, align_bytes=64) for i in range(3)]
-        for u in range(UNITS):
-            nc.vector.memset(homes[u][:, PAD - 1 : PAD + PAIR * D + 1 : PAIR * D + 1], (D * EPS) ** 0.5)
+        eps_cols = homes[:].rearrange("p (u c) -> p u c", c=HOME)[:, :, PAD - 1 : PAD + PAIR * D + 1 : PAIR * D + 1]
+        nc.vector.memset(eps_cols, (D * EPS) ** 0.5)
 
         def home(u, first, last):
-            return homes[u][:, PAD + first : PAD + last]
+            return homes[:, u * HOME + PAD + first : u * HOME + PAD + last]
 
         def xb(u, first, last):
             return biased[u % 3 if u < SCALAR_HALF else 1 + u % 2][:, first:last]

@@ -25,13 +25,11 @@ LAST = UNITS - 1
 WORDS = D // 2
 PAD = 16
 HOME = PAD + PAIR * D + PAD
-LAG = 5
-
-VECTOR_HELPS = 3
-SCALAR_HALF = 6
-GPSIMD_FIRST, GPSIMD_NEXT, GPSIMD_STEADY = 128, 512, 768
-EVERY = 4
+LAG = 4
+STEADY = 5
+GPSIMD_RAMP, GPSIMD_STEADY = 512, 768
 REST = GPSIMD_STEADY - D
+EVERY = 2
 WO_VECTOR = 320
 
 
@@ -41,8 +39,9 @@ def tile_transformerblock_pb_t_kernel(tc, x, ao, wo_bytes, wo_scale, bo, g2, w1,
         const = ctx.enter_context(tc.tile_pool(name="const", bufs=1))
         keep = ctx.enter_context(tc.tile_pool(name="keep", bufs=1))
         results = ctx.enter_context(tc.tile_pool(name="results", bufs=10))
-        stages = ctx.enter_context(tc.tile_pool(name="stages", bufs=3))
-        work = ctx.enter_context(tc.tile_pool(name="work", bufs=3))
+        stages = ctx.enter_context(tc.tile_pool(name="stages", bufs=4))
+        work = ctx.enter_context(tc.tile_pool(name="work", bufs=4))
+        single = ctx.enter_context(tc.tile_pool(name="single", bufs=1))
         psum2 = ctx.enter_context(tc.psum_pool(name="psum2", bufs=2))
         psum1 = ctx.enter_context(tc.psum_pool(name="psum1", bufs=1))
         ctx.enter_context(tc.manual_schedule())
@@ -62,7 +61,7 @@ def tile_transformerblock_pb_t_kernel(tc, x, ao, wo_bytes, wo_scale, bo, g2, w1,
 
         wo_sc = const.tile([P, PACK], F32)
         wo_raw = [const.tile([P, 2, D], U8, name="wo_raw%d" % half, align_bytes=64) for half in range(2)]
-        w_raw = const.tile([P, 2, PACK, F], BF16, align_bytes=64)
+        w_raw = [const.tile([P, PACK, F], BF16, name="w_raw%d" % i, align_bytes=64) for i in range(2)]
         a_tiles = {}
         x_units = {}
 
@@ -70,10 +69,11 @@ def tile_transformerblock_pb_t_kernel(tc, x, ao, wo_bytes, wo_scale, bo, g2, w1,
             b, i = divmod(PAIR * u, ROWS)
             return t[b].rearrange("(p i) d -> p i d", i=ROWS)[:, i : i + PAIR, :]
 
-        def load_a(tile):
-            a_tiles[tile] = keep.tile([P, H, DK], BF16, name="a%d" % tile, align_bytes=64)
-            src = ao[tile // ROWS].rearrange("h (p i) d -> p i h d", i=ROWS)[:, tile % ROWS, :, :]
-            nc.sync.dma_start(out=a_tiles[tile][:], in_=src)
+        def load_a(u):
+            for tile in range(PAIR * u, PAIR * u + PAIR):
+                a_tiles[tile] = keep.tile([P, H, DK], BF16, name="a%d" % tile, align_bytes=64)
+                src = ao[tile // ROWS].rearrange("h (p i) d -> p i h d", i=ROWS)[:, tile % ROWS, :, :]
+                nc.sync.dma_start(out=a_tiles[tile][:], in_=src)
 
         def load_x(u):
             xt = keep.tile([P, PAIR, D], BF16, name="x%d" % u, align_bytes=64)
@@ -81,7 +81,7 @@ def tile_transformerblock_pb_t_kernel(tc, x, ao, wo_bytes, wo_scale, bo, g2, w1,
             x_units[u] = xt[:].rearrange("p a d -> p (a d)")
 
         def load_w(i, w):
-            nc.sync.dma_start(out=w_raw[:, i], in_=w.rearrange("(p t) f -> p t f", t=PACK))
+            nc.sync.dma_start(out=w_raw[i][:], in_=w.rearrange("(p t) f -> p t f", t=PACK))
 
         def load_row(i, v):
             nc.sync.dma_start(out=rows[0:1, i, :], in_=v.rearrange("(o n) -> o n", o=1))
@@ -89,74 +89,65 @@ def tile_transformerblock_pb_t_kernel(tc, x, ao, wo_bytes, wo_scale, bo, g2, w1,
         nc.sync.dma_start(out=wo_sc[:], in_=wo_scale.rearrange("(p t) o -> p (t o)", t=PACK))
         for half in range(2):
             nc.sync.dma_start(out=wo_raw[half][:], in_=wo_bytes.rearrange("(p t) n -> p t n", t=PACK)[:, 2 * half : 2 * half + 2, :])
-        load_w(0, w1)
-        load_a(0)
         load_row(0, bo)
-        load_a(1)
         load_row(1, g2)
-        load_w(1, w3)
-        load_a(2)
-        load_a(3)
+        load_a(0)
         load_x(0)
+        load_a(1)
         load_x(1)
-        for u in range(2, UNITS):
-            load_a(PAIR * u)
-            load_a(PAIR * u + 1)
+        load_a(2)
+        load_x(2)
+        load_w(0, w1)
+        load_a(3)
+        load_x(3)
+        load_w(1, w3)
+        for u in range(4, UNITS):
+            load_a(u)
             load_x(u)
 
         homes = keep.tile([P, UNITS * HOME], F32, align_bytes=64)
-        biased = [keep.tile([P, PAIR * D], F32, name="biased%d" % i, align_bytes=64) for i in range(3)]
         eps_cols = homes[:].rearrange("p (u c) -> p u c", c=HOME)[:, :, PAD - 1 : PAD + PAIR * D + 1 : PAIR * D + 1]
         nc.vector.memset(eps_cols, (D * EPS) ** 0.5)
+        made = {}
 
         def home(u, first, last):
             return homes[:, u * HOME + PAD + first : u * HOME + PAD + last]
 
-        def xb(u, first, last):
-            return biased[u % 3 if u < SCALAR_HALF else 1 + u % 2][:, first:last]
-
         def stage(call, first, last):
-            if call < SCALAR_HALF:
-                return xb(call, first, last)
             if ("stage", call) not in made:
                 made["stage", call] = stages.tile([P, PAIR * D], F32, name="stage", align_bytes=64)
             return made["stage", call][:, first:last]
 
+        def biased(u, first, last):
+            return (stage if u > 1 else home)(u, first, last)
+
         def a_count(u):
             return PAIR if u < UNITS else 0
 
-        made = {}
-
-        def turn(rows_bf16, bank_name):
-            bank = psum1.tile([P, PAIR, 2, P], F32, name=bank_name)
-            for a, row in enumerate(rows_bf16):
-                words = row.bitcast(F32)
-                for e in range(2):
-                    nc.tensor.transpose(bank[:, a, e, :], words[:, e : WORDS : 2], ident[:])
-            return bank
-
-        def copy_turned(bank, u, first):
-            dst = stage(u, first, first + PAIR * WORDS).rearrange("p (a r e) -> p a r e", a=PAIR, e=2)
-            nc.scalar.copy(out=dst, in_=bank[:].rearrange("p a e r -> p a r e"))
+        def turn_row(bank, a, row):
+            words = row.bitcast(F32)
+            for e in range(2):
+                nc.tensor.transpose(bank[:, a, e, :], words[:, e:WORDS:2], ident[:])
 
         def turn_a(u, bank_name="aT_ps"):
-            made["aT", u] = turn([a_tiles[PAIR * u + a][:].rearrange("p h d -> p (h d)") for a in range(PAIR)], bank_name)
+            made["aT", u] = psum1.tile([P, PAIR, 2, P], F32, name=bank_name)
+            for a in range(PAIR):
+                turn_row(made["aT", u], a, a_tiles[PAIR * u + a][:].rearrange("p h d -> p (h d)"))
 
-        def copy_a(u):
-            copy_turned(made["aT", u], u, 0)
-
-        def turn_n(u, bank_name="nT_ps"):
-            made["nT", u] = turn([made["n", u, a][:] for a in range(PAIR)], bank_name)
-
-        def turn_n_tile(u, a, bank_name):
+        def turn_n(u, a, bank_name="nT_ps"):
             if a == 0:
                 made["nT", u] = psum1.tile([P, PAIR, 2, P], F32, name=bank_name)
-            words = made["n", u, a][:].bitcast(F32)
-            for e in range(2):
-                nc.tensor.transpose(made["nT", u][:, a, e, :], words[:, e:WORDS:2], ident[:])
+            turn_row(made["nT", u], a, made["n", u, a][:])
 
-        def copy_n(u):
-            copy_turned(made["nT", u], u + LAG, a_count(u + LAG) * WORDS)
+        def copy_turned(copy, bank, call, first):
+            dst = stage(call, first, first + PAIR * WORDS).rearrange("p (a r e) -> p a r e", a=PAIR, e=2)
+            copy(out=dst, in_=bank[:].rearrange("p a e r -> p a r e"))
+
+        def copy_a(u):
+            copy_turned(nc.scalar.copy, made["aT", u], u, 0)
+
+        def copy_n(u, copy=nc.scalar.copy):
+            copy_turned(copy, made["nT", u], u + LAG, a_count(u + LAG) * WORDS)
 
         def quantise(u):
             tiles = a_count(u) + (PAIR if u >= LAG else 0)
@@ -167,30 +158,47 @@ def tile_transformerblock_pb_t_kernel(tc, x, ao, wo_bytes, wo_scale, bo, g2, w1,
             )
             made["q", u] = (codes, scales)
 
-        def warm_tensor(bank_name, pool=psum1):
-            bank = pool.tile([P, PACK, P], F32, name=bank_name)
-            nc.tensor.matmul(bank[:], lhsT=ident_bf[:], rhs=ident_bf[:].unsqueeze(1).to_broadcast([P, PACK, P]), start=True, stop=True)
+        def finish_tile(u, a):
+            first = a * WORDS
+            nc.scalar.copy(
+                out=stage(u + LAG, first, first + WORDS).rearrange("p (r e) -> p r e", e=2), in_=made["nT", u, a][:].rearrange("p e r -> p r e")
+            )
+
+        def turn_tile(u, a, bank_name):
+            made["nT", u, a] = psum1.tile([P, 2, P], F32, name=bank_name)
+            words = made["n", u, a][:].bitcast(F32)
+            for e in range(2):
+                nc.tensor.transpose(made["nT", u, a][:, e, :], words[:, e:WORDS:2], ident[:])
+
+        def quantise_tile(u, a):
+            codes = work.tile([P, 2 * PAIR * P], U32, name="codes", align_bytes=64)
+            scales = work.tile([P, 2 * PAIR * P], U8, name="scales", align_bytes=64)
+            nc.vector.quantize_mx(out=codes[:, 0:P].bitcast(FP8X4), scales=scales[:, 0:P], in_=stage(u + LAG, a * WORDS, (a + 1) * WORDS).bitcast(BF16))
+            made["q", u, a] = (codes, scales)
+
+        def half_tile(u, a, i, pool, name):
+            bank = pool.tile([P, F], F32, name=name)
+            made["uv", u, a, i] = bank
+            mx(bank[:], made["q", u, a], 0, w_codes[:, i * F : (i + 1) * F], w_scales[:, i * F : (i + 1) * F])
+
+        def silu_tile(u, a):
+            made["silu", u, a] = work.tile([P, PAIR, F], F32, name="silu")
+            nc.scalar.activation(out=made["silu", u, a][:, 0, :], in_=made["uv", u, a, 0][:], func=ACT.Silu)
+
+        def product_tile(u, a):
+            h = results.tile([P, PAIR, F], F32, name="h")
+            nc.vector.tensor_tensor(out=h[:, 0, :], in0=made["uv", u, a, 1][:], in1=made["silu", u, a][:, 0, :], op=ALU.mult)
+            nc.sync.dma_start(out=unit_rows(out_1, u)[:, a, :], in_=h[:, 0, :])
 
         def gpsimd_cols(u):
-            return GPSIMD_FIRST if u < VECTOR_HELPS else GPSIMD_NEXT if u < SCALAR_HALF else GPSIMD_STEADY
+            return GPSIMD_RAMP if u < STEADY else GPSIMD_STEADY
 
         def bias_gpsimd(u):
             n = gpsimd_cols(u)
-            nc.gpsimd.tensor_tensor(out=xb(u, 0, n), in0=x_units[u][:, 0:n], in1=bo_all[:, 0:n], op=ALU.add)
+            nc.gpsimd.tensor_tensor(out=biased(u, 0, n), in0=x_units[u][:, 0:n], in1=bo_all[:, 0:n], op=ALU.add)
 
-        def bias_vector(u):
-            for first, last in ((gpsimd_cols(u), D), (D, PAIR * D))[: VECTOR_HELPS - u]:
-                nc.vector.tensor_tensor(out=xb(u, first, last), in0=bo_ps[:, first % D : D], in1=x_units[u][:, first:last], op=ALU.add)
-
-        def bias_tensor(u, bank_name="xb_ps"):
-            n = D
-            bank = psum1.tile([P, D], F32, name=bank_name)
-            nc.tensor.matmul(bank[:, 0:n], lhsT=ident_bf[:], rhs=x_units[u][:, D:], start=True, stop=False)
-            nc.tensor.matmul(bank[:, 0:n], lhsT=ones[:], rhs=rows[:, 0, D - n : D], start=False, stop=True)
-            made["xb", u] = bank[:, 0:n]
-
-        def bias_scalar(u):
-            nc.scalar.copy(out=xb(u, D, PAIR * D), in_=made["xb", u])
+        def bias_vector(u, first, last):
+            nc.vector.tensor_tensor(out=biased(u, first, last), in0=bo_ps[:, first % D : D], in1=x_units[u][:, first:last], op=ALU.add)
 
         def mx(out, q, tile, w_codes, w_scales):
             codes, scales = q
@@ -200,13 +208,10 @@ def tile_transformerblock_pb_t_kernel(tc, x, ao, wo_bytes, wo_scale, bo, g2, w1,
             )
 
         def turned(u):
-            return u >= SCALAR_HALF and (LAST - u) % EVERY != 0
+            return STEADY <= u < LAST and (u % EVERY == 1 or u == LAST - 1)
 
-        def next_plain(u):
-            return u + (LAST - u) % EVERY
-
-        def project(u):
-            for a in range(PAIR):
+        def project(u, tiles=range(PAIR)):
+            for a in tiles:
                 bank = psum2.tile([P, D], F32, name="y_ps")
                 made["y", u, a] = bank
                 if a == 1 and turned(u):
@@ -221,52 +226,47 @@ def tile_transformerblock_pb_t_kernel(tc, x, ao, wo_bytes, wo_scale, bo, g2, w1,
             made["yT", u] = work.tile([P, D - REST], F32, name="yT")
             nc.scalar.copy(out=made["yT", u][:], in_=made["y", u, 1][:, REST:D])
 
-        def sum_tensor(u):
-            if not turned(u):
-                made["sums", u] = psum1.tile([P, 2, D - REST], F32, name="xb_ps")
-            out = made["sums", next_plain(u)][:, 0, :] if turned(u) else made["sums", u][:, 1, :]
-            nc.tensor.matmul(out, lhsT=ident_bf[:], rhs=x_units[u][:, D + REST :], start=True, stop=False)
-            nc.tensor.matmul(out, lhsT=ones[:], rhs=rows[:, 0, REST:D], start=False, stop=not turned(u))
-            if turned(u):
-                chunks = (D - REST) // P
-                for c in range(chunks):
-                    cols = slice(c * P, (c + 1) * P)
-                    nc.tensor.matmul(out[:, cols], lhsT=made["yT", u][:, cols], rhs=ident[:], is_transpose=True, start=False, stop=c == chunks - 1)
+        def sum_plain(u, bank_name="sum_ps"):
+            first = gpsimd_cols(u) - D
+            bank = psum1.tile([P, D], F32, name=bank_name)
+            made["sum", u] = bank[:, first:D]
+            nc.tensor.matmul(made["sum", u], lhsT=ident_bf[:], rhs=x_units[u][:, D + first :], start=True, stop=False)
+            nc.tensor.matmul(made["sum", u], lhsT=ones[:], rhs=rows[:, 0, first:D], start=False, stop=not turned(u))
+
+        def sum_turn(u):
+            chunks = (D - REST) // P
+            for c in range(chunks):
+                cols = slice(c * P, (c + 1) * P)
+                nc.tensor.matmul(made["sum", u][:, cols], lhsT=made["yT", u][:, cols], rhs=ident[:], is_transpose=True, start=False, stop=c == chunks - 1)
 
         def sum_scalar(u):
-            if turned(u):
-                nc.scalar.copy(out=home(u, D + REST, PAIR * D), in_=made["sums", next_plain(u)][:, 0, :])
-            else:
-                nc.scalar.copy(out=xb(u, D + REST, PAIR * D), in_=made["sums", u][:, 1, :])
+            nc.scalar.copy(out=(home if turned(u) else biased)(u, gpsimd_cols(u), PAIR * D), in_=made["sum", u])
 
         def store_x1(u):
             nc.sync.dma_start(out=unit_rows(out_0, u), in_=home(u, 0, PAIR * D).rearrange("p (a d) -> p a d", d=D))
 
-        def residual(u):
-            for a in range(PAIR):
+        def residual(u, tiles=range(PAIR)):
+            for a in tiles:
                 n = REST if a == 1 and turned(u) else D
-                nc.vector.tensor_tensor(out=home(u, a * D, a * D + n), in0=made["y", u, a][:, 0:n], in1=xb(u, a * D, a * D + n), op=ALU.add)
-            if not turned(u):
-                store_x1(u)
+                nc.vector.tensor_tensor(out=home(u, a * D, a * D + n), in0=made["y", u, a][:, 0:n], in1=biased(u, a * D, a * D + n), op=ALU.add)
 
-        def squares(u):
-            made["ms", u] = work.tile([P, PAIR], F32, name="ms")
-            for a in range(PAIR):
-                sq = work.tile([P, D + 1], BF16, name="sq")
-                row = home(u, a * (D + 1) - 1, a * (D + 1) + D)
-                nc.scalar.activation(out=sq[:], in_=row, func=ACT.Square, scale=D**-0.5, accum_out=made["ms", u][:, a : a + 1])
+        def squares(u, a):
+            if ("ms", u) not in made:
+                made["ms", u] = work.tile([P, PAIR], F32, name="ms")
+            sq = work.tile([P, D + 1], BF16, name="sq")
+            row = home(u, a * (D + 1) - 1, a * (D + 1) + D)
+            nc.scalar.activation(out=sq[:], in_=row, func=ACT.Square, scale=D**-0.5, accum_out=made["ms", u][:, a : a + 1])
 
         def inverse_root(u):
-            made["rstd", u] = work.tile([P, PAIR], F32, name="rstd")
-            nc.gpsimd.tensor_tensor(out=made["rstd", u][:], in0=made["ms", u][:], in1=neg_half[:], op=ALU.pow)
+            rstd = (single if u >= STEADY - 3 else work).tile([P, PAIR], F32, name="rstd")
+            made["rstd", u] = rstd[:]
+            nc.gpsimd.tensor_tensor(out=made["rstd", u], in0=made["ms", u][:], in1=neg_half[:], op=ALU.pow)
 
-        def gain_gpsimd(u, a, out):
-            made["gained"] = out
-            nc.gpsimd.tensor_tensor(out=out, in0=home(u, a * D, (a + 1) * D), in1=g2_all[:], op=ALU.mult)
-
-        def norm_scalar(u, a):
-            made["n", u, a] = work.tile([P, D], BF16, name="n%d" % a, align_bytes=64)
-            nc.scalar.activation(out=made["n", u, a][:], in_=made["gained"], func=ACT.Copy, scale=made["rstd", u][:, a : a + 1])
+        def inverse_root_tile(u, a):
+            if a == 0:
+                rstd = work.tile([P, PAIR], F32, name="rstd")
+                made["rstd", u] = rstd[:]
+            nc.gpsimd.tensor_tensor(out=made["rstd", u][:, a : a + 1], in0=made["ms", u][:, a : a + 1], in1=neg_half[:, 0:1], op=ALU.pow)
 
         def norm(u, tiles=range(PAIR)):
             for a in tiles:
@@ -314,129 +314,185 @@ def tile_transformerblock_pb_t_kernel(tc, x, ao, wo_bytes, wo_scale, bo, g2, w1,
         bo_all = const.tile([P, GPSIMD_STEADY], BF16)
         bo_ps = psum1.tile([P, D], F32, name="gate_ps")
         g2_ps = psum1.tile([P, D], F32, name="g2_ps")
-        g2_all = const.tile([P, D], BF16)
 
         def interleave(copy, dst, src):
             copy(out=dst.rearrange("p (c i) t -> p c t i", i=4), in_=src.rearrange("p t (c i) -> p c t i", i=4))
 
+        def interleave_w(i, bank_name):
+            bank = psum1.tile([P, F, PACK], BF16, name=bank_name)
+            made["w", i] = bank
+            for c in range(0, F, P):
+                nc.tensor.matmul(bank[:, c : c + P, :], lhsT=ident_bf[:], rhs=w_raw[i][:, :, c : c + P].rearrange("p t c -> p c t"), start=True, stop=True)
+
+        def copy_w(i):
+            nc.scalar.copy(out=w_packed[:, i * F : (i + 1) * F, :], in_=made["w", i][:])
+
         def quantise_weight(codes, scales, packed):
             nc.vector.quantize_mx(out=codes.bitcast(FP8X4), scales=scales, in_=packed.rearrange("p n t -> p (n t)"))
+
+        def quantise_w(i):
+            cols = slice(i * F, (i + 1) * F)
+            quantise_weight(w_codes[:, cols], w_scales[:, cols], w_packed[:, cols, :])
+
+        def each(work_on, u, *more):
+            if 0 <= u < UNITS:
+                work_on(u, *more)
 
         for t in range(PACK - 1):
             nc.vector.tensor_scalar(
                 out=wo_wide[:, t, :], in0=wo_raw[t // 2][:, t % 2, :].bitcast(FP8), scalar1=wo_sc[:, t : t + 1], scalar2=None, op0=ALU.mult
             )
         nc.scalar.activation(out=wo_wide[:, PACK - 1, :], in_=wo_raw[1][:, 1, :].bitcast(FP8), func=ACT.Copy, scale=wo_sc[:, PACK - 1 : PACK])
-        turn_a(0)
         nc.tensor.matmul(bo_ps[:], lhsT=ones[:], rhs=rows[:, 0, :], start=True, stop=True)
         nc.tensor.matmul(g2_ps[:], lhsT=ones[:], rhs=rows[:, 1, :], start=True, stop=True)
+        turn_a(0)
+        sum_plain(0)
         turn_a(1, "nT_ps")
-        interleave(nc.vector.tensor_copy, w_packed[:, 0:F, :], w_raw[:, 0])
         interleave(nc.vector.tensor_copy, wo_packed[:, 0:WO_VECTOR, :], wo_wide[:, :, 0:WO_VECTOR])
         interleave(nc.scalar.copy, wo_packed[:, WO_VECTOR:D, :], wo_wide[:, :, WO_VECTOR:D])
-        quantise_weight(w_codes[:, 0:F], w_scales[:, 0:F], w_packed[:, 0:F, :])
-        quantise_weight(wo_codes[:], wo_scales[:], wo_packed[:])
-        interleave(nc.vector.tensor_copy, w_packed[:, F : 2 * F, :], w_raw[:, 1])
+        bias_vector(0, 0, D)
         copy_a(0)
         nc.scalar.copy(out=bo_all[:, 0:D], in_=bo_ps[:])
-        nc.scalar.copy(out=bo_all[:, D:], in_=bo_all[:, 0 : GPSIMD_STEADY - D])
-        copy_a(1)
-        nc.scalar.copy(out=g2_all[:], in_=g2_ps[:])
+        sum_scalar(0)
+        quantise_weight(wo_codes[:], wo_scales[:], wo_packed[:])
         quantise(0)
-        quantise_weight(w_codes[:, F : 2 * F], w_scales[:, F : 2 * F], w_packed[:, F : 2 * F, :])
-        nc.vector.tensor_tensor(out=xb(0, 0, D), in0=bo_ps[:], in1=x_units[0][:, 0:D], op=ALU.add)
-        nc.gpsimd.tensor_tensor(out=xb(0, D, PAIR * D), in0=x_units[0][:, D:], in1=bo_all[:, 0:D], op=ALU.add)
+        bias_gpsimd(1)
+        bias_vector(1, D, PAIR * D)
+        copy_a(1)
+        nc.scalar.copy(out=bo_all[:, D:], in_=bo_all[:, 0 : GPSIMD_STEADY - D])
+        project(0)
+        residual(0, (0,))
+        quantise(1)
+        residual(0, (1,))
+        store_x1(0)
+        turn_a(2)
+        project(1)
+        interleave_w(0, "up_ps")
+        squares(0, 0)
+        copy_a(2)
+        squares(0, 1)
+        residual(1, (0,))
+        quantise(2)
+        residual(1, (1,))
+        bias_vector(2, D, PAIR * D)
+        store_x1(1)
+        inverse_root(0)
+        bias_gpsimd(2)
+        turn_a(3)
+        project(2, (1, 0))
+        sum_plain(3)
+        squares(1, 0)
+        squares(1, 1)
+        copy_a(3)
+        copy_w(0)
+        sum_scalar(3)
+        inverse_root(1)
+        norm(0)
+        turn_n(0, 0)
+        turn_n(0, 1)
+        turn_a(4)
+        interleave_w(1, "up_ps")
+        residual(2, (1, 0))
+        store_x1(2)
+        quantise(3)
+        quantise_w(0)
+        bias_gpsimd(3)
+        project(3, (1, 0))
+        copy_n(0)
+        squares(2, 1)
+        squares(2, 0)
+        copy_a(4)
+        copy_w(1)
+        inverse_root(2)
+        norm(1)
+        turn_n(1, 0)
+        turn_n(1, 1)
+        turn_a(5)
+        sum_plain(4)
+        residual(3, (1, 0))
+        store_x1(3)
+        quantise(4)
+        quantise_w(1)
+        bias_gpsimd(4)
+        gate_up(0)
+        project(4)
+        squares(3, 1)
+        copy_a(5)
+        squares(3, 0)
+        copy_n(1)
+        silu(0)
+        turn_a(6)
+        norm(2)
+        turn_n(2, 0)
+        turn_n(2, 1)
 
-        def each(stage, u, first=0):
-            if first <= u < UNITS:
-                stage(u)
-
-        for p in range(LAST):
-            project(p)
-            if p == 0:
-                residual(0)
+        for p in range(STEADY - 1, LAST):
             quantise(p + 1)
+            inverse_root(p - 1)
             bias_gpsimd(p + 1)
-            each(product, p - LAG)
-            if turned(p - 1):
-                sum_scalar(p - 1)
-                store_x1(p - 1)
-            each(squares, p - 1)
-            if p == 1:
-                bias_scalar(2)
-            if VECTOR_HELPS <= p + 1 < SCALAR_HALF:
-                bias_scalar(p + 1)
-            elif turned(p):
-                copy_y(p)
-            elif p >= SCALAR_HALF:
-                sum_scalar(p)
-            each(inverse_root, p - 1)
-            each(copy_n, p - 3)
-            each(turn_a, p + 2)
+            product(p - 4)
+            (copy_y if turned(p) else sum_scalar)(p)
             each(copy_a, p + 2)
-            if p == 0:
-                bias_tensor(2, "up_ps")
-            each(gate_up, p + 1 - LAG)
-            if VECTOR_HELPS <= p + 2 < SCALAR_HALF:
-                bias_tensor(p + 2)
-            elif turned(p):
-                sum_tensor(p)
-            elif p + 1 >= SCALAR_HALF:
-                sum_tensor(next_plain(p + 1))
-            each(norm, p - 2)
-            each(turn_n, p - 2)
-            each(silu, p + 1 - LAG)
-            each(residual, p, first=1)
-            if p + 1 < VECTOR_HELPS:
-                bias_vector(p + 1)
+            copy_n(p - 2)
+            if p + 1 == LAST:
+                sum_plain(LAST, "aT_ps")
+                sum_scalar(LAST)
+            gate_up(p - 3)
+            silu(p - 3)
+            residual(p)
+            if turned(p):
+                sum_turn(p)
+                sum_scalar(p)
+            each(turn_a, p + 3)
+            project(p + 1)
+            if p + 1 < LAST:
+                sum_plain(p + 1)
+            squares(p, 0)
+            squares(p, 1)
+            store_x1(p)
+            norm(p - 1)
+            turn_n(p - 1, 0)
+            turn_n(p - 1, 1)
 
-        project(LAST)
-        quantise(LAST - 4 + LAG)
-        gain_gpsimd(LAST - 2, 1, stage(LAST - 4 + LAG, 0, D))
-        product(LAST - 5)
-        sum_scalar(LAST)
-        sum_scalar(LAST - 1)
-        store_x1(LAST - 1)
-        squares(LAST - 1)
-        residual(LAST)
-        inverse_root(LAST - 1)
-        copy_n(LAST - 3)
-        squares(LAST)
-        gate_up(LAST - 4)
-        norm(LAST - 2, (0,))
-        norm_scalar(LAST - 2, 1)
         quantise(LAST - 3 + LAG)
-        inverse_root(LAST)
-        warm_tensor("xb_ps")
-        gate(LAST - 3, psum2, "y_ps")
-        up(LAST - 3, psum2, "y_ps")
-        turn_n(LAST - 2)
-        silu(LAST - 4)
+        inverse_root(LAST - 1)
+        copy_n(LAST - 2)
+        gate(LAST - 3, psum1, "sum_ps")
+        up(LAST - 3, psum1, "aT_ps")
+        residual(LAST)
+        store_x1(LAST)
+        quantise(LAST - 2 + LAG)
+        for a in range(PAIR):
+            squares(LAST, a)
+            inverse_root_tile(LAST, a)
         silu(LAST - 3)
         norm(LAST - 1)
-        turn_n(LAST - 1, "aT_ps")
-        copy_n(LAST - 2)
-        norm(LAST)
-        product(LAST - 4)
-        quantise(LAST - 2 + LAG)
+        gate(LAST - 2, psum2, "y_ps")
+        turn_n(LAST - 1, 0)
+        turn_n(LAST - 1, 1)
+        up(LAST - 2, psum2, "y_ps")
         copy_n(LAST - 1)
-        turn_n_tile(LAST, 0, "xb_ps")
-        warm_tensor("gate_ps")
-        turn_n_tile(LAST, 1, "xb_ps")
-        warm_tensor("gate_ps")
-        gate(LAST - 2)
-        copy_n(LAST)
         silu(LAST - 2)
+        norm(LAST)
+        turn_tile(LAST, 0, "gate_ps")
+        turn_tile(LAST, 1, "sum_ps")
+        finish_tile(LAST, 0)
+        finish_tile(LAST, 1)
+        product(LAST - 4)
         quantise(LAST - 1 + LAG)
         gate(LAST - 1, psum1, "nT_ps")
-        up(LAST - 2)
-        up(LAST - 1, psum1, "aT_ps")
+        up(LAST - 1)
         product(LAST - 3)
-        quantise(LAST + LAG)
-        gate(LAST, psum2, "y_ps")
-        up(LAST, psum1, "xb_ps")
+        quantise_tile(LAST, 0)
+        quantise_tile(LAST, 1)
         silu(LAST - 1)
-        silu(LAST, 1)
-        product(LAST - 2)
-        product(LAST - 1)
-        product(LAST, 1)
+        half_tile(LAST, 0, 0, psum1, "gate_ps")
+        half_tile(LAST, 1, 0, psum1, "sum_ps")
+        half_tile(LAST, 0, 1, psum1, "aT_ps")
+        product(LAST - 2, 1)
+        half_tile(LAST, 1, 1, psum2, "y_ps")
+        silu_tile(LAST, 0)
+        silu_tile(LAST, 1)
+        product(LAST - 1, 1)
+        product_tile(LAST, 0)
+        product_tile(LAST, 1)

@@ -322,7 +322,8 @@ def tile_transformerblock_pb_t_kernel(tc, x, ao, wo_bytes, wo_scale, bo, g2, w1,
             bank = psum1.tile([P, F, PACK], BF16, name=bank_name)
             made["w", i] = bank
             for c in range(0, F, P):
-                nc.tensor.matmul(bank[:, c : c + P, :], lhsT=ident_bf[:], rhs=w_raw[i][:, :, c : c + P].rearrange("p t c -> p c t"), start=True, stop=True)
+                src = w_raw[i][:, :, c : c + P].rearrange("p t (c i) -> p c t i", i=8)
+                nc.tensor.matmul(bank[:, c : c + P, :].rearrange("p (c i) t -> p c t i", i=8), lhsT=ident_bf[:], rhs=src, start=True, stop=True)
 
         def copy_w(i):
             nc.scalar.copy(out=w_packed[:, i * F : (i + 1) * F, :], in_=made["w", i][:])
@@ -418,8 +419,8 @@ def tile_transformerblock_pb_t_kernel(tc, x, ao, wo_bytes, wo_scale, bo, g2, w1,
         project(4)
         squares(3, 1)
         copy_a(5)
-        squares(3, 0)
         copy_n(1)
+        squares(3, 0)
         silu(0)
         turn_a(6)
         norm(2)

@@ -25,11 +25,11 @@ LAST = UNITS - 1
 WORDS = D // 2
 PAD = 16
 HOME = PAD + PAIR * D + PAD
-LAG = 4
-STEADY = 5
-GPSIMD_RAMP, GPSIMD_STEADY = 512, 768
+LAG = 5
+STEADY = 6
+GPSIMD_RAMP, GPSIMD_NEXT, GPSIMD_STEADY = 512, 640, 768
 REST = GPSIMD_STEADY - D
-EVERY = 2
+EVERY = 4
 WO_VECTOR = 320
 
 
@@ -41,7 +41,6 @@ def tile_transformerblock_pb_t_kernel(tc, x, ao, wo_bytes, wo_scale, bo, g2, w1,
         results = ctx.enter_context(tc.tile_pool(name="results", bufs=10))
         stages = ctx.enter_context(tc.tile_pool(name="stages", bufs=4))
         work = ctx.enter_context(tc.tile_pool(name="work", bufs=4))
-        single = ctx.enter_context(tc.tile_pool(name="single", bufs=1))
         psum2 = ctx.enter_context(tc.psum_pool(name="psum2", bufs=2))
         psum1 = ctx.enter_context(tc.psum_pool(name="psum1", bufs=1))
         ctx.enter_context(tc.manual_schedule())
@@ -97,11 +96,13 @@ def tile_transformerblock_pb_t_kernel(tc, x, ao, wo_bytes, wo_scale, bo, g2, w1,
         load_x(1)
         load_a(2)
         load_x(2)
-        load_w(0, w1)
         load_a(3)
         load_x(3)
+        load_w(0, w1)
+        load_a(4)
+        load_x(4)
         load_w(1, w3)
-        for u in range(4, UNITS):
+        for u in range(5, UNITS):
             load_a(u)
             load_x(u)
 
@@ -119,7 +120,7 @@ def tile_transformerblock_pb_t_kernel(tc, x, ao, wo_bytes, wo_scale, bo, g2, w1,
             return made["stage", call][:, first:last]
 
         def biased(u, first, last):
-            return (stage if u > 1 else home)(u, first, last)
+            return (home if u <= 1 or (u == LAST and first >= D) else stage)(u, first, last)
 
         def a_count(u):
             return PAIR if u < UNITS else 0
@@ -191,7 +192,7 @@ def tile_transformerblock_pb_t_kernel(tc, x, ao, wo_bytes, wo_scale, bo, g2, w1,
             nc.sync.dma_start(out=unit_rows(out_1, u)[:, a, :], in_=h[:, 0, :])
 
         def gpsimd_cols(u):
-            return GPSIMD_RAMP if u < STEADY else GPSIMD_STEADY
+            return GPSIMD_STEADY if STEADY <= u < LAST else GPSIMD_NEXT if 3 <= u < STEADY else GPSIMD_RAMP
 
         def bias_gpsimd(u):
             n = gpsimd_cols(u)
@@ -208,11 +209,11 @@ def tile_transformerblock_pb_t_kernel(tc, x, ao, wo_bytes, wo_scale, bo, g2, w1,
             )
 
         def turned(u):
-            return STEADY <= u < LAST and (u % EVERY == 1 or u == LAST - 1)
+            return u >= STEADY and (LAST - u) % EVERY != 0
 
-        def project(u, tiles=range(PAIR)):
+        def project(u, tiles=range(PAIR), pool=psum2, name="y_ps"):
             for a in tiles:
-                bank = psum2.tile([P, D], F32, name="y_ps")
+                bank = pool.tile([P, D], F32, name=name)
                 made["y", u, a] = bank
                 if a == 1 and turned(u):
                     codes, scales = made["q", u]
@@ -258,15 +259,32 @@ def tile_transformerblock_pb_t_kernel(tc, x, ao, wo_bytes, wo_scale, bo, g2, w1,
             nc.scalar.activation(out=sq[:], in_=row, func=ACT.Square, scale=D**-0.5, accum_out=made["ms", u][:, a : a + 1])
 
         def inverse_root(u):
-            rstd = (single if u >= STEADY - 3 else work).tile([P, PAIR], F32, name="rstd")
-            made["rstd", u] = rstd[:]
+            if u < 2:
+                made["rstd", u] = x_units[2][:, D : D + 2 * PAIR].bitcast(F32)
+            elif u < LAST - 2:
+                made["rstd", u] = w_packed[:, 0 if u == 2 else F, :].bitcast(F32)
+            else:
+                rstd = work.tile([P, PAIR], F32, name="rstd")
+                made["rstd", u] = rstd[:]
             nc.gpsimd.tensor_tensor(out=made["rstd", u], in0=made["ms", u][:], in1=neg_half[:], op=ALU.pow)
 
         def inverse_root_tile(u, a):
-            if a == 0:
+            if ("rstd", u) not in made:
                 rstd = work.tile([P, PAIR], F32, name="rstd")
                 made["rstd", u] = rstd[:]
             nc.gpsimd.tensor_tensor(out=made["rstd", u][:, a : a + 1], in0=made["ms", u][:, a : a + 1], in1=neg_half[:, 0:1], op=ALU.pow)
+
+        def gain_gpsimd(u, a, out):
+            made["gained", u, a] = out
+            nc.gpsimd.tensor_tensor(out=out, in0=home(u, a * D, (a + 1) * D), in1=g2_all[:], op=ALU.mult)
+
+        def norm_scalar(u, a):
+            made["n", u, a] = work.tile([P, D], BF16, name="n%d" % a, align_bytes=64)
+            nc.scalar.activation(out=made["n", u, a][:], in_=made["gained", u, a], func=ACT.Copy, scale=made["rstd", u][:, a : a + 1])
+
+        def warm_tensor(bank_name, pool=psum1):
+            bank = pool.tile([P, PACK, P], F32, name=bank_name)
+            nc.tensor.matmul(bank[:], lhsT=ident_bf[:], rhs=ident_bf[:].unsqueeze(1).to_broadcast([P, PACK, P]), start=True, stop=True)
 
         def norm(u, tiles=range(PAIR)):
             for a in tiles:
@@ -314,6 +332,7 @@ def tile_transformerblock_pb_t_kernel(tc, x, ao, wo_bytes, wo_scale, bo, g2, w1,
         bo_all = const.tile([P, GPSIMD_STEADY], BF16)
         bo_ps = psum1.tile([P, D], F32, name="gate_ps")
         g2_ps = psum1.tile([P, D], F32, name="g2_ps")
+        g2_all = const.tile([P, D], BF16)
 
         def interleave(copy, dst, src):
             copy(out=dst.rearrange("p (c i) t -> p c t i", i=4), in_=src.rearrange("p t (c i) -> p c t i", i=4))
@@ -361,139 +380,203 @@ def tile_transformerblock_pb_t_kernel(tc, x, ao, wo_bytes, wo_scale, bo, g2, w1,
         bias_vector(1, D, PAIR * D)
         copy_a(1)
         nc.scalar.copy(out=bo_all[:, D:], in_=bo_all[:, 0 : GPSIMD_STEADY - D])
+        nc.scalar.copy(out=g2_all[:], in_=g2_ps[:])
         project(0)
+        turn_a(2)
+        copy_a(2)
         residual(0, (0,))
         quantise(1)
         residual(0, (1,))
         store_x1(0)
-        turn_a(2)
         project(1)
-        interleave_w(0, "up_ps")
-        squares(0, 0)
-        copy_a(2)
-        squares(0, 1)
-        residual(1, (0,))
+        turn_a(3, "nT_ps")
         quantise(2)
-        residual(1, (1,))
-        bias_vector(2, D, PAIR * D)
-        store_x1(1)
-        inverse_root(0)
         bias_gpsimd(2)
-        turn_a(3)
-        project(2, (1, 0))
+        squares(0, 0)
+        squares(0, 1)
+        copy_a(3)
+        residual(1)
+        store_x1(1)
+        bias_vector(2, D, PAIR * D)
+        project(2)
         sum_plain(3)
+        turn_a(4)
+        interleave_w(0, "up_ps")
+        quantise(3)
+        inverse_root(0)
+        bias_gpsimd(3)
         squares(1, 0)
         squares(1, 1)
-        copy_a(3)
-        copy_w(0)
         sum_scalar(3)
-        inverse_root(1)
+        copy_a(4)
+        residual(2)
+        store_x1(2)
+        project(3)
+        sum_plain(4)
+        turn_a(5)
+        squares(2, 0)
+        copy_w(0)
+        squares(2, 1)
         norm(0)
         turn_n(0, 0)
         turn_n(0, 1)
-        turn_a(4)
-        interleave_w(1, "up_ps")
-        residual(2, (1, 0))
-        store_x1(2)
-        quantise(3)
-        quantise_w(0)
-        bias_gpsimd(3)
-        project(3, (1, 0))
+        interleave_w(1, "gate_ps")
+        quantise(4)
+        inverse_root(1)
+        bias_gpsimd(4)
+        sum_scalar(4)
+        copy_a(5)
         copy_n(0)
-        squares(2, 1)
-        squares(2, 0)
-        copy_a(4)
-        copy_w(1)
-        inverse_root(2)
+        residual(3)
+        store_x1(3)
+        project(4)
+        sum_plain(5)
+        turn_a(6)
         norm(1)
         turn_n(1, 0)
         turn_n(1, 1)
-        turn_a(5)
-        sum_plain(4)
-        residual(3, (1, 0))
-        store_x1(3)
-        quantise(4)
-        quantise_w(1)
-        bias_gpsimd(4)
-        gate_up(0)
-        project(4)
-        squares(3, 1)
-        copy_a(5)
-        copy_n(1)
+        quantise_w(0)
+        quantise(5)
+        inverse_root(2)
+        bias_gpsimd(5)
         squares(3, 0)
+        copy_w(1)
+        squares(3, 1)
+        copy_a(6)
+        copy_n(1)
+        gate(0)
         silu(0)
-        turn_a(6)
+        residual(4)
+        project(5)
+        turn_a(7)
+        sum_scalar(5)
+        squares(4, 0)
+        squares(4, 1)
+        store_x1(4)
         norm(2)
+        quantise_w(1)
+        up(0)
         turn_n(2, 0)
         turn_n(2, 1)
+        quantise(6)
+        inverse_root(3)
+        bias_gpsimd(6)
+        residual(5, (0,))
+        product(0)
+        copy_a(7)
+        copy_n(2)
+        gate_up(1)
+        silu(1)
+        residual(5, (1,))
+        turn_a(8)
+        project(6)
+        sum_plain(6)
+        squares(5, 0)
+        squares(5, 1)
+        store_x1(5)
+        norm(3)
+        turn_n(3, 0)
+        turn_n(3, 1)
 
-        for p in range(STEADY - 1, LAST):
+        for p in range(STEADY, LAST - 1):
             quantise(p + 1)
-            inverse_root(p - 1)
+            inverse_root(p - 2)
             bias_gpsimd(p + 1)
-            product(p - 4)
+            product(p - 5)
             (copy_y if turned(p) else sum_scalar)(p)
-            each(copy_a, p + 2)
-            copy_n(p - 2)
-            if p + 1 == LAST:
-                sum_plain(LAST, "aT_ps")
-                sum_scalar(LAST)
-            gate_up(p - 3)
-            silu(p - 3)
+            copy_a(p + 2)
+            copy_n(p - 3)
+            gate_up(p - 4)
+            silu(p - 4)
             residual(p)
             if turned(p):
                 sum_turn(p)
                 sum_scalar(p)
             each(turn_a, p + 3)
             project(p + 1)
-            if p + 1 < LAST:
-                sum_plain(p + 1)
+            sum_plain(p + 1)
+            if p + 2 == LAST:
+                sum_plain(LAST, "aT_ps")
             squares(p, 0)
             squares(p, 1)
             store_x1(p)
-            norm(p - 1)
-            turn_n(p - 1, 0)
-            turn_n(p - 1, 1)
+            norm(p - 2)
+            turn_n(p - 2, 0)
+            turn_n(p - 2, 1)
 
-        quantise(LAST - 3 + LAG)
-        inverse_root(LAST - 1)
-        copy_n(LAST - 2)
-        gate(LAST - 3, psum1, "sum_ps")
-        up(LAST - 3, psum1, "aT_ps")
-        residual(LAST)
-        store_x1(LAST)
-        quantise(LAST - 2 + LAG)
-        for a in range(PAIR):
-            squares(LAST, a)
-            inverse_root_tile(LAST, a)
-        silu(LAST - 3)
-        norm(LAST - 1)
-        gate(LAST - 2, psum2, "y_ps")
-        turn_n(LAST - 1, 0)
-        turn_n(LAST - 1, 1)
-        up(LAST - 2, psum2, "y_ps")
-        copy_n(LAST - 1)
-        silu(LAST - 2)
-        norm(LAST)
-        turn_tile(LAST, 0, "gate_ps")
-        turn_tile(LAST, 1, "sum_ps")
-        finish_tile(LAST, 0)
-        finish_tile(LAST, 1)
-        product(LAST - 4)
-        quantise(LAST - 1 + LAG)
-        gate(LAST - 1, psum1, "nT_ps")
-        up(LAST - 1)
-        product(LAST - 3)
-        quantise_tile(LAST, 0)
-        quantise_tile(LAST, 1)
-        silu(LAST - 1)
-        half_tile(LAST, 0, 0, psum1, "gate_ps")
-        half_tile(LAST, 1, 0, psum1, "sum_ps")
-        half_tile(LAST, 0, 1, psum1, "aT_ps")
-        product(LAST - 2, 1)
-        half_tile(LAST, 1, 1, psum2, "y_ps")
-        silu_tile(LAST, 0)
-        silu_tile(LAST, 1)
-        product(LAST - 1, 1)
-        product_tile(LAST, 0)
-        product_tile(LAST, 1)
+        quantise(15)
+        inverse_root(12)
+        bias_gpsimd(15)
+        product(9)
+        copy_y(14)
+        sum_scalar(15)
+        copy_n(11)
+        gate_up(10)
+        silu(10)
+        sum_turn(14)
+        residual(14)
+        project(15, (1,), psum1, "aT_ps")
+        project(15, (0,))
+        sum_scalar(14)
+        squares(14, 0)
+        squares(14, 1)
+        store_x1(14)
+        norm(12)
+        turn_n(12, 0)
+        turn_n(12, 1)
+        quantise(16)
+        inverse_root(13)
+        gain_gpsimd(13, 1, stage(16, 0, D))
+        inverse_root(14)
+        residual(15, (1, 0))
+        store_x1(15)
+        gate(11)
+        up(11, psum1, "aT_ps")
+        product(10)
+        copy_n(12)
+        squares(15, 1)
+        squares(15, 0)
+        warm_tensor("up_ps")
+        norm(13, (0,))
+        quantise(17)
+        inverse_root(15)
+        norm_scalar(13, 1)
+        silu(11)
+        gate(12, psum2, "y_ps")
+        turn_n(13, 0)
+        turn_n(13, 1)
+        up(12, psum2, "y_ps")
+        norm(14)
+        copy_n(13)
+        turn_n(14, 0, "sum_ps")
+        turn_n(14, 1, "sum_ps")
+        warm_tensor("up_ps")
+        silu(12)
+        norm(15, (1, 0))
+        quantise(18)
+        copy_n(14)
+        turn_tile(15, 1, "nT_ps")
+        turn_tile(15, 0, "gate_ps")
+        product(11)
+        gate(13, psum1, "up_ps")
+        up(13, psum1, "aT_ps")
+        finish_tile(15, 1)
+        finish_tile(15, 0)
+        silu(13)
+        quantise(19)
+        product(12)
+        gate(14, psum1, "sum_ps")
+        up(14, psum2, "y_ps")
+        quantise_tile(15, 1)
+        quantise_tile(15, 0)
+        product(13)
+        silu(14)
+        half_tile(15, 1, 0, psum1, "nT_ps")
+        half_tile(15, 0, 0, psum1, "gate_ps")
+        half_tile(15, 1, 1, psum2, "y_ps")
+        half_tile(15, 0, 1, psum1, "up_ps")
+        product(14)
+        silu_tile(15, 1)
+        silu_tile(15, 0)
+        product_tile(15, 1)
+        product_tile(15, 0)

@@ -125,6 +125,11 @@ def tile_transformerblock_pb_t_kernel(tc, x, ao, wo_bytes, wo_scale, bo, g2, w1,
         def a_count(u):
             return PAIR if u < UNITS else 0
 
+        def n_place(u):
+            if u + LAG < UNITS:
+                return u + LAG, PAIR
+            return (UNITS, PAIR) if u + LAG == UNITS + 1 else (u + LAG, 0)
+
         def turn_row(bank, a, row):
             words = row.bitcast(F32)
             for e in range(2):
@@ -148,10 +153,11 @@ def tile_transformerblock_pb_t_kernel(tc, x, ao, wo_bytes, wo_scale, bo, g2, w1,
             copy_turned(nc.scalar.copy, made["aT", u], u, 0)
 
         def copy_n(u, copy=nc.scalar.copy):
-            copy_turned(copy, made["nT", u], u + LAG, a_count(u + LAG) * WORDS)
+            call, tile = n_place(u)
+            copy_turned(copy, made["nT", u], call, tile * WORDS)
 
         def quantise(u):
-            tiles = a_count(u) + (PAIR if u >= LAG else 0)
+            tiles = 2 * PAIR if LAG <= u <= UNITS else PAIR
             codes = work.tile([P, 2 * PAIR * P], U32, name="codes", align_bytes=64)
             scales = work.tile([P, 2 * PAIR * P], U8, name="scales", align_bytes=64)
             nc.vector.quantize_mx(
@@ -297,8 +303,9 @@ def tile_transformerblock_pb_t_kernel(tc, x, ao, wo_bytes, wo_scale, bo, g2, w1,
             bank = pool.tile([P, PAIR, F], F32, name=name)
             made["uv", u, i] = bank
             cols = slice(i * F, (i + 1) * F)
+            call, tile = n_place(u)
             for a in range(PAIR):
-                mx(bank[:, a, :], made["q", u + LAG], a_count(u + LAG) + a, w_codes[:, cols], w_scales[:, cols])
+                mx(bank[:, a, :], made["q", call], tile + a, w_codes[:, cols], w_scales[:, cols])
 
         def gate(u, pool=psum1, name="gate_ps"):
             half(u, 0, pool, name)
@@ -524,37 +531,36 @@ def tile_transformerblock_pb_t_kernel(tc, x, ao, wo_bytes, wo_scale, bo, g2, w1,
         norm(12)
         turn_n(12, 0)
         turn_n(12, 1)
-        quantise(16)
         inverse_root(13)
-        gain_gpsimd(13, 1, stage(16, 0, D))
+        gain_gpsimd(13, 1, stage(15, D, PAIR * D))
         inverse_root(14)
         residual(15, (1, 0))
         store_x1(15)
-        gate(11)
-        up(11, psum1, "aT_ps")
+        warm_tensor("aT_ps")
         product(10)
+        warm_tensor("up_ps")
         copy_n(12)
         squares(15, 1)
         squares(15, 0)
-        warm_tensor("up_ps")
-        norm(13, (0,))
-        quantise(17)
-        inverse_root(15)
         norm_scalar(13, 1)
-        silu(11)
-        gate(12, psum2, "y_ps")
+        norm(13, (0,))
+        quantise(16)
+        inverse_root(15)
         turn_n(13, 0)
+        gate(11)
+        gate(12, psum2, "y_ps")
         turn_n(13, 1)
-        up(12, psum2, "y_ps")
+        silu(11)
         norm(14)
         copy_n(13)
         turn_n(14, 0, "sum_ps")
         turn_n(14, 1, "sum_ps")
-        warm_tensor("up_ps")
+        up(11, psum1, "aT_ps")
+        up(12, psum2, "y_ps")
+        copy_n(14)
         silu(12)
         norm(15, (1, 0))
         quantise(18)
-        copy_n(14)
         turn_tile(15, 1, "nT_ps")
         turn_tile(15, 0, "gate_ps")
         product(11)
@@ -569,13 +575,13 @@ def tile_transformerblock_pb_t_kernel(tc, x, ao, wo_bytes, wo_scale, bo, g2, w1,
         up(14, psum2, "y_ps")
         quantise_tile(15, 1)
         quantise_tile(15, 0)
-        product(13)
+        product(13, 1)
         silu(14)
         half_tile(15, 1, 0, psum1, "nT_ps")
         half_tile(15, 0, 0, psum1, "gate_ps")
         half_tile(15, 1, 1, psum2, "y_ps")
         half_tile(15, 0, 1, psum1, "up_ps")
-        product(14)
+        product(14, 1)
         silu_tile(15, 1)
         silu_tile(15, 0)
         product_tile(15, 1)

@@ -252,6 +252,12 @@ def tile_transformerblock_pb_t_kernel(tc, x, ao, wo_bytes, wo_scale, bo, g2, w1,
         def store_x1(u):
             nc.sync.dma_start(out=unit_rows(out_0, u), in_=home(u, 0, PAIR * D).rearrange("p (a d) -> p a d", d=D))
 
+        def store_x1_pair(u):
+            b, i = divmod(PAIR * u, ROWS)
+            dst = out_0[b].rearrange("(p i) d -> p i d", i=ROWS)[:, i : i + 2 * PAIR, :].rearrange("p (u a) d -> p u (a d)", a=PAIR)
+            src = homes[:, u * HOME : (u + 2) * HOME].rearrange("p (u c) -> p u c", c=HOME)[:, :, PAD : PAD + PAIR * D]
+            nc.sync.dma_start(out=dst, in_=src)
+
         def residual(u, tiles=range(PAIR)):
             for a in tiles:
                 n = REST if a == 1 and turned(u) else D
@@ -289,8 +295,8 @@ def tile_transformerblock_pb_t_kernel(tc, x, ao, wo_bytes, wo_scale, bo, g2, w1,
             nc.scalar.activation(out=made["n", u, a][:], in_=made["gained", u, a], func=ACT.Copy, scale=made["rstd", u][:, a : a + 1])
 
         def warm_tensor(bank_name, pool=psum1):
-            bank = pool.tile([P, PACK, P], F32, name=bank_name)
-            nc.tensor.matmul(bank[:], lhsT=ident_bf[:], rhs=ident_bf[:].unsqueeze(1).to_broadcast([P, PACK, P]), start=True, stop=True)
+            bank = pool.tile([P, P], F32, name=bank_name)
+            nc.tensor.matmul(bank[:], lhsT=ident[:], rhs=ident[:], start=True, stop=True)
 
         def norm(u, tiles=range(PAIR)):
             for a in tiles:
@@ -394,7 +400,6 @@ def tile_transformerblock_pb_t_kernel(tc, x, ao, wo_bytes, wo_scale, bo, g2, w1,
         residual(0, (0,))
         quantise(1)
         residual(0, (1,))
-        store_x1(0)
         project(1)
         turn_a(3, "nT_ps")
         quantise(2)
@@ -403,7 +408,7 @@ def tile_transformerblock_pb_t_kernel(tc, x, ao, wo_bytes, wo_scale, bo, g2, w1,
         squares(0, 1)
         copy_a(3)
         residual(1)
-        store_x1(1)
+        store_x1_pair(0)
         bias_vector(2, D, PAIR * D)
         project(2)
         sum_plain(3)
@@ -417,7 +422,6 @@ def tile_transformerblock_pb_t_kernel(tc, x, ao, wo_bytes, wo_scale, bo, g2, w1,
         sum_scalar(3)
         copy_a(4)
         residual(2)
-        store_x1(2)
         project(3)
         sum_plain(4)
         turn_a(5)
@@ -435,7 +439,7 @@ def tile_transformerblock_pb_t_kernel(tc, x, ao, wo_bytes, wo_scale, bo, g2, w1,
         copy_a(5)
         copy_n(0)
         residual(3)
-        store_x1(3)
+        store_x1_pair(2)
         project(4)
         sum_plain(5)
         turn_a(6)
@@ -536,7 +540,8 @@ def tile_transformerblock_pb_t_kernel(tc, x, ao, wo_bytes, wo_scale, bo, g2, w1,
         inverse_root(14)
         residual(15, (1, 0))
         store_x1(15)
-        warm_tensor("aT_ps")
+        warm_tensor("y_ps", psum2)
+        warm_tensor("y_ps", psum2)
         product(10)
         warm_tensor("up_ps")
         copy_n(12)

from contextlib import ExitStack

import concourse.mybir as mybir
from concourse.masks import make_identity

F32 = mybir.dt.float32
BF16 = mybir.dt.bfloat16
U32 = mybir.dt.uint32
U8 = mybir.dt.uint8
FP8 = mybir.dt.float8_e4m3fn
FP8X4 = mybir.dt.float8_e4m3fn_x4
ACT = mybir.ActivationFunctionType
ALU = mybir.AluOpType

B, S, D, H, DK, F = 2, 2048, 512, 4, 128, 256
EPS = 1e-6
FLOPS = 2 * B * S * (H * DK * D + D * 2 * F)

P = 128
PACK = 4
ROWS = S // P
PAIR = 2
UNITS = B * ROWS // PAIR
LAST = UNITS - 1
WORDS = D // 2
PAD = 16
HOME = PAD + PAIR * D + PAD
LAG = 5
STEADY = 6
GPSIMD_RAMP, GPSIMD_NEXT, GPSIMD_STEADY = 512, 640, 768
REST = GPSIMD_STEADY - D
EVERY = 4
WO_VECTOR = 320


def tile_transformerblock_pb_t_kernel(tc, x, ao, wo_bytes, wo_scale, bo, g2, w1, w3, out_0, out_1):
    nc = tc.nc
    with ExitStack() as ctx:
        const = ctx.enter_context(tc.tile_pool(name="const", bufs=1))
        keep = ctx.enter_context(tc.tile_pool(name="keep", bufs=1))
        results = ctx.enter_context(tc.tile_pool(name="results", bufs=10))
        stages = ctx.enter_context(tc.tile_pool(name="stages", bufs=4))
        work = ctx.enter_context(tc.tile_pool(name="work", bufs=4))
        psum2 = ctx.enter_context(tc.psum_pool(name="psum2", bufs=2))
        psum1 = ctx.enter_context(tc.psum_pool(name="psum1", bufs=1))
        ctx.enter_context(tc.manual_schedule())

        ones = const.tile([P, P], BF16)
        nc.vector.memset(ones[:], 1.0)
        rows = const.tile([P, 2, D], BF16)
        nc.vector.memset(rows[:], 0.0)
        ident = const.tile([P, P], F32)
        make_identity(nc, ident[:])
        ident_bf = const.tile([P, P], BF16)
        neg_half = const.tile([P, PAIR], F32)
        nc.gpsimd.memset(neg_half[:], -0.5)
        warm = const.tile([P, 2], F32)
        nc.scalar.activation(out=warm[:], in_=ones[:, 0:2], func=ACT.Silu)
        nc.scalar.copy(out=ident_bf[:], in_=ident[:])

        wo_sc = const.tile([P, PACK], F32)
        wo_raw = [const.tile([P, 2, D], U8, name="wo_raw%d" % half, align_bytes=64) for half in range(2)]
        w_raw = [const.tile([P, PACK, F], BF16, name="w_raw%d" % i, align_bytes=64) for i in range(2)]
        a_tiles = {}
        x_units = {}

        def unit_rows(t, u):
            b, i = divmod(PAIR * u, ROWS)
            return t[b].rearrange("(p i) d -> p i d", i=ROWS)[:, i : i + PAIR, :]

        def load_a(u):
            for tile in range(PAIR * u, PAIR * u + PAIR):
                a_tiles[tile] = keep.tile([P, H, DK], BF16, name="a%d" % tile, align_bytes=64)
                src = ao[tile // ROWS].rearrange("h (p i) d -> p i h d", i=ROWS)[:, tile % ROWS, :, :]
                nc.sync.dma_start(out=a_tiles[tile][:], in_=src)

        def load_x(u):
            xt = keep.tile([P, PAIR, D], BF16, name="x%d" % u, align_bytes=64)
            nc.sync.dma_start(out=xt[:], in_=unit_rows(x, u))
            x_units[u] = xt[:].rearrange("p a d -> p (a d)")

        def load_w(i, w):
            nc.sync.dma_start(out=w_raw[i][:], in_=w.rearrange("(p t) f -> p t f", t=PACK))

        def load_row(i, v):
            nc.sync.dma_start(out=rows[0:1, i, :], in_=v.rearrange("(o n) -> o n", o=1))

        nc.sync.dma_start(out=wo_sc[:], in_=wo_scale.rearrange("(p t) o -> p (t o)", t=PACK))
        for half in range(2):
            nc.sync.dma_start(out=wo_raw[half][:], in_=wo_bytes.rearrange("(p t) n -> p t n", t=PACK)[:, 2 * half : 2 * half + 2, :])
        load_row(0, bo)
        load_row(1, g2)
        load_a(0)
        load_x(0)
        load_a(1)
        load_x(1)
        load_a(2)
        load_x(2)
        load_a(3)
        load_x(3)
        load_w(0, w1)
        load_a(4)
        load_x(4)
        load_w(1, w3)
        for u in range(5, UNITS):
            load_a(u)
            load_x(u)

        homes = keep.tile([P, UNITS * HOME], F32, align_bytes=64)
        eps_cols = homes[:].rearrange("p (u c) -> p u c", c=HOME)[:, :, PAD - 1 : PAD + PAIR * D + 1 : PAIR * D + 1]
        nc.vector.memset(eps_cols, (D * EPS) ** 0.5)
        made = {}

        def home(u, first, last):
            return homes[:, u * HOME + PAD + first : u * HOME + PAD + last]

        def stage(call, first, last):
            if ("stage", call) not in made:
                made["stage", call] = stages.tile([P, PAIR * D], F32, name="stage", align_bytes=64)
            return made["stage", call][:, first:last]

        def biased(u, first, last):
            return (home if u <= 1 or (u == LAST and first >= D) else stage)(u, first, last)

        def a_count(u):
            return PAIR if u < UNITS else 0

        def n_place(u):
            if u + LAG < UNITS:
                return u + LAG, PAIR
            return (UNITS, PAIR) if u + LAG == UNITS + 1 else (u + LAG, 0)

        def turn_row(bank, a, row):
            words = row.bitcast(F32)
            for e in range(2):
                nc.tensor.transpose(bank[:, a, e, :], words[:, e:WORDS:2], ident[:])

        def turn_a(u, bank_name="aT_ps"):
            made["aT", u] = psum1.tile([P, PAIR, 2, P], F32, name=bank_name)
            for a in range(PAIR):
                turn_row(made["aT", u], a, a_tiles[PAIR * u + a][:].rearrange("p h d -> p (h d)"))

        def turn_n(u, a, bank_name="nT_ps"):
            if a == 0:
                made["nT", u] = psum1.tile([P, PAIR, 2, P], F32, name=bank_name)
            turn_row(made["nT", u], a, made["n", u, a][:])

        def copy_turned(copy, bank, call, first):
            dst = stage(call, first, first + PAIR * WORDS).rearrange("p (a r e) -> p a r e", a=PAIR, e=2)
            copy(out=dst, in_=bank[:].rearrange("p a e r -> p a r e"))

        def copy_a(u):
            copy_turned(nc.scalar.copy, made["aT", u], u, 0)

        def copy_n(u, copy=nc.scalar.copy):
            call, tile = n_place(u)
            copy_turned(copy, made["nT", u], call, tile * WORDS)

        def quantise(u):
            tiles = 2 * PAIR if LAG <= u <= UNITS else PAIR
            codes = work.tile([P, 2 * PAIR * P], U32, name="codes", align_bytes=64)
            scales = work.tile([P, 2 * PAIR * P], U8, name="scales", align_bytes=64)
            nc.vector.quantize_mx(
                out=codes[:, 0 : tiles * P].bitcast(FP8X4), scales=scales[:, 0 : tiles * P], in_=stage(u, 0, tiles * WORDS).bitcast(BF16)
            )
            made["q", u] = (codes, scales)

        def finish_tile(u, a):
            first = a * WORDS
            nc.scalar.copy(
                out=stage(u + LAG, first, first + WORDS).rearrange("p (r e) -> p r e", e=2), in_=made["nT", u, a][:].rearrange("p e r -> p r e")
            )

        def turn_tile(u, a, bank_name):
            made["nT", u, a] = psum1.tile([P, 2, P], F32, name=bank_name)
            words = made["n", u, a][:].bitcast(F32)
            for e in range(2):
                nc.tensor.transpose(made["nT", u, a][:, e, :], words[:, e:WORDS:2], ident[:])

        def quantise_tile(u, a):
            codes = work.tile([P, 2 * PAIR * P], U32, name="codes", align_bytes=64)
            scales = work.tile([P, 2 * PAIR * P], U8, name="scales", align_bytes=64)
            nc.vector.quantize_mx(out=codes[:, 0:P].bitcast(FP8X4), scales=scales[:, 0:P], in_=stage(u + LAG, a * WORDS, (a + 1) * WORDS).bitcast(BF16))
            made["q", u, a] = (codes, scales)

        def half_tile(u, a, i, pool, name):
            bank = pool.tile([P, F], F32, name=name)
            made["uv", u, a, i] = bank
            mx(bank[:], made["q", u, a], 0, w_codes[:, i * F : (i + 1) * F], w_scales[:, i * F : (i + 1) * F])

        def silu_tile(u, a):
            made["silu", u, a] = work.tile([P, PAIR, F], F32, name="silu")
            nc.scalar.activation(out=made["silu", u, a][:, 0, :], in_=made["uv", u, a, 0][:], func=ACT.Silu)

        def product_tile(u, a):
            h = results.tile([P, PAIR, F], F32, name="h")
            nc.vector.tensor_tensor(out=h[:, 0, :], in0=made["uv", u, a, 1][:], in1=made["silu", u, a][:, 0, :], op=ALU.mult)
            nc.sync.dma_start(out=unit_rows(out_1, u)[:, a, :], in_=h[:, 0, :])

        def gpsimd_cols(u):
            return GPSIMD_STEADY if STEADY <= u < LAST else GPSIMD_NEXT if 3 <= u < STEADY else GPSIMD_RAMP

        def bias_gpsimd(u):
            n = gpsimd_cols(u)
            nc.gpsimd.tensor_tensor(out=biased(u, 0, n), in0=x_units[u][:, 0:n], in1=bo_all[:, 0:n], op=ALU.add)

        def bias_vector(u, first, last):
            nc.vector.tensor_tensor(out=biased(u, first, last), in0=bo_ps[:, first % D : D], in1=x_units[u][:, first:last], op=ALU.add)

        def mx(out, q, tile, w_codes, w_scales):
            codes, scales = q
            cols = slice(tile * P, (tile + 1) * P)
            nc.tensor.matmul_mx(
                out=out, lhsT=codes[:, cols].bitcast(FP8X4), lhsT_scale=scales[:, cols], rhs=w_codes.bitcast(FP8X4), rhs_scale=w_scales, start=True, stop=True
            )

        def turned(u):
            return u >= STEADY and (LAST - u) % EVERY != 0

        def project(u, tiles=range(PAIR), pool=psum2, name="y_ps"):
            for a in tiles:
                bank = pool.tile([P, D], F32, name=name)
                made["y", u, a] = bank
                if a == 1 and turned(u):
                    codes, scales = made["q", u]
                    mx(bank[:, 0:REST], made["q", u], a, wo_codes[:, 0:REST], wo_scales[:, 0:REST])
                    for c in range(REST // P, D // P):
                        mx(bank[:, c * P : (c + 1) * P], (wo_codes, wo_scales), c, codes[:, P : 2 * P], scales[:, P : 2 * P])
                else:
                    mx(bank[:], made["q", u], a, wo_codes[:], wo_scales[:])

        def copy_y(u):
            made["yT", u] = work.tile([P, D - REST], F32, name="yT")
            nc.scalar.copy(out=made["yT", u][:], in_=made["y", u, 1][:, REST:D])

        def sum_plain(u, bank_name="sum_ps"):
            first = gpsimd_cols(u) - D
            bank = psum1.tile([P, D], F32, name=bank_name)
            made["sum", u] = bank[:, first:D]
            nc.tensor.matmul(made["sum", u], lhsT=ident_bf[:], rhs=x_units[u][:, D + first :], start=True, stop=False)
            nc.tensor.matmul(made["sum", u], lhsT=ones[:], rhs=rows[:, 0, first:D], start=False, stop=not turned(u))

        def sum_turn(u):
            chunks = (D - REST) // P
            for c in range(chunks):
                cols = slice(c * P, (c + 1) * P)
                nc.tensor.matmul(made["sum", u][:, cols], lhsT=made["yT", u][:, cols], rhs=ident[:], is_transpose=True, start=False, stop=c == chunks - 1)

        def sum_scalar(u):
            nc.scalar.copy(out=(home if turned(u) else biased)(u, gpsimd_cols(u), PAIR * D), in_=made["sum", u])

        def store_x1(u):
            nc.sync.dma_start(out=unit_rows(out_0, u), in_=home(u, 0, PAIR * D).rearrange("p (a d) -> p a d", d=D))

        def store_x1_pair(u):
            b, i = divmod(PAIR * u, ROWS)
            dst = out_0[b].rearrange("(p i) d -> p i d", i=ROWS)[:, i : i + 2 * PAIR, :].rearrange("p (u a) d -> p u (a d)", a=PAIR)
            src = homes[:, u * HOME : (u + 2) * HOME].rearrange("p (u c) -> p u c", c=HOME)[:, :, PAD : PAD + PAIR * D]
            nc.sync.dma_start(out=dst, in_=src)

        def residual(u, tiles=range(PAIR)):
            for a in tiles:
                n = REST if a == 1 and turned(u) else D
                nc.vector.tensor_tensor(out=home(u, a * D, a * D + n), in0=made["y", u, a][:, 0:n], in1=biased(u, a * D, a * D + n), op=ALU.add)

        def squares(u, a):
            if ("ms", u) not in made:
                made["ms", u] = work.tile([P, PAIR], F32, name="ms")
            sq = work.tile([P, D + 1], BF16, name="sq")
            row = home(u, a * (D + 1) - 1, a * (D + 1) + D)
            nc.scalar.activation(out=sq[:], in_=row, func=ACT.Square, scale=D**-0.5, accum_out=made["ms", u][:, a : a + 1])

        def inverse_root(u):
            if u < 2:
                made["rstd", u] = x_units[2][:, D : D + 2 * PAIR].bitcast(F32)
            elif u < LAST - 2:
                made["rstd", u] = w_packed[:, 0 if u == 2 else F, :].bitcast(F32)
            else:
                rstd = work.tile([P, PAIR], F32, name="rstd")
                made["rstd", u] = rstd[:]
            nc.gpsimd.tensor_tensor(out=made["rstd", u], in0=made["ms", u][:], in1=neg_half[:], op=ALU.pow)

        def inverse_root_tile(u, a):
            if ("rstd", u) not in made:
                rstd = work.tile([P, PAIR], F32, name="rstd")
                made["rstd", u] = rstd[:]
            nc.gpsimd.tensor_tensor(out=made["rstd", u][:, a : a + 1], in0=made["ms", u][:, a : a + 1], in1=neg_half[:, 0:1], op=ALU.pow)

        def gain_gpsimd(u, a, out):
            made["gained", u, a] = out
            nc.gpsimd.tensor_tensor(out=out, in0=home(u, a * D, (a + 1) * D), in1=g2_all[:], op=ALU.mult)

        def norm_scalar(u, a):
            made["n", u, a] = work.tile([P, D], BF16, name="n%d" % a, align_bytes=64)
            nc.scalar.activation(out=made["n", u, a][:], in_=made["gained", u, a], func=ACT.Copy, scale=made["rstd", u][:, a : a + 1])

        def warm_tensor(bank_name, pool=psum1):
            bank = pool.tile([P, P], F32, name=bank_name)
            nc.tensor.matmul(bank[:], lhsT=ident[:], rhs=ident[:], start=True, stop=True)

        def norm(u, tiles=range(PAIR)):
            for a in tiles:
                made["n", u, a] = work.tile([P, D], BF16, name="n%d" % a, align_bytes=64)
                nc.vector.scalar_tensor_tensor(
                    out=made["n", u, a][:], in0=home(u, a * D, (a + 1) * D), scalar=made["rstd", u][:, a : a + 1], in1=g2_ps[:], op0=ALU.mult, op1=ALU.mult
                )

        def half(u, i, pool, name):
            bank = pool.tile([P, PAIR, F], F32, name=name)
            made["uv", u, i] = bank
            cols = slice(i * F, (i + 1) * F)
            call, tile = n_place(u)
            for a in range(PAIR):
                mx(bank[:, a, :], made["q", call], tile + a, w_codes[:, cols], w_scales[:, cols])

        def gate(u, pool=psum1, name="gate_ps"):
            half(u, 0, pool, name)

        def up(u, pool=psum1, name="up_ps"):
            half(u, 1, pool, name)

        def gate_up(u):
            gate(u)
            up(u)

        def silu(u, step=PAIR):
            made["silu", u] = work.tile([P, PAIR, F], F32, name="silu")
            for a in range(0, PAIR, step):
                nc.scalar.activation(out=made["silu", u][:, a : a + step], in_=made["uv", u, 0][:, a : a + step], func=ACT.Silu)

        def product(u, step=PAIR):
            h = results.tile([P, PAIR, F], F32, name="h")
            for a in range(0, PAIR, step):
                part = slice(a, a + step)
                nc.vector.tensor_tensor(out=h[:, part], in0=made["uv", u, 1][:, part], in1=made["silu", u][:, part], op=ALU.mult)
                nc.sync.dma_start(out=unit_rows(out_1, u)[:, part, :], in_=h[:, part, :])

        wo_wide = const.tile([P, PACK, D], BF16, align_bytes=64)
        wo_packed = const.tile([P, D, PACK], BF16, align_bytes=64)
        wo_codes = const.tile([P, D], U32, align_bytes=64)
        wo_scales = const.tile([P, D], U8, align_bytes=64)
        w_packed = const.tile([P, 2 * F, PACK], BF16, align_bytes=64)
        w_codes = const.tile([P, 2 * F], U32, align_bytes=64)
        w_scales = const.tile([P, 2 * F], U8, align_bytes=64)
        bo_all = const.tile([P, GPSIMD_STEADY], BF16)
        bo_ps = psum1.tile([P, D], F32, name="gate_ps")
        g2_ps = psum1.tile([P, D], F32, name="g2_ps")
        g2_all = const.tile([P, D], BF16)

        def interleave(copy, dst, src):
            copy(out=dst.rearrange("p (c i) t -> p c t i", i=4), in_=src.rearrange("p t (c i) -> p c t i", i=4))

        def interleave_w(i, bank_name):
            bank = psum1.tile([P, F, PACK], BF16, name=bank_name)
            made["w", i] = bank
            for c in range(0, F, P):
                src = w_raw[i][:, :, c : c + P].rearrange("p t (c i) -> p c t i", i=8)
                nc.tensor.matmul(bank[:, c : c + P, :].rearrange("p (c i) t -> p c t i", i=8), lhsT=ident_bf[:], rhs=src, start=True, stop=True)

        def copy_w(i):
            nc.scalar.copy(out=w_packed[:, i * F : (i + 1) * F, :], in_=made["w", i][:])

        def quantise_weight(codes, scales, packed):
            nc.vector.quantize_mx(out=codes.bitcast(FP8X4), scales=scales, in_=packed.rearrange("p n t -> p (n t)"))

        def quantise_w(i):
            cols = slice(i * F, (i + 1) * F)
            quantise_weight(w_codes[:, cols], w_scales[:, cols], w_packed[:, cols, :])

        def each(work_on, u, *more):
            if 0 <= u < UNITS:
                work_on(u, *more)

        for t in range(PACK - 1):
            nc.vector.tensor_scalar(
                out=wo_wide[:, t, :], in0=wo_raw[t // 2][:, t % 2, :].bitcast(FP8), scalar1=wo_sc[:, t : t + 1], scalar2=None, op0=ALU.mult
            )
        nc.scalar.activation(out=wo_wide[:, PACK - 1, :], in_=wo_raw[1][:, 1, :].bitcast(FP8), func=ACT.Copy, scale=wo_sc[:, PACK - 1 : PACK])
        nc.tensor.matmul(bo_ps[:], lhsT=ones[:], rhs=rows[:, 0, :], start=True, stop=True)
        nc.tensor.matmul(g2_ps[:], lhsT=ones[:], rhs=rows[:, 1, :], start=True, stop=True)
        turn_a(0)
        sum_plain(0)
        turn_a(1, "nT_ps")
        interleave(nc.vector.tensor_copy, wo_packed[:, 0:WO_VECTOR, :], wo_wide[:, :, 0:WO_VECTOR])
        interleave(nc.scalar.copy, wo_packed[:, WO_VECTOR:D, :], wo_wide[:, :, WO_VECTOR:D])
        bias_vector(0, 0, D)
        copy_a(0)
        nc.scalar.copy(out=bo_all[:, 0:D], in_=bo_ps[:])
        sum_scalar(0)
        quantise_weight(wo_codes[:], wo_scales[:], wo_packed[:])
        quantise(0)
        bias_gpsimd(1)
        bias_vector(1, D, PAIR * D)
        copy_a(1)
        nc.scalar.copy(out=bo_all[:, D:], in_=bo_all[:, 0 : GPSIMD_STEADY - D])
        nc.scalar.copy(out=g2_all[:], in_=g2_ps[:])
        project(0)
        turn_a(2)
        copy_a(2)
        residual(0, (0,))
        quantise(1)
        residual(0, (1,))
        project(1)
        turn_a(3, "nT_ps")
        quantise(2)
        bias_gpsimd(2)
        squares(0, 0)
        squares(0, 1)
        copy_a(3)
        residual(1)
        store_x1_pair(0)
        bias_vector(2, D, PAIR * D)
        project(2)
        sum_plain(3)
        turn_a(4)
        interleave_w(0, "up_ps")
        quantise(3)
        inverse_root(0)
        bias_gpsimd(3)
        squares(1, 0)
        squares(1, 1)
        sum_scalar(3)
        copy_a(4)
        residual(2)
        project(3)
        sum_plain(4)
        turn_a(5)
        squares(2, 0)
        copy_w(0)
        squares(2, 1)
        norm(0)
        turn_n(0, 0)
        turn_n(0, 1)
        interleave_w(1, "gate_ps")
        quantise(4)
        inverse_root(1)
        bias_gpsimd(4)
        sum_scalar(4)
        copy_a(5)
        copy_n(0)
        residual(3)
        store_x1_pair(2)
        project(4)
        sum_plain(5)
        turn_a(6)
        norm(1)
        turn_n(1, 0)
        turn_n(1, 1)
        quantise_w(0)
        quantise(5)
        inverse_root(2)
        bias_gpsimd(5)
        squares(3, 0)
        copy_w(1)
        squares(3, 1)
        copy_a(6)
        copy_n(1)
        gate(0)
        silu(0)
        residual(4)
        project(5)
        turn_a(7)
        sum_scalar(5)
        squares(4, 0)
        squares(4, 1)
        store_x1(4)
        norm(2)
        quantise_w(1)
        up(0)
        turn_n(2, 0)
        turn_n(2, 1)
        quantise(6)
        inverse_root(3)
        bias_gpsimd(6)
        residual(5, (0,))
        product(0)
        copy_a(7)
        copy_n(2)
        gate_up(1)
        silu(1)
        residual(5, (1,))
        turn_a(8)
        project(6)
        sum_plain(6)
        squares(5, 0)
        squares(5, 1)
        store_x1(5)
        norm(3)
        turn_n(3, 0)
        turn_n(3, 1)

        for p in range(STEADY, LAST - 1):
            quantise(p + 1)
            inverse_root(p - 2)
            bias_gpsimd(p + 1)
            product(p - 5)
            (copy_y if turned(p) else sum_scalar)(p)
            copy_a(p + 2)
            copy_n(p - 3)
            gate_up(p - 4)
            silu(p - 4)
            residual(p)
            if turned(p):
                sum_turn(p)
                sum_scalar(p)
            each(turn_a, p + 3)
            project(p + 1)
            sum_plain(p + 1)
            if p + 2 == LAST:
                sum_plain(LAST, "aT_ps")
            squares(p, 0)
            squares(p, 1)
            store_x1(p)
            norm(p - 2)
            turn_n(p - 2, 0)
            turn_n(p - 2, 1)

        quantise(15)
        inverse_root(12)
        bias_gpsimd(15)
        product(9)
        copy_y(14)
        sum_scalar(15)
        copy_n(11)
        gate_up(10)
        silu(10)
        sum_turn(14)
        residual(14)
        project(15, (1,), psum1, "aT_ps")
        project(15, (0,))
        sum_scalar(14)
        squares(14, 0)
        squares(14, 1)
        store_x1(14)
        norm(12)
        turn_n(12, 0)
        turn_n(12, 1)
        inverse_root(13)
        gain_gpsimd(13, 1, stage(15, D, PAIR * D))
        inverse_root(14)
        residual(15, (1, 0))
        store_x1(15)
        warm_tensor("y_ps", psum2)
        warm_tensor("y_ps", psum2)
        product(10)
        warm_tensor("up_ps")
        copy_n(12)
        squares(15, 1)
        squares(15, 0)
        norm_scalar(13, 1)
        norm(13, (0,))
        quantise(16)
        inverse_root(15)
        turn_n(13, 0)
        gate(11)
        gate(12, psum2, "y_ps")
        turn_n(13, 1)
        silu(11)
        norm(14)
        copy_n(13)
        turn_n(14, 0, "sum_ps")
        turn_n(14, 1, "sum_ps")
        up(11, psum1, "aT_ps")
        up(12, psum2, "y_ps")
        copy_n(14)
        silu(12)
        norm(15, (1, 0))
        quantise(18)
        turn_tile(15, 1, "nT_ps")
        turn_tile(15, 0, "gate_ps")
        product(11)
        gate(13, psum1, "up_ps")
        up(13, psum1, "aT_ps")
        finish_tile(15, 1)
        finish_tile(15, 0)
        silu(13)
        quantise(19)
        product(12)
        gate(14, psum1, "sum_ps")
        up(14, psum2, "y_ps")
        quantise_tile(15, 1)
        quantise_tile(15, 0)
        product(13, 1)
        silu(14)
        half_tile(15, 1, 0, psum1, "nT_ps")
        half_tile(15, 0, 0, psum1, "gate_ps")
        half_tile(15, 1, 1, psum2, "y_ps")
        half_tile(15, 0, 1, psum1, "up_ps")
        product(14, 1)
        silu_tile(15, 1)
        silu_tile(15, 0)
        product_tile(15, 1)
        product_tile(15, 0)
